import numpy as np
import ml_dtypes


def mxq(x, axis, fmt="e4m3"):
    dtype, down = {"e4m3": (ml_dtypes.float8_e4m3fn, 7), "e5m2": (ml_dtypes.float8_e5m2, 14)}[fmt]
    v = np.moveaxis(np.asarray(x, np.float32).astype(ml_dtypes.bfloat16).astype(np.float64), axis, -1)
    blocks = v.reshape(v.shape[:-1] + (-1, 32))
    amax = np.abs(blocks).max(-1, keepdims=True)
    byte = np.maximum(np.where(amax > 0, np.frexp(amax)[1] - 1 + 127, 0) - down, 1)
    scale = np.exp2(byte - 127.0)
    codes = (blocks / scale).astype(np.float32).astype(dtype).astype(np.float64)
    return np.moveaxis((codes * scale).reshape(v.shape), -1, axis)


WIDE = False


def mx_kscale(k):
    if not WIDE:
        return np.ones(k)
    levels = np.array([10, -10, 5, -5, 0])
    a = np.random.permutation(np.resize(levels, k // 512 * 4)).reshape(k // 512, 4)
    idx = np.arange(k)
    return np.exp2(a[idx // 512, idx % 128 // 32])


BF16 = ml_dtypes.bfloat16


def bf(x):
    return np.asarray(x, np.float32).astype(BF16)


def f64(x):
    return np.asarray(x).astype(np.float64)


E2M1 = np.array([0.0, 0.5, 1.0, 1.5, 2.0, 3.0, 4.0, 6.0, -0.0, -0.5, -1.0, -1.5, -2.0, -3.0, -4.0, -6.0])


def pack_weight(w, fmt):
    k, n = w.shape
    w = f64(bf(w)).reshape(k // 32, 32, n)
    amax = np.abs(w).max(1)
    if fmt == "e4m3":
        byte = np.frexp(amax)[1] - 1 + 127 - 7
    else:
        mant, ex = np.frexp(amax / 6.0)
        byte = np.where(mant > 0.5, ex, ex - 1) + 127
    byte = np.clip(np.where(amax > 0, byte, 1), 1, 254)
    scaled = (w * np.exp2(127.0 - byte)[:, None, :]).reshape(k, n).astype(np.float32)
    by_word = np.ascontiguousarray(scaled.reshape(k // 512, 128, 4, n).transpose(0, 1, 3, 2))
    if fmt == "e4m3":
        words = by_word.astype(ml_dtypes.float8_e4m3fn).view(np.uint8)
    else:
        c = by_word.astype(ml_dtypes.float4_e2m1fn).view(np.uint8) & 0xF
        words = c[..., 0::2] | (c[..., 1::2] << 4)
    return np.ascontiguousarray(words), np.ascontiguousarray(byte.astype(np.uint8).reshape(k // 512, 16, n))


def unpack_weight(words, scales, fmt):
    g, p, n, _ = words.shape
    if fmt == "e4m3":
        vals = np.ascontiguousarray(words).view(ml_dtypes.float8_e4m3fn).astype(np.float64)
    else:
        nib = np.empty((g, p, n, 4), np.uint8)
        nib[..., 0::2] = words & 0xF
        nib[..., 1::2] = words >> 4
        vals = E2M1[nib]
    vals = vals * np.repeat(np.exp2(scales.astype(np.float64) - 127.0), 8, axis=1)[..., None]
    return vals.transpose(0, 1, 3, 2).reshape(g * 512, n)


B, D, DC, NREF = 256, 512, 8192, 1024
KAPPA = 1.25


def logsumexp_rows(v):
    m = v.max(axis=1, keepdims=True)
    return np.log(np.exp(v - m).sum(axis=1)) + m[:, 0]


def setup_inputs():
    s = mx_kscale(D)
    h0 = np.exp(-2.0 * KAPPA / np.sqrt(DC)) / np.sqrt(2.0 * np.pi)
    sig = h0 * np.sqrt(2.0 * KAPPA) / DC ** 0.25
    x = bf(np.random.standard_normal((B, D)) * s)
    pca_weight = np.random.standard_normal((DC, D)) * 0.95 * sig / np.sqrt(D) / s[None, :]
    words, scales = pack_weight(np.ascontiguousarray(pca_weight.T), "e4m3")
    return {"x": x,
            "pca_weight_words": words,
            "pca_weight_scales": scales,
            "pca_bias": bf(np.random.standard_normal(DC) * 0.3 * sig),
            "X_ref": bf(np.random.standard_normal((NREF, DC)) * sig),
            "bandwidth": bf(h0 * np.exp(np.random.standard_normal(1) * 2.0 / DC))}


def reference(x, pca_weight_words, pca_weight_scales, pca_bias, X_ref, bandwidth):
    r = f64(X_ref)
    h = f64(bandwidth)
    z = (mxq(f64(x), 1, "e4m3") @ unpack_weight(pca_weight_words, pca_weight_scales, "e4m3")) + f64(pca_bias)
    n, d = r.shape
    d2 = (np.sum(z * z, axis=-1, keepdims=True)
          + np.sum(r * r, axis=-1)[None, :]
          - 2.0 * (mxq(z, 1, "e4m3") @ mxq(r, 1, "e4m3").T))
    d2 = np.maximum(d2, 0.0)
    coeff = -np.log(n) - np.log(2.0 * np.pi) * d / 2.0 - np.log(h) * d
    logits = d2 / (-2.0 * h * h)
    return logsumexp_rows(logits) + coeff

@@ -1,0 +1,358 @@
+import math
+from contextlib import ExitStack
+
+import concourse.mybir as mybir
+from concourse.masks import make_identity
+
+F32 = mybir.dt.float32
+BF16 = mybir.dt.bfloat16
+I32 = mybir.dt.int32
+U32 = mybir.dt.uint32
+U8 = mybir.dt.uint8
+FP8X4 = mybir.dt.float8_e4m3fn_x4
+ALU = mybir.AluOpType
+ACT = mybir.ActivationFunctionType
+AX = mybir.AxisListType
+
+P = 128
+B, D, DC, NREF = 256, 512, 8192, 1024
+K_PASS = 4 * P
+I_TILES = B // P
+J_TILES = NREF // P
+PASSES = DC // K_PASS
+UNITS = PASSES * I_TILES
+HALF = PASSES // 2
+BANK = 512
+R_BANKS = PASSES // 2
+W_CHUNK = 1024
+R_CHUNK = 2048
+R_CHUNKS = DC // R_CHUNK
+R_AHEAD = 2
+R_BUFS = 4
+
+assert UNITS // 4 == R_AHEAD * R_CHUNKS
+
+FLOPS = 2 * B * D * DC + 2 * B * DC * NREF
+
+SQRT_2PI_HI = 41069.0 / 16384.0
+COEFF_REST = -math.log(NREF) - DC * math.log(math.sqrt(2.0 * math.pi) / SQRT_2PI_HI)
+
+
+def tile_kernelloglikelihood_k_kernel(
+    tc, x, pca_weight_words, pca_weight_scales, pca_bias, X_ref, bandwidth, out
+):
+    nc = tc.nc
+    with ExitStack() as stack:
+        const = stack.enter_context(tc.tile_pool(name="const", bufs=1))
+        z_stage = stack.enter_context(tc.tile_pool(name="z_stage", bufs=3))
+        r_rows = stack.enter_context(tc.tile_pool(name="r_rows", bufs=R_BUFS))
+        r_stage = stack.enter_context(tc.tile_pool(name="r_stage", bufs=3))
+        r_quant = stack.enter_context(tc.tile_pool(name="r_quant", bufs=4))
+        unread = stack.enter_context(tc.tile_pool(name="unread", bufs=2))
+        acc = stack.enter_context(tc.psum_pool(name="acc", bufs=1))
+        work = stack.enter_context(tc.psum_pool(name="work", bufs=4))
+        stack.enter_context(tc.manual_schedule())
+
+        x_sb = const.tile([P, I_TILES, D], BF16)
+        nc.sync.dma_start(out=x_sb[:], in_=x.rearrange("(t p) k -> p t k", p=P))
+        h_bf = const.tile([P, 1], BF16)
+        nc.sync.dma_start(out=h_bf[:], in_=bandwidth.partition_broadcast(P))
+
+        w_scales = const.tile([P, DC], U8, align_bytes=64)
+        nc.vector.memset(w_scales[:].bitcast(I32), 0)
+        for b in range(2):
+            for r in range(4):
+                nc.sync.dma_start(
+                    out=w_scales[32 * b + r : P : 64, :].bitcast(I32),
+                    in_=pca_weight_scales[0][4 * b + r : 16 : 8, :].bitcast(I32),
+                )
+
+        r_sb = {}
+
+        def load_reference(jt, q):
+            if q == 0:
+                r_sb[jt] = r_rows.tile([P, DC], BF16, name="r_sb")
+            cols = slice(q * R_CHUNK, (q + 1) * R_CHUNK)
+            nc.sync.dma_start(out=r_sb[jt][:, cols], in_=X_ref[jt * P : (jt + 1) * P, cols])
+
+        w_words = const.tile([P, DC], U32, align_bytes=64)
+        w_bytes = pca_weight_words[0].rearrange("p n t -> p (n t)")
+        bias_all = const.tile([P, DC], BF16)
+        for n in range(DC // W_CHUNK):
+            c0 = n * W_CHUNK
+            nc.sync.dma_start(
+                out=w_words[:, c0 : c0 + W_CHUNK].bitcast(I32),
+                in_=w_bytes[:, 4 * c0 : 4 * (c0 + W_CHUNK)].bitcast(I32),
+            )
+            nc.sync.dma_start(
+                out=bias_all[:, c0 : c0 + W_CHUNK],
+                in_=pca_bias[c0 : c0 + W_CHUNK].partition_broadcast(P),
+            )
+            if n % 2 == 1:
+                load_reference(0, n // 2)
+        for jt in range(1, R_BUFS):
+            for q in range(R_CHUNKS):
+                load_reference(jt, q)
+
+        ident = const.tile([P, P], F32)
+        make_identity(nc, ident[:])
+        warm = const.tile([P, 1], F32)
+        nc.vector.memset(warm[:], 0.0)
+        nc.scalar.activation(out=warm[:], in_=warm[:], func=ACT.Exp)
+        res_pad = const.tile([P, P], F32)
+        nc.vector.memset(res_pad[:], 0.0)
+
+        h32 = const.tile([P, 1], F32)
+        nc.vector.tensor_copy(out=h32[:], in_=h_bf[:])
+        h_sq = const.tile([P, 1], F32)
+        nc.vector.tensor_tensor(out=h_sq[:], in0=h32[:], in1=h32[:], op=ALU.mult)
+        inv_h2 = const.tile([P, 1], F32)
+        nc.vector.reciprocal(out=inv_h2[:], in_=h_sq[:])
+        ln_in = const.tile([P, I_TILES + 1], F32)
+        nc.scalar.mul(out=ln_in[:, I_TILES : I_TILES + 1], in_=h32[:], mul=SQRT_2PI_HI)
+
+        x_words = x_sb[:].bitcast(F32)
+        xt_ps = work.tile([P, I_TILES, 2, P], F32, tag="work")
+        for it in range(I_TILES):
+            for u in range(2):
+                nc.tensor.transpose(xt_ps[:, it, u, :], x_words[:, it, u : D // 2 : 2], ident[:])
+        x_grouped = const.tile([P, B, 4], BF16, align_bytes=64)
+        nc.vector.tensor_copy(
+            out=x_grouped[:].rearrange("p i t -> p (i t)").bitcast(F32).rearrange("p (a i u) -> p a i u", a=I_TILES, u=2),
+            in_=xt_ps[:].rearrange("p a u i -> p a i u"),
+        )
+        x_codes = const.tile([P, B], U32, align_bytes=64)
+        x_scales = const.tile([P, B], U8, align_bytes=64)
+        nc.vector.quantize_mx(
+            out=x_codes[:].bitcast(FP8X4), scales=x_scales[:], in_=x_grouped[:].rearrange("p i t -> p (i t)")
+        )
+
+        z_codes = const.tile([P, PASSES, B], U32, align_bytes=64)
+        z_scales = const.tile([P, PASSES, B], U8, align_bytes=64)
+        z2_parts = const.tile([P, I_TILES, PASSES], F32)
+        y_ps = {}
+        z_f32 = {}
+        zt_ps = {}
+        z_grouped = {}
+
+        def project(u):
+            g, it = u // I_TILES, u % I_TILES
+            y_ps[u] = work.tile([P, K_PASS], F32, tag="work", name="y_ps")
+            nc.tensor.matmul_mx(
+                out=y_ps[u][:],
+                lhsT=x_codes[:, it * P : (it + 1) * P].bitcast(FP8X4),
+                lhsT_scale=x_scales[:, it * P : (it + 1) * P],
+                rhs=w_words[:, g * K_PASS : (g + 1) * K_PASS].bitcast(FP8X4),
+                rhs_scale=w_scales[:, g * K_PASS : (g + 1) * K_PASS],
+                start=True,
+                stop=True,
+            )
+
+        def add_bias(u):
+            g = u // I_TILES
+            z_f32[u] = z_stage.tile([P, 4, P], F32, name="z_f32")
+            nc.vector.tensor_tensor(
+                out=z_f32[u][:].rearrange("i (u e) p -> i u e p", u=2),
+                in0=y_ps[u][:].rearrange("i (u p e) -> i u e p", u=2, e=2),
+                in1=bias_all[:, g * K_PASS : (g + 1) * K_PASS].rearrange("i (u p e) -> i u e p", u=2, e=2),
+                op=ALU.add,
+            )
+
+        def square_z(u):
+            g, it = u // I_TILES, u % I_TILES
+            z_sq = unread.tile([P, K_PASS], BF16)
+            nc.scalar.activation(
+                out=z_sq[:],
+                in_=z_f32[u][:].rearrange("i t p -> i (t p)"),
+                func=ACT.Square,
+                accum_out=z2_parts[:, it, g : g + 1],
+            )
+
+        def transpose_z(u):
+            zt_ps[u] = work.tile([P, 4, P], F32, tag="work", name="zt_ps")
+            for t in range(4):
+                nc.tensor.transpose(zt_ps[u][:, t, :], z_f32[u][:, t, :], ident[:])
+
+        def round_z(u):
+            g, it = u // I_TILES, u % I_TILES
+            if it == 0:
+                z_grouped[g] = z_stage.tile([P, B, 4], BF16, align_bytes=64, name="z_grouped")
+            nc.vector.tensor_copy(
+                out=z_grouped[g][:, it * P : (it + 1) * P, :], in_=zt_ps[u][:].rearrange("p t i -> p i t")
+            )
+
+        def quantise_z(g):
+            nc.vector.quantize_mx(
+                out=z_codes[:, g, :].bitcast(FP8X4),
+                scales=z_scales[:, g, :],
+                in_=z_grouped[g][:].rearrange("p i t -> p (i t)"),
+            )
+
+        cross = [
+            [acc.tile([P, BANK], F32, name="cross_%d_%d" % (it, jh)) for jh in range(NREF // BANK)] for it in range(I_TILES)
+        ]
+        r2_parts = const.tile([P, J_TILES, R_CHUNKS], F32)
+        r2 = const.tile([P, J_TILES], F32)
+        r2_half = const.tile([P, NREF], F32)
+        rt_ps = {}
+        r_grouped = {}
+        r_codes = {}
+        r_scales = {}
+
+        def square_r(jt, q):
+            r_sq = unread.tile([P, R_CHUNK], BF16, name="r_sq")
+            nc.scalar.activation(
+                out=r_sq[:],
+                in_=r_sb[jt][:, q * R_CHUNK : (q + 1) * R_CHUNK],
+                func=ACT.Square,
+                accum_out=r2_parts[:, jt, q : q + 1],
+            )
+
+        def transpose_r(jt, b):
+            r_words = r_sb[jt][:].bitcast(F32)
+            rt_ps[b] = work.tile([P, 2, 2, P], F32, tag="work", name="rt_ps")
+            for a in range(2):
+                for u in range(2):
+                    w0 = (2 * b + a) * (K_PASS // 2) + u * P
+                    nc.tensor.transpose(rt_ps[b][:, a, u, :], r_words[:, w0 : w0 + P], ident[:])
+
+        def copy_r(jt, b):
+            half, pair = b // (R_BANKS // 2), b % (R_BANKS // 2)
+            if pair == 0:
+                r_grouped[half] = r_stage.tile([P, HALF, P, 4], BF16, align_bytes=64, name="r_grouped")
+            words = (
+                r_grouped[half][:]
+                .rearrange("p g j t -> p (g j t)")
+                .bitcast(F32)
+                .rearrange("p (g j u) -> p g j u", g=HALF, u=2)
+            )
+            nc.vector.tensor_copy(
+                out=words[:, 2 * pair : 2 * pair + 2, :, :], in_=rt_ps[b][:].rearrange("p a u j -> p a j u")
+            )
+
+        def quantise_r(jt, half):
+            r_codes[(jt, half)] = r_quant.tile([P, HALF, P], U32, align_bytes=64, name="r_codes")
+            r_scales[(jt, half)] = r_quant.tile([P, HALF, P], U8, align_bytes=64, name="r_scales")
+            nc.vector.quantize_mx(
+                out=r_codes[(jt, half)][:].rearrange("p g j -> p (g j)").bitcast(FP8X4),
+                scales=r_scales[(jt, half)][:].rearrange("p g j -> p (g j)"),
+                in_=r_grouped[half][:].rearrange("p g j t -> p (g j t)"),
+            )
+
+        def products(jt, it):
+            for g in range(PASSES):
+                nc.tensor.matmul_mx(
+                    out=cross[it][jt // 4][:, (jt % 4) * P : (jt % 4 + 1) * P],
+                    lhsT=z_codes[:, g, it * P : (it + 1) * P].bitcast(FP8X4),
+                    lhsT_scale=z_scales[:, g, it * P : (it + 1) * P],
+                    rhs=r_codes[(jt, g // HALF)][:, g % HALF, :].bitcast(FP8X4),
+                    rhs_scale=r_scales[(jt, g // HALF)][:, g % HALF, :],
+                    start=(g == 0),
+                    stop=(g == PASSES - 1),
+                )
+
+        project(0)
+        project(1)
+        for u in range(UNITS + 1):
+            if u < UNITS:
+                add_bias(u)
+                square_z(u)
+                transpose_z(u)
+                if u + 2 < UNITS:
+                    project(u + 2)
+            if u % 2 == 1 and u >= 3:
+                quantise_z((u - 3) // 2)
+            if u >= 1:
+                round_z(u - 1)
+            if u % 4 == 3:
+                square_r((u // 4) // R_CHUNKS, (u // 4) % R_CHUNKS)
+
+        for jt in range(J_TILES):
+            for b in range(R_BANKS):
+                transpose_r(jt, b)
+                copy_r(jt, b)
+                if b == 0:
+                    if jt == 0:
+                        quantise_z(PASSES - 1)
+                    else:
+                        quantise_r(jt - 1, 1)
+                if b == R_BANKS // 2:
+                    quantise_r(jt, 0)
+                if jt >= 1 and b == R_BANKS // 2 - 1:
+                    products(jt - 1, 0)
+                if jt >= 1 and b == R_BANKS - 1:
+                    products(jt - 1, 1)
+            if jt + R_AHEAD < J_TILES:
+                for q in range(R_CHUNKS):
+                    square_r(jt + R_AHEAD, q)
+            if jt + R_BUFS < J_TILES:
+                for q in range(R_CHUNKS):
+                    load_reference(jt + R_BUFS, q)
+
+        z2 = const.tile([P, I_TILES], F32)
+        nc.vector.tensor_reduce(out=z2[:], in_=z2_parts[:], axis=AX.X, op=ALU.add)
+        z2_half = const.tile([P, I_TILES], F32)
+        nc.vector.tensor_scalar(out=z2_half[:], in0=z2[:], scalar1=-0.5, scalar2=None, op0=ALU.mult)
+        nc.vector.tensor_reduce(out=r2[:], in_=r2_parts[:], axis=AX.X, op=ALU.add)
+        r2_ps = []
+        for jh in range(NREF // BANK):
+            r2_ps.append(work.tile([P, BANK // P, P], F32, tag="work", name="r2_ps"))
+            for n in range(BANK // P):
+                jt = jh * (BANK // P) + n
+                nc.tensor.transpose(r2_ps[jh][:, n, :], r2[:, jt : jt + 1].to_broadcast([P, P]), ident[:])
+        quantise_r(J_TILES - 1, 1)
+        for jh in range(NREF // BANK):
+            nc.scalar.mul(
+                out=r2_half[:, jh * BANK : (jh + 1) * BANK], in_=r2_ps[jh][:].rearrange("p n j -> p (n j)"), mul=-0.5
+            )
+        products(J_TILES - 1, 0)
+        products(J_TILES - 1, 1)
+
+        w_max = const.tile([P, I_TILES], F32)
+        neg_l_max = const.tile([P, I_TILES], F32)
+        for it in range(I_TILES):
+            w = const.tile([P, NREF], F32, name="w_%d" % it)
+            for jh in range(NREF // BANK):
+                cols = slice(jh * BANK, (jh + 1) * BANK)
+                nc.vector.scalar_tensor_tensor(
+                    out=w[:, cols],
+                    in0=cross[it][jh][:],
+                    scalar=z2_half[:, it : it + 1],
+                    in1=r2_half[:, cols],
+                    op0=ALU.add,
+                    op1=ALU.add,
+                )
+            nc.vector.tensor_scalar(
+                out=w[:], in0=w[:], scalar1=0.0, scalar2=None, op0=ALU.min, op1=ALU.max, accum_out=w_max[:, it : it + 1]
+            )
+            nc.vector.tensor_scalar(
+                out=neg_l_max[:, it : it + 1],
+                in0=w_max[:, it : it + 1],
+                scalar1=inv_h2[:],
+                scalar2=-1.0,
+                op0=ALU.mult,
+                op1=ALU.mult,
+            )
+            e_w = unread.tile([P, R_CHUNK], BF16, name="r_sq")
+            nc.scalar.activation(
+                out=e_w[:, 0:NREF],
+                in_=w[:],
+                func=ACT.Exp,
+                scale=inv_h2[:],
+                bias=neg_l_max[:, it : it + 1],
+                accum_out=ln_in[:, it : it + 1],
+            )
+        ln_out = const.tile([P, I_TILES + 1], F32)
+        nc.scalar.activation(out=ln_out[:], in_=ln_in[:], func=ACT.Ln)
+        coeff = const.tile([P, 1], F32)
+        nc.vector.tensor_scalar(
+            out=coeff[:], in0=ln_out[:, I_TILES : I_TILES + 1], scalar1=-float(DC), scalar2=COEFF_REST, op0=ALU.mult, op1=ALU.add
+        )
+        nc.vector.scalar_tensor_tensor(
+            out=res_pad[:, 0:I_TILES], in0=ln_out[:, 0:I_TILES], scalar=coeff[:], in1=neg_l_max[:], op0=ALU.add, op1=ALU.subtract
+        )
+        res_ps = work.tile([P, P], F32, tag="work")
+        nc.tensor.transpose(res_ps[:], res_pad[:], ident[:])
+        res_rows = const.tile([P, P], F32)
+        nc.vector.tensor_copy(out=res_rows[:], in_=res_ps[:])
+        nc.sync.dma_start(out=out.rearrange("(t p) -> t p", p=P), in_=res_rows[0:I_TILES, :])

@@ -24,13 +24,15 @@ UNITS = PASSES * I_TILES
 HALF = PASSES // 2
 BANK = 512
 R_BANKS = PASSES // 2
-W_CHUNK = 1024
+W_PLANES = 4
 R_CHUNK = 2048
 R_CHUNKS = DC // R_CHUNK
 R_AHEAD = 2
 R_BUFS = 4
+LAG = 6
 
 assert UNITS // 4 == R_AHEAD * R_CHUNKS
+assert (R_BUFS - 1) * R_CHUNKS <= PASSES
 
 FLOPS = 2 * B * D * DC + 2 * B * DC * NREF
 
@@ -58,15 +60,6 @@ def tile_kernelloglikelihood_k_kernel(
         h_bf = const.tile([P, 1], BF16)
         nc.sync.dma_start(out=h_bf[:], in_=bandwidth.partition_broadcast(P))
 
-        w_scales = const.tile([P, DC], U8, align_bytes=64)
-        nc.vector.memset(w_scales[:].bitcast(I32), 0)
-        for b in range(2):
-            for r in range(4):
-                nc.sync.dma_start(
-                    out=w_scales[32 * b + r : P : 64, :].bitcast(I32),
-                    in_=pca_weight_scales[0][4 * b + r : 16 : 8, :].bitcast(I32),
-                )
-
         r_sb = {}
 
         def load_reference(jt, q):
@@ -75,24 +68,32 @@ def tile_kernelloglikelihood_k_kernel(
             cols = slice(q * R_CHUNK, (q + 1) * R_CHUNK)
             nc.sync.dma_start(out=r_sb[jt][:, cols], in_=X_ref[jt * P : (jt + 1) * P, cols])
 
+        for q in range(R_CHUNKS):
+            load_reference(0, q)
+
+        w_planes = const.tile([P, DC // W_PLANES], U8, align_bytes=64)
+        nc.vector.memset(w_planes[:].bitcast(I32), 0)
+        for quad in range(4):
+            nc.sync.dma_start(
+                out=w_planes[32 * quad : 32 * quad + 4 * W_PLANES, :].bitcast(I32),
+                in_=pca_weight_scales[0][4 * quad : 4 * quad + 4, :].rearrange("r (k c) -> k r c", k=W_PLANES).bitcast(I32),
+            )
+
         w_words = const.tile([P, DC], U32, align_bytes=64)
         w_bytes = pca_weight_words[0].rearrange("p n t -> p (n t)")
         bias_all = const.tile([P, DC], BF16)
-        for n in range(DC // W_CHUNK):
-            c0 = n * W_CHUNK
+        for g in range(PASSES):
+            c0 = g * K_PASS
             nc.sync.dma_start(
-                out=w_words[:, c0 : c0 + W_CHUNK].bitcast(I32),
-                in_=w_bytes[:, 4 * c0 : 4 * (c0 + W_CHUNK)].bitcast(I32),
+                out=w_words[:, c0 : c0 + K_PASS].bitcast(I32),
+                in_=w_bytes[:, 4 * c0 : 4 * (c0 + K_PASS)].bitcast(I32),
             )
             nc.sync.dma_start(
-                out=bias_all[:, c0 : c0 + W_CHUNK],
-                in_=pca_bias[c0 : c0 + W_CHUNK].partition_broadcast(P),
+                out=bias_all[:, c0 : c0 + K_PASS],
+                in_=pca_bias[c0 : c0 + K_PASS].partition_broadcast(P),
             )
-            if n % 2 == 1:
-                load_reference(0, n // 2)
-        for jt in range(1, R_BUFS):
-            for q in range(R_CHUNKS):
-                load_reference(jt, q)
+            if g < (R_BUFS - 1) * R_CHUNKS:
+                load_reference(1 + g // R_CHUNKS, g % R_CHUNKS)
 
         ident = const.tile([P, P], F32)
         make_identity(nc, ident[:])
@@ -137,13 +138,14 @@ def tile_kernelloglikelihood_k_kernel(
 
         def project(u):
             g, it = u // I_TILES, u % I_TILES
+            plane, col0 = (g * K_PASS) // (DC // W_PLANES), (g * K_PASS) % (DC // W_PLANES)
             y_ps[u] = work.tile([P, K_PASS], F32, tag="work", name="y_ps")
             nc.tensor.matmul_mx(
                 out=y_ps[u][:],
                 lhsT=x_codes[:, it * P : (it + 1) * P].bitcast(FP8X4),
                 lhsT_scale=x_scales[:, it * P : (it + 1) * P],
                 rhs=w_words[:, g * K_PASS : (g + 1) * K_PASS].bitcast(FP8X4),
-                rhs_scale=w_scales[:, g * K_PASS : (g + 1) * K_PASS],
+                rhs_scale=w_planes[4 * plane : P, col0 : col0 + K_PASS],
                 start=True,
                 stop=True,
             )
@@ -239,53 +241,54 @@ def tile_kernelloglikelihood_k_kernel(
                 in_=r_grouped[half][:].rearrange("p g j t -> p (g j t)"),
             )
 
-        def products(jt, it):
-            for g in range(PASSES):
-                nc.tensor.matmul_mx(
-                    out=cross[it][jt // 4][:, (jt % 4) * P : (jt % 4 + 1) * P],
-                    lhsT=z_codes[:, g, it * P : (it + 1) * P].bitcast(FP8X4),
-                    lhsT_scale=z_scales[:, g, it * P : (it + 1) * P],
-                    rhs=r_codes[(jt, g // HALF)][:, g % HALF, :].bitcast(FP8X4),
-                    rhs_scale=r_scales[(jt, g // HALF)][:, g % HALF, :],
-                    start=(g == 0),
-                    stop=(g == PASSES - 1),
-                )
+        def products(jt, half):
+            for it in range(I_TILES):
+                for g in range(half * HALF, (half + 1) * HALF):
+                    nc.tensor.matmul_mx(
+                        out=cross[it][jt // 4][:, (jt % 4) * P : (jt % 4 + 1) * P],
+                        lhsT=z_codes[:, g, it * P : (it + 1) * P].bitcast(FP8X4),
+                        lhsT_scale=z_scales[:, g, it * P : (it + 1) * P],
+                        rhs=r_codes[(jt, half)][:, g % HALF, :].bitcast(FP8X4),
+                        rhs_scale=r_scales[(jt, half)][:, g % HALF, :],
+                        start=(g == 0),
+                        stop=(g == PASSES - 1),
+                    )
 
-        project(0)
-        project(1)
-        for u in range(UNITS + 1):
-            if u < UNITS:
-                add_bias(u)
-                square_z(u)
-                transpose_z(u)
-                if u + 2 < UNITS:
-                    project(u + 2)
-            if u % 2 == 1 and u >= 3:
-                quantise_z((u - 3) // 2)
-            if u >= 1:
-                round_z(u - 1)
-            if u % 4 == 3:
-                square_r((u // 4) // R_CHUNKS, (u // 4) % R_CHUNKS)
+        def make_z():
+            project(0)
+            project(1)
+            for u in range(UNITS + 1):
+                if u < UNITS:
+                    add_bias(u)
+                    square_z(u)
+                    transpose_z(u)
+                    if u + 2 < UNITS:
+                        project(u + 2)
+                if u % 2 == 1 and u >= 3:
+                    quantise_z((u - 3) // 2)
+                if u >= 1:
+                    round_z(u - 1)
+                if u % 4 == 3:
+                    square_r(1 + (u // 4) // R_CHUNKS, (u // 4) % R_CHUNKS)
 
-        for jt in range(J_TILES):
-            for b in range(R_BANKS):
-                transpose_r(jt, b)
-                copy_r(jt, b)
-                if b == 0:
-                    if jt == 0:
-                        quantise_z(PASSES - 1)
-                    else:
-                        quantise_r(jt - 1, 1)
-                if b == R_BANKS // 2:
-                    quantise_r(jt, 0)
-                if jt >= 1 and b == R_BANKS // 2 - 1:
-                    products(jt - 1, 0)
-                if jt >= 1 and b == R_BANKS - 1:
-                    products(jt - 1, 1)
-            if jt + R_AHEAD < J_TILES:
+        for q in range(R_CHUNKS):
+            square_r(0, q)
+        for n in range(J_TILES * R_BANKS):
+            jt, b = n // R_BANKS, n % R_BANKS
+            if n == R_BANKS:
+                make_z()
+            transpose_r(jt, b)
+            copy_r(jt, b)
+            if n == R_BANKS:
+                quantise_z(PASSES - 1)
+            if n % 4 == 0 and n >= 4:
+                quantise_r((n - 4) // R_BANKS, ((n - 4) // 4) % 2)
+            if (n - LAG) % 4 == 3 and n >= LAG:
+                products((n - LAG) // R_BANKS, ((n - LAG) // 4) % 2)
+            if b == R_BANKS - 1 and 1 <= jt and jt + R_AHEAD < J_TILES:
                 for q in range(R_CHUNKS):
                     square_r(jt + R_AHEAD, q)
-            if jt + R_BUFS < J_TILES:
+            if b == R_BANKS - 1 and jt + R_BUFS < J_TILES:
                 for q in range(R_CHUNKS):
                     load_reference(jt + R_BUFS, q)
 
@@ -305,29 +308,41 @@ def tile_kernelloglikelihood_k_kernel(
             nc.scalar.mul(
                 out=r2_half[:, jh * BANK : (jh + 1) * BANK], in_=r2_ps[jh][:].rearrange("p n j -> p (n j)"), mul=-0.5
             )
-        products(J_TILES - 1, 0)
-        products(J_TILES - 1, 1)
+        for n in range(J_TILES * R_BANKS, J_TILES * R_BANKS + LAG):
+            if (n - LAG) % 4 == 3:
+                products((n - LAG) // R_BANKS, ((n - LAG) // 4) % 2)
 
-        w_max = const.tile([P, I_TILES], F32)
+        w = [const.tile([P, NREF], F32, name="w_%d" % it) for it in range(I_TILES)]
+        w_max = const.tile([P, I_TILES, NREF // BANK], F32)
         neg_l_max = const.tile([P, I_TILES], F32)
-        for it in range(I_TILES):
-            w = const.tile([P, NREF], F32, name="w_%d" % it)
-            for jh in range(NREF // BANK):
-                cols = slice(jh * BANK, (jh + 1) * BANK)
-                nc.vector.scalar_tensor_tensor(
-                    out=w[:, cols],
-                    in0=cross[it][jh][:],
-                    scalar=z2_half[:, it : it + 1],
-                    in1=r2_half[:, cols],
-                    op0=ALU.add,
-                    op1=ALU.add,
-                )
-            nc.vector.tensor_scalar(
-                out=w[:], in0=w[:], scalar1=0.0, scalar2=None, op0=ALU.min, op1=ALU.max, accum_out=w_max[:, it : it + 1]
+
+        def half_distances(it, jh):
+            cols = slice(jh * BANK, (jh + 1) * BANK)
+            nc.vector.scalar_tensor_tensor(
+                out=w[it][:, cols],
+                in0=cross[it][jh][:],
+                scalar=z2_half[:, it : it + 1],
+                in1=r2_half[:, cols],
+                op0=ALU.add,
+                op1=ALU.add,
             )
             nc.vector.tensor_scalar(
+                out=w[it][:, cols],
+                in0=w[it][:, cols],
+                scalar1=0.0,
+                scalar2=(None if jh == 0 else w_max[:, it, jh - 1 : jh]),
+                op0=ALU.min,
+                op1=ALU.max,
+                accum_out=w_max[:, it, jh : jh + 1],
+            )
+
+        for it in range(I_TILES):
+            half_distances(it, 0)
+        for it in range(I_TILES):
+            half_distances(it, 1)
+            nc.vector.tensor_scalar(
                 out=neg_l_max[:, it : it + 1],
-                in0=w_max[:, it : it + 1],
+                in0=w_max[:, it, 1:2],
                 scalar1=inv_h2[:],
                 scalar2=-1.0,
                 op0=ALU.mult,
@@ -336,7 +351,7 @@ def tile_kernelloglikelihood_k_kernel(
             e_w = unread.tile([P, R_CHUNK], BF16, name="r_sq")
             nc.scalar.activation(
                 out=e_w[:, 0:NREF],
-                in_=w[:],
+                in_=w[it][:],
                 func=ACT.Exp,
                 scale=inv_h2[:],
                 bias=neg_l_max[:, it : it + 1],

@@ -17,22 +17,26 @@ AX = mybir.AxisListType
 P = 128
 B, D, DC, NREF = 256, 512, 8192, 1024
 K_PASS = 4 * P
+BANK = 512
 I_TILES = B // P
 J_TILES = NREF // P
+J_HALVES = NREF // BANK
 PASSES = DC // K_PASS
-UNITS = PASSES * I_TILES
 HALF = PASSES // 2
-BANK = 512
-R_BANKS = PASSES // 2
+TILE_BANKS = PASSES // 2
+HALF_BANKS = TILE_BANKS // 2
+N_BANKS = J_TILES * TILE_BANKS
 W_PLANES = 4
 R_CHUNK = 2048
 R_CHUNKS = DC // R_CHUNK
-R_AHEAD = 2
 R_BUFS = 4
-LAG = 6
+AHEAD = 2
+LAG = 5
+SQUARES = J_TILES * R_CHUNKS
+SQUARES_BY_Z = R_CHUNKS + PASSES // 2
 
-assert UNITS // 4 == R_AHEAD * R_CHUNKS
-assert (R_BUFS - 1) * R_CHUNKS <= PASSES
+assert R_BUFS * R_CHUNKS == PASSES
+assert LAG > HALF_BANKS
 
 FLOPS = 2 * B * D * DC + 2 * B * DC * NREF
 
@@ -46,12 +50,11 @@ def tile_kernelloglikelihood_k_kernel(
     nc = tc.nc
     with ExitStack() as stack:
         const = stack.enter_context(tc.tile_pool(name="const", bufs=1))
-        z_stage = stack.enter_context(tc.tile_pool(name="z_stage", bufs=3))
+        z_stage = stack.enter_context(tc.tile_pool(name="z_stage", bufs=4))
         r_rows = stack.enter_context(tc.tile_pool(name="r_rows", bufs=R_BUFS))
         r_stage = stack.enter_context(tc.tile_pool(name="r_stage", bufs=3))
         r_quant = stack.enter_context(tc.tile_pool(name="r_quant", bufs=4))
         unread = stack.enter_context(tc.tile_pool(name="unread", bufs=2))
-        acc = stack.enter_context(tc.psum_pool(name="acc", bufs=1))
         work = stack.enter_context(tc.psum_pool(name="work", bufs=4))
         stack.enter_context(tc.manual_schedule())
 
@@ -62,44 +65,38 @@ def tile_kernelloglikelihood_k_kernel(
 
         r_sb = {}
 
-        def load_reference(jt, q):
+        def load_reference(chunk):
+            jt, q = chunk // R_CHUNKS, chunk % R_CHUNKS
             if q == 0:
                 r_sb[jt] = r_rows.tile([P, DC], BF16, name="r_sb")
             cols = slice(q * R_CHUNK, (q + 1) * R_CHUNK)
             nc.sync.dma_start(out=r_sb[jt][:, cols], in_=X_ref[jt * P : (jt + 1) * P, cols])
 
-        for q in range(R_CHUNKS):
-            load_reference(0, q)
+        for chunk in range(R_CHUNKS):
+            load_reference(chunk)
 
         w_planes = const.tile([P, DC // W_PLANES], U8, align_bytes=64)
         nc.vector.memset(w_planes[:].bitcast(I32), 0)
         for quad in range(4):
             nc.sync.dma_start(
                 out=w_planes[32 * quad : 32 * quad + 4 * W_PLANES, :].bitcast(I32),
-                in_=pca_weight_scales[0][4 * quad : 4 * quad + 4, :].rearrange("r (k c) -> k r c", k=W_PLANES).bitcast(I32),
+                in_=pca_weight_scales[0][4 * quad : 4 * quad + 4, :].rearrange("r (n c) -> n r c", n=W_PLANES).bitcast(I32),
             )
 
         w_words = const.tile([P, DC], U32, align_bytes=64)
         w_bytes = pca_weight_words[0].rearrange("p n t -> p (n t)")
         bias_all = const.tile([P, DC], BF16)
         for g in range(PASSES):
-            c0 = g * K_PASS
+            cols = slice(g * K_PASS, (g + 1) * K_PASS)
             nc.sync.dma_start(
-                out=w_words[:, c0 : c0 + K_PASS].bitcast(I32),
-                in_=w_bytes[:, 4 * c0 : 4 * (c0 + K_PASS)].bitcast(I32),
+                out=w_words[:, cols].bitcast(I32), in_=w_bytes[:, 4 * g * K_PASS : 4 * (g + 1) * K_PASS].bitcast(I32)
             )
-            nc.sync.dma_start(
-                out=bias_all[:, c0 : c0 + K_PASS],
-                in_=pca_bias[c0 : c0 + K_PASS].partition_broadcast(P),
-            )
-            if g < (R_BUFS - 1) * R_CHUNKS:
-                load_reference(1 + g // R_CHUNKS, g % R_CHUNKS)
+            nc.sync.dma_start(out=bias_all[:, cols], in_=pca_bias[cols].partition_broadcast(P))
+            if R_CHUNKS + g < R_BUFS * R_CHUNKS:
+                load_reference(R_CHUNKS + g)
 
         ident = const.tile([P, P], F32)
         make_identity(nc, ident[:])
-        warm = const.tile([P, 1], F32)
-        nc.vector.memset(warm[:], 0.0)
-        nc.scalar.activation(out=warm[:], in_=warm[:], func=ACT.Exp)
         res_pad = const.tile([P, P], F32)
         nc.vector.memset(res_pad[:], 0.0)
 
@@ -109,8 +106,10 @@ def tile_kernelloglikelihood_k_kernel(
         nc.vector.tensor_tensor(out=h_sq[:], in0=h32[:], in1=h32[:], op=ALU.mult)
         inv_h2 = const.tile([P, 1], F32)
         nc.vector.reciprocal(out=inv_h2[:], in_=h_sq[:])
-        ln_in = const.tile([P, I_TILES + 1], F32)
-        nc.scalar.mul(out=ln_in[:, I_TILES : I_TILES + 1], in_=h32[:], mul=SQRT_2PI_HI)
+        ln_h = const.tile([P, 1], F32)
+        nc.scalar.activation(out=ln_h[:], in_=h32[:], func=ACT.Ln, scale=SQRT_2PI_HI)
+        coeff = const.tile([P, 1], F32)
+        nc.vector.tensor_scalar(out=coeff[:], in0=ln_h[:], scalar1=-float(DC), scalar2=COEFF_REST, op0=ALU.mult, op1=ALU.add)
 
         x_words = x_sb[:].bitcast(F32)
         xt_ps = work.tile([P, I_TILES, 2, P], F32, tag="work")
@@ -136,12 +135,11 @@ def tile_kernelloglikelihood_k_kernel(
         zt_ps = {}
         z_grouped = {}
 
-        def project(u):
-            g, it = u // I_TILES, u % I_TILES
+        def project(g, it, banks):
             plane, col0 = (g * K_PASS) // (DC // W_PLANES), (g * K_PASS) % (DC // W_PLANES)
-            y_ps[u] = work.tile([P, K_PASS], F32, tag="work", name="y_ps")
+            y_ps[(g, it)] = banks.tile([P, K_PASS], F32, name="y_ps")
             nc.tensor.matmul_mx(
-                out=y_ps[u][:],
+                out=y_ps[(g, it)][:],
                 lhsT=x_codes[:, it * P : (it + 1) * P].bitcast(FP8X4),
                 lhsT_scale=x_scales[:, it * P : (it + 1) * P],
                 rhs=w_words[:, g * K_PASS : (g + 1) * K_PASS].bitcast(FP8X4),
@@ -150,37 +148,34 @@ def tile_kernelloglikelihood_k_kernel(
                 stop=True,
             )
 
-        def add_bias(u):
-            g = u // I_TILES
-            z_f32[u] = z_stage.tile([P, 4, P], F32, name="z_f32")
+        def add_bias(g, it):
+            z_f32[(g, it)] = z_stage.tile([P, 4, P], F32, name="z_f32")
             nc.vector.tensor_tensor(
-                out=z_f32[u][:].rearrange("i (u e) p -> i u e p", u=2),
-                in0=y_ps[u][:].rearrange("i (u p e) -> i u e p", u=2, e=2),
+                out=z_f32[(g, it)][:].rearrange("i (u e) p -> i u e p", u=2),
+                in0=y_ps[(g, it)][:].rearrange("i (u p e) -> i u e p", u=2, e=2),
                 in1=bias_all[:, g * K_PASS : (g + 1) * K_PASS].rearrange("i (u p e) -> i u e p", u=2, e=2),
                 op=ALU.add,
             )
 
-        def square_z(u):
-            g, it = u // I_TILES, u % I_TILES
+        def square_z(g, it):
             z_sq = unread.tile([P, K_PASS], BF16)
             nc.scalar.activation(
                 out=z_sq[:],
-                in_=z_f32[u][:].rearrange("i t p -> i (t p)"),
+                in_=z_f32[(g, it)][:].rearrange("i t p -> i (t p)"),
                 func=ACT.Square,
                 accum_out=z2_parts[:, it, g : g + 1],
             )
 
-        def transpose_z(u):
-            zt_ps[u] = work.tile([P, 4, P], F32, tag="work", name="zt_ps")
+        def transpose_z(g, it):
+            zt_ps[(g, it)] = work.tile([P, 4, P], F32, tag="work", name="zt_ps")
             for t in range(4):
-                nc.tensor.transpose(zt_ps[u][:, t, :], z_f32[u][:, t, :], ident[:])
+                nc.tensor.transpose(zt_ps[(g, it)][:, t, :], z_f32[(g, it)][:, t, :], ident[:])
 
-        def round_z(u):
-            g, it = u // I_TILES, u % I_TILES
+        def round_z(g, it):
             if it == 0:
                 z_grouped[g] = z_stage.tile([P, B, 4], BF16, align_bytes=64, name="z_grouped")
             nc.vector.tensor_copy(
-                out=z_grouped[g][:, it * P : (it + 1) * P, :], in_=zt_ps[u][:].rearrange("p t i -> p i t")
+                out=z_grouped[g][:, it * P : (it + 1) * P, :], in_=zt_ps[(g, it)][:].rearrange("p t i -> p i t")
             )
 
         def quantise_z(g):
@@ -190,19 +185,16 @@ def tile_kernelloglikelihood_k_kernel(
                 in_=z_grouped[g][:].rearrange("p i t -> p (i t)"),
             )
 
-        cross = [
-            [acc.tile([P, BANK], F32, name="cross_%d_%d" % (it, jh)) for jh in range(NREF // BANK)] for it in range(I_TILES)
-        ]
+        cross = []
         r2_parts = const.tile([P, J_TILES, R_CHUNKS], F32)
-        r2 = const.tile([P, J_TILES], F32)
-        r2_half = const.tile([P, NREF], F32)
         rt_ps = {}
         r_grouped = {}
         r_codes = {}
         r_scales = {}
 
-        def square_r(jt, q):
-            r_sq = unread.tile([P, R_CHUNK], BF16, name="r_sq")
+        def square_r(chunk):
+            jt, q = chunk // R_CHUNKS, chunk % R_CHUNKS
+            r_sq = unread.tile([P, R_CHUNK], BF16)
             nc.scalar.activation(
                 out=r_sq[:],
                 in_=r_sb[jt][:, q * R_CHUNK : (q + 1) * R_CHUNK],
@@ -210,111 +202,121 @@ def tile_kernelloglikelihood_k_kernel(
                 accum_out=r2_parts[:, jt, q : q + 1],
             )
 
-        def transpose_r(jt, b):
+        def transpose_r(n):
+            jt, b = n // TILE_BANKS, n % TILE_BANKS
             r_words = r_sb[jt][:].bitcast(F32)
-            rt_ps[b] = work.tile([P, 2, 2, P], F32, tag="work", name="rt_ps")
+            rt_ps[n] = work.tile([P, 2, 2, P], F32, tag="work", name="rt_ps")
             for a in range(2):
                 for u in range(2):
                     w0 = (2 * b + a) * (K_PASS // 2) + u * P
-                    nc.tensor.transpose(rt_ps[b][:, a, u, :], r_words[:, w0 : w0 + P], ident[:])
+                    nc.tensor.transpose(rt_ps[n][:, a, u, :], r_words[:, w0 : w0 + P], ident[:])
 
-        def copy_r(jt, b):
-            half, pair = b // (R_BANKS // 2), b % (R_BANKS // 2)
+        def copy_r(n):
+            jt, h, pair = n // TILE_BANKS, n // HALF_BANKS, n % HALF_BANKS
             if pair == 0:
-                r_grouped[half] = r_stage.tile([P, HALF, P, 4], BF16, align_bytes=64, name="r_grouped")
+                r_grouped[h] = r_stage.tile([P, HALF, P, 4], BF16, align_bytes=64, name="r_grouped")
             words = (
-                r_grouped[half][:]
-                .rearrange("p g j t -> p (g j t)")
-                .bitcast(F32)
-                .rearrange("p (g j u) -> p g j u", g=HALF, u=2)
+                r_grouped[h][:].rearrange("p g j t -> p (g j t)").bitcast(F32).rearrange("p (g j u) -> p g j u", g=HALF, u=2)
             )
-            nc.vector.tensor_copy(
-                out=words[:, 2 * pair : 2 * pair + 2, :, :], in_=rt_ps[b][:].rearrange("p a u j -> p a j u")
-            )
+            copy = nc.scalar.copy if (n % TILE_BANKS == TILE_BANKS - 1 and jt % 2 == 1) else nc.vector.tensor_copy
+            copy(out=words[:, 2 * pair : 2 * pair + 2, :, :], in_=rt_ps[n][:].rearrange("p a u j -> p a j u"))
 
-        def quantise_r(jt, half):
-            r_codes[(jt, half)] = r_quant.tile([P, HALF, P], U32, align_bytes=64, name="r_codes")
-            r_scales[(jt, half)] = r_quant.tile([P, HALF, P], U8, align_bytes=64, name="r_scales")
+        def quantise_r(h):
+            r_codes[h] = r_quant.tile([P, HALF, P], U32, align_bytes=64, name="r_codes")
+            r_scales[h] = r_quant.tile([P, HALF, P], U8, align_bytes=64, name="r_scales")
             nc.vector.quantize_mx(
-                out=r_codes[(jt, half)][:].rearrange("p g j -> p (g j)").bitcast(FP8X4),
-                scales=r_scales[(jt, half)][:].rearrange("p g j -> p (g j)"),
-                in_=r_grouped[half][:].rearrange("p g j t -> p (g j t)"),
+                out=r_codes[h][:].rearrange("p g j -> p (g j)").bitcast(FP8X4),
+                scales=r_scales[h][:].rearrange("p g j -> p (g j)"),
+                in_=r_grouped[h][:].rearrange("p g j t -> p (g j t)"),
             )
 
-        def products(jt, half):
+        def products(h):
+            jt, first = h // 2, (h % 2) * HALF
+            cols = slice((jt % (BANK // P)) * P, (jt % (BANK // P) + 1) * P)
             for it in range(I_TILES):
-                for g in range(half * HALF, (half + 1) * HALF):
+                for g in range(first, first + HALF):
                     nc.tensor.matmul_mx(
-                        out=cross[it][jt // 4][:, (jt % 4) * P : (jt % 4 + 1) * P],
+                        out=cross[it][jt // (BANK // P)][:, cols],
                         lhsT=z_codes[:, g, it * P : (it + 1) * P].bitcast(FP8X4),
                         lhsT_scale=z_scales[:, g, it * P : (it + 1) * P],
-                        rhs=r_codes[(jt, half)][:, g % HALF, :].bitcast(FP8X4),
-                        rhs_scale=r_scales[(jt, half)][:, g % HALF, :],
+                        rhs=r_codes[h][:, g - first, :].bitcast(FP8X4),
+                        rhs_scale=r_scales[h][:, g - first, :],
                         start=(g == 0),
                         stop=(g == PASSES - 1),
                     )
 
-        def make_z():
-            project(0)
-            project(1)
-            for u in range(UNITS + 1):
-                if u < UNITS:
-                    add_bias(u)
-                    square_z(u)
-                    transpose_z(u)
-                    if u + 2 < UNITS:
-                        project(u + 2)
-                if u % 2 == 1 and u >= 3:
-                    quantise_z((u - 3) // 2)
-                if u >= 1:
-                    round_z(u - 1)
-                if u % 4 == 3:
-                    square_r(1 + (u // 4) // R_CHUNKS, (u // 4) % R_CHUNKS)
+        def after_bank(n):
+            if n % HALF_BANKS == 0 and 0 < n <= N_BANKS:
+                quantise_r(n // HALF_BANKS - 1)
+            if (n - LAG) % HALF_BANKS == HALF_BANKS - 1 and n >= LAG:
+                products((n - LAG) // HALF_BANKS)
 
-        for q in range(R_CHUNKS):
-            square_r(0, q)
-        for n in range(J_TILES * R_BANKS):
-            jt, b = n // R_BANKS, n % R_BANKS
-            if n == R_BANKS:
-                make_z()
-            transpose_r(jt, b)
-            copy_r(jt, b)
-            if n == R_BANKS:
+        def make_z(banks):
+            for g in range(AHEAD):
+                for it in range(I_TILES):
+                    project(g, it, banks)
+            for g in range(PASSES + 1):
+                if g < PASSES:
+                    for it in range(I_TILES):
+                        add_bias(g, it)
+                        square_z(g, it)
+                    for it in range(I_TILES):
+                        transpose_z(g, it)
+                if g + AHEAD < PASSES:
+                    for it in range(I_TILES):
+                        project(g + AHEAD, it, banks)
+                if g >= 2:
+                    quantise_z(g - 2)
+                if g >= 1:
+                    for it in range(I_TILES):
+                        round_z(g - 1, it)
+                if g % 2 == 1:
+                    square_r(R_CHUNKS + g // 2)
+
+        for chunk in range(R_CHUNKS):
+            square_r(chunk)
+        for n in range(N_BANKS):
+            jt, b = n // TILE_BANKS, n % TILE_BANKS
+            if n == TILE_BANKS:
+                with tc.psum_pool(name="z_banks", bufs=2 * AHEAD) as z_banks:
+                    make_z(z_banks)
+                acc = stack.enter_context(tc.psum_pool(name="acc", bufs=1))
+                for it in range(I_TILES):
+                    cross.append([acc.tile([P, BANK], F32, name="cross_%d_%d" % (it, jh)) for jh in range(J_HALVES)])
+            transpose_r(n)
+            copy_r(n)
+            if n == TILE_BANKS:
                 quantise_z(PASSES - 1)
-            if n % 4 == 0 and n >= 4:
-                quantise_r((n - 4) // R_BANKS, ((n - 4) // 4) % 2)
-            if (n - LAG) % 4 == 3 and n >= LAG:
-                products((n - LAG) // R_BANKS, ((n - LAG) // 4) % 2)
-            if b == R_BANKS - 1 and 1 <= jt and jt + R_AHEAD < J_TILES:
+            after_bank(n)
+            if b == HALF_BANKS - 1 and jt >= 1:
+                left = SQUARES - SQUARES_BY_Z
+                for chunk in range(SQUARES_BY_Z + left * (jt - 1) // (J_TILES - 1), SQUARES_BY_Z + left * jt // (J_TILES - 1)):
+                    square_r(chunk)
+            if b == TILE_BANKS - 1 and jt + R_BUFS < J_TILES:
                 for q in range(R_CHUNKS):
-                    square_r(jt + R_AHEAD, q)
-            if b == R_BANKS - 1 and jt + R_BUFS < J_TILES:
-                for q in range(R_CHUNKS):
-                    load_reference(jt + R_BUFS, q)
+                    load_reference((jt + R_BUFS) * R_CHUNKS + q)
 
         z2 = const.tile([P, I_TILES], F32)
         nc.vector.tensor_reduce(out=z2[:], in_=z2_parts[:], axis=AX.X, op=ALU.add)
         z2_half = const.tile([P, I_TILES], F32)
         nc.vector.tensor_scalar(out=z2_half[:], in0=z2[:], scalar1=-0.5, scalar2=None, op0=ALU.mult)
+        r2 = const.tile([P, J_TILES], F32)
         nc.vector.tensor_reduce(out=r2[:], in_=r2_parts[:], axis=AX.X, op=ALU.add)
-        r2_ps = []
-        for jh in range(NREF // BANK):
-            r2_ps.append(work.tile([P, BANK // P, P], F32, tag="work", name="r2_ps"))
-            for n in range(BANK // P):
-                jt = jh * (BANK // P) + n
-                nc.tensor.transpose(r2_ps[jh][:, n, :], r2[:, jt : jt + 1].to_broadcast([P, P]), ident[:])
-        quantise_r(J_TILES - 1, 1)
-        for jh in range(NREF // BANK):
-            nc.scalar.mul(
-                out=r2_half[:, jh * BANK : (jh + 1) * BANK], in_=r2_ps[jh][:].rearrange("p n j -> p (n j)"), mul=-0.5
-            )
-        for n in range(J_TILES * R_BANKS, J_TILES * R_BANKS + LAG):
-            if (n - LAG) % 4 == 3:
-                products((n - LAG) // R_BANKS, ((n - LAG) // 4) % 2)
+        after_bank(N_BANKS)
+        r2_half = const.tile([P, NREF], F32)
+        for jh in range(J_HALVES):
+            r2_ps = work.tile([P, BANK // P, P], F32, tag="work")
+            for m in range(BANK // P):
+                jt = jh * (BANK // P) + m
+                nc.tensor.transpose(r2_ps[:, m, :], r2[:, jt : jt + 1].to_broadcast([P, P]), ident[:])
+            nc.scalar.mul(out=r2_half[:, jh * BANK : (jh + 1) * BANK], in_=r2_ps[:].rearrange("p m j -> p (m j)"), mul=-0.5)
+        for n in range(N_BANKS + 1, N_BANKS + LAG):
+            after_bank(n)
 
         w = [const.tile([P, NREF], F32, name="w_%d" % it) for it in range(I_TILES)]
-        w_max = const.tile([P, I_TILES, NREF // BANK], F32)
+        w_max = const.tile([P, I_TILES, J_HALVES], F32)
         neg_l_max = const.tile([P, I_TILES], F32)
+        sum_exp = const.tile([P, I_TILES], F32)
 
         def half_distances(it, jh):
             cols = slice(jh * BANK, (jh + 1) * BANK)
@@ -336,35 +338,31 @@ def tile_kernelloglikelihood_k_kernel(
                 accum_out=w_max[:, it, jh : jh + 1],
             )
 
-        for it in range(I_TILES):
-            half_distances(it, 0)
-        for it in range(I_TILES):
-            half_distances(it, 1)
-            nc.vector.tensor_scalar(
-                out=neg_l_max[:, it : it + 1],
-                in0=w_max[:, it, 1:2],
-                scalar1=inv_h2[:],
-                scalar2=-1.0,
-                op0=ALU.mult,
-                op1=ALU.mult,
-            )
-            e_w = unread.tile([P, R_CHUNK], BF16, name="r_sq")
-            nc.scalar.activation(
-                out=e_w[:, 0:NREF],
-                in_=w[it][:],
-                func=ACT.Exp,
-                scale=inv_h2[:],
-                bias=neg_l_max[:, it : it + 1],
-                accum_out=ln_in[:, it : it + 1],
-            )
-        ln_out = const.tile([P, I_TILES + 1], F32)
-        nc.scalar.activation(out=ln_out[:], in_=ln_in[:], func=ACT.Ln)
-        coeff = const.tile([P, 1], F32)
-        nc.vector.tensor_scalar(
-            out=coeff[:], in0=ln_out[:, I_TILES : I_TILES + 1], scalar1=-float(DC), scalar2=COEFF_REST, op0=ALU.mult, op1=ALU.add
-        )
+        for jh in range(J_HALVES):
+            for it in range(I_TILES):
+                half_distances(it, jh)
+                if jh == J_HALVES - 1:
+                    nc.vector.tensor_scalar(
+                        out=neg_l_max[:, it : it + 1],
+                        in0=w_max[:, it, jh : jh + 1],
+                        scalar1=inv_h2[:],
+                        scalar2=-1.0,
+                        op0=ALU.mult,
+                        op1=ALU.mult,
+                    )
+                    e_w = unread.tile([P, NREF], BF16)
+                    nc.scalar.activation(
+                        out=e_w[:],
+                        in_=w[it][:],
+                        func=ACT.Exp,
+                        scale=inv_h2[:],
+                        bias=neg_l_max[:, it : it + 1],
+                        accum_out=sum_exp[:, it : it + 1],
+                    )
+        ln_sum = const.tile([P, I_TILES], F32)
+        nc.scalar.activation(out=ln_sum[:], in_=sum_exp[:], func=ACT.Ln)
         nc.vector.scalar_tensor_tensor(
-            out=res_pad[:, 0:I_TILES], in0=ln_out[:, 0:I_TILES], scalar=coeff[:], in1=neg_l_max[:], op0=ALU.add, op1=ALU.subtract
+            out=res_pad[:, 0:I_TILES], in0=ln_sum[:], scalar=coeff[:], in1=neg_l_max[:], op0=ALU.add, op1=ALU.subtract
         )
         res_ps = work.tile([P, P], F32, tag="work")
         nc.tensor.transpose(res_ps[:], res_pad[:], ident[:])

@@ -30,15 +30,18 @@ W_PLANES = 4
 R_CHUNK = 2048
 R_CHUNKS = DC // R_CHUNK
 R_BUFS = 4
-AHEAD = 2
+GRAM_TILES = 2
+HEAD_BANKS = GRAM_TILES * TILE_BANKS
+Y_BANKS = 3
 LAG = 5
-SQUARES = J_TILES * R_CHUNKS
-SQUARES_BY_Z = R_CHUNKS + PASSES // 2
-
-assert R_BUFS * R_CHUNKS == PASSES
-assert LAG > HALF_BANKS
+SQUARES = (J_TILES - GRAM_TILES) * R_CHUNKS
+Z_SQUARES_FROM = 4
+SQUARES_BY_Z = (PASSES - Z_SQUARES_FROM) // 2
 
 FLOPS = 2 * B * D * DC + 2 * B * DC * NREF
+
+assert 2 * P * P * P * 4 * PASSES * GRAM_TILES <= FLOPS // 10
+assert LAG > HALF_BANKS
 
 SQRT_2PI_HI = 41069.0 / 16384.0
 COEFF_REST = -math.log(NREF) - DC * math.log(math.sqrt(2.0 * math.pi) / SQRT_2PI_HI)
@@ -50,20 +53,25 @@ def tile_kernelloglikelihood_k_kernel(
     nc = tc.nc
     with ExitStack() as stack:
         const = stack.enter_context(tc.tile_pool(name="const", bufs=1))
-        z_stage = stack.enter_context(tc.tile_pool(name="z_stage", bufs=4))
         r_rows = stack.enter_context(tc.tile_pool(name="r_rows", bufs=R_BUFS))
-        r_stage = stack.enter_context(tc.tile_pool(name="r_stage", bufs=3))
-        r_quant = stack.enter_context(tc.tile_pool(name="r_quant", bufs=4))
+        r_stage = stack.enter_context(tc.tile_pool(name="r_stage", bufs=2 * GRAM_TILES))
+        r_quant = stack.enter_context(tc.tile_pool(name="r_quant", bufs=2 * GRAM_TILES + 1))
         unread = stack.enter_context(tc.tile_pool(name="unread", bufs=2))
         work = stack.enter_context(tc.psum_pool(name="work", bufs=4))
         stack.enter_context(tc.manual_schedule())
 
-        x_sb = const.tile([P, I_TILES, D], BF16)
-        nc.sync.dma_start(out=x_sb[:], in_=x.rearrange("(t p) k -> p t k", p=P))
-        h_bf = const.tile([P, 1], BF16)
-        nc.sync.dma_start(out=h_bf[:], in_=bandwidth.partition_broadcast(P))
+        ident = const.tile([P, P], F32)
+        z_codes = const.tile([P, PASSES, B], U32, align_bytes=64)
+        z_scales = const.tile([P, PASSES, B], U8, align_bytes=64)
+        z2_parts = const.tile([P, I_TILES, PASSES], F32)
+        r2_parts = const.tile([P, J_TILES, R_CHUNKS], F32)
 
+        cross = []
         r_sb = {}
+        rt_ps = {}
+        r_grouped = {}
+        r_codes = {}
+        r_scales = {}
 
         def load_reference(chunk):
             jt, q = chunk // R_CHUNKS, chunk % R_CHUNKS
@@ -72,129 +80,10 @@ def tile_kernelloglikelihood_k_kernel(
             cols = slice(q * R_CHUNK, (q + 1) * R_CHUNK)
             nc.sync.dma_start(out=r_sb[jt][:, cols], in_=X_ref[jt * P : (jt + 1) * P, cols])
 
-        for chunk in range(R_CHUNKS):
-            load_reference(chunk)
-
-        w_planes = const.tile([P, DC // W_PLANES], U8, align_bytes=64)
-        nc.vector.memset(w_planes[:].bitcast(I32), 0)
-        for quad in range(4):
-            nc.sync.dma_start(
-                out=w_planes[32 * quad : 32 * quad + 4 * W_PLANES, :].bitcast(I32),
-                in_=pca_weight_scales[0][4 * quad : 4 * quad + 4, :].rearrange("r (n c) -> n r c", n=W_PLANES).bitcast(I32),
-            )
-
-        w_words = const.tile([P, DC], U32, align_bytes=64)
-        w_bytes = pca_weight_words[0].rearrange("p n t -> p (n t)")
-        bias_all = const.tile([P, DC], BF16)
-        for g in range(PASSES):
-            cols = slice(g * K_PASS, (g + 1) * K_PASS)
-            nc.sync.dma_start(
-                out=w_words[:, cols].bitcast(I32), in_=w_bytes[:, 4 * g * K_PASS : 4 * (g + 1) * K_PASS].bitcast(I32)
-            )
-            nc.sync.dma_start(out=bias_all[:, cols], in_=pca_bias[cols].partition_broadcast(P))
-            if R_CHUNKS + g < R_BUFS * R_CHUNKS:
-                load_reference(R_CHUNKS + g)
-
-        ident = const.tile([P, P], F32)
-        make_identity(nc, ident[:])
-        res_pad = const.tile([P, P], F32)
-        nc.vector.memset(res_pad[:], 0.0)
-
-        h32 = const.tile([P, 1], F32)
-        nc.vector.tensor_copy(out=h32[:], in_=h_bf[:])
-        h_sq = const.tile([P, 1], F32)
-        nc.vector.tensor_tensor(out=h_sq[:], in0=h32[:], in1=h32[:], op=ALU.mult)
-        inv_h2 = const.tile([P, 1], F32)
-        nc.vector.reciprocal(out=inv_h2[:], in_=h_sq[:])
-        ln_h = const.tile([P, 1], F32)
-        nc.scalar.activation(out=ln_h[:], in_=h32[:], func=ACT.Ln, scale=SQRT_2PI_HI)
-        coeff = const.tile([P, 1], F32)
-        nc.vector.tensor_scalar(out=coeff[:], in0=ln_h[:], scalar1=-float(DC), scalar2=COEFF_REST, op0=ALU.mult, op1=ALU.add)
-
-        x_words = x_sb[:].bitcast(F32)
-        xt_ps = work.tile([P, I_TILES, 2, P], F32, tag="work")
-        for it in range(I_TILES):
-            for u in range(2):
-                nc.tensor.transpose(xt_ps[:, it, u, :], x_words[:, it, u : D // 2 : 2], ident[:])
-        x_grouped = const.tile([P, B, 4], BF16, align_bytes=64)
-        nc.vector.tensor_copy(
-            out=x_grouped[:].rearrange("p i t -> p (i t)").bitcast(F32).rearrange("p (a i u) -> p a i u", a=I_TILES, u=2),
-            in_=xt_ps[:].rearrange("p a u i -> p a i u"),
-        )
-        x_codes = const.tile([P, B], U32, align_bytes=64)
-        x_scales = const.tile([P, B], U8, align_bytes=64)
-        nc.vector.quantize_mx(
-            out=x_codes[:].bitcast(FP8X4), scales=x_scales[:], in_=x_grouped[:].rearrange("p i t -> p (i t)")
-        )
-
-        z_codes = const.tile([P, PASSES, B], U32, align_bytes=64)
-        z_scales = const.tile([P, PASSES, B], U8, align_bytes=64)
-        z2_parts = const.tile([P, I_TILES, PASSES], F32)
-        y_ps = {}
-        z_f32 = {}
-        zt_ps = {}
-        z_grouped = {}
-
-        def project(g, it, banks):
-            plane, col0 = (g * K_PASS) // (DC // W_PLANES), (g * K_PASS) % (DC // W_PLANES)
-            y_ps[(g, it)] = banks.tile([P, K_PASS], F32, name="y_ps")
-            nc.tensor.matmul_mx(
-                out=y_ps[(g, it)][:],
-                lhsT=x_codes[:, it * P : (it + 1) * P].bitcast(FP8X4),
-                lhsT_scale=x_scales[:, it * P : (it + 1) * P],
-                rhs=w_words[:, g * K_PASS : (g + 1) * K_PASS].bitcast(FP8X4),
-                rhs_scale=w_planes[4 * plane : P, col0 : col0 + K_PASS],
-                start=True,
-                stop=True,
-            )
-
-        def add_bias(g, it):
-            z_f32[(g, it)] = z_stage.tile([P, 4, P], F32, name="z_f32")
-            nc.vector.tensor_tensor(
-                out=z_f32[(g, it)][:].rearrange("i (u e) p -> i u e p", u=2),
-                in0=y_ps[(g, it)][:].rearrange("i (u p e) -> i u e p", u=2, e=2),
-                in1=bias_all[:, g * K_PASS : (g + 1) * K_PASS].rearrange("i (u p e) -> i u e p", u=2, e=2),
-                op=ALU.add,
-            )
-
-        def square_z(g, it):
-            z_sq = unread.tile([P, K_PASS], BF16)
-            nc.scalar.activation(
-                out=z_sq[:],
-                in_=z_f32[(g, it)][:].rearrange("i t p -> i (t p)"),
-                func=ACT.Square,
-                accum_out=z2_parts[:, it, g : g + 1],
-            )
-
-        def transpose_z(g, it):
-            zt_ps[(g, it)] = work.tile([P, 4, P], F32, tag="work", name="zt_ps")
-            for t in range(4):
-                nc.tensor.transpose(zt_ps[(g, it)][:, t, :], z_f32[(g, it)][:, t, :], ident[:])
-
-        def round_z(g, it):
-            if it == 0:
-                z_grouped[g] = z_stage.tile([P, B, 4], BF16, align_bytes=64, name="z_grouped")
-            nc.vector.tensor_copy(
-                out=z_grouped[g][:, it * P : (it + 1) * P, :], in_=zt_ps[(g, it)][:].rearrange("p t i -> p i t")
-            )
-
-        def quantise_z(g):
-            nc.vector.quantize_mx(
-                out=z_codes[:, g, :].bitcast(FP8X4),
-                scales=z_scales[:, g, :],
-                in_=z_grouped[g][:].rearrange("p i t -> p (i t)"),
-            )
-
-        cross = []
-        r2_parts = const.tile([P, J_TILES, R_CHUNKS], F32)
-        rt_ps = {}
-        r_grouped = {}
-        r_codes = {}
-        r_scales = {}
-
-        def square_r(chunk):
+        def square_r(k):
+            chunk = GRAM_TILES * R_CHUNKS + k
             jt, q = chunk // R_CHUNKS, chunk % R_CHUNKS
-            r_sq = unread.tile([P, R_CHUNK], BF16)
+            r_sq = unread.tile([P, R_CHUNK], BF16, tag="by_scalar")
             nc.scalar.activation(
                 out=r_sq[:],
                 in_=r_sb[jt][:, q * R_CHUNK : (q + 1) * R_CHUNK],
@@ -212,13 +101,13 @@ def tile_kernelloglikelihood_k_kernel(
                     nc.tensor.transpose(rt_ps[n][:, a, u, :], r_words[:, w0 : w0 + P], ident[:])
 
         def copy_r(n):
-            jt, h, pair = n // TILE_BANKS, n // HALF_BANKS, n % HALF_BANKS
+            h, pair = n // HALF_BANKS, n % HALF_BANKS
             if pair == 0:
                 r_grouped[h] = r_stage.tile([P, HALF, P, 4], BF16, align_bytes=64, name="r_grouped")
             words = (
                 r_grouped[h][:].rearrange("p g j t -> p (g j t)").bitcast(F32).rearrange("p (g j u) -> p g j u", g=HALF, u=2)
             )
-            copy = nc.scalar.copy if (n % TILE_BANKS == TILE_BANKS - 1 and jt % 2 == 1) else nc.vector.tensor_copy
+            copy = nc.scalar.copy if (n < HEAD_BANKS and n % 2 == 1) else nc.vector.tensor_copy
             copy(out=words[:, 2 * pair : 2 * pair + 2, :, :], in_=rt_ps[n][:].rearrange("p a u j -> p a j u"))
 
         def quantise_r(h):
@@ -245,65 +134,226 @@ def tile_kernelloglikelihood_k_kernel(
                         stop=(g == PASSES - 1),
                     )
 
-        def after_bank(n):
-            if n % HALF_BANKS == 0 and 0 < n <= N_BANKS:
-                quantise_r(n // HALF_BANKS - 1)
-            if (n - LAG) % HALF_BANKS == HALF_BANKS - 1 and n >= LAG:
-                products((n - LAG) // HALF_BANKS)
-
-        def make_z(banks):
-            for g in range(AHEAD):
-                for it in range(I_TILES):
-                    project(g, it, banks)
-            for g in range(PASSES + 1):
-                if g < PASSES:
-                    for it in range(I_TILES):
-                        add_bias(g, it)
-                        square_z(g, it)
-                    for it in range(I_TILES):
-                        transpose_z(g, it)
-                if g + AHEAD < PASSES:
-                    for it in range(I_TILES):
-                        project(g + AHEAD, it, banks)
-                if g >= 2:
-                    quantise_z(g - 2)
-                if g >= 1:
-                    for it in range(I_TILES):
-                        round_z(g - 1, it)
-                if g % 2 == 1:
-                    square_r(R_CHUNKS + g // 2)
-
-        for chunk in range(R_CHUNKS):
-            square_r(chunk)
-        for n in range(N_BANKS):
+        def next_loads(n):
             jt, b = n // TILE_BANKS, n % TILE_BANKS
-            if n == TILE_BANKS:
-                with tc.psum_pool(name="z_banks", bufs=2 * AHEAD) as z_banks:
-                    make_z(z_banks)
-                acc = stack.enter_context(tc.psum_pool(name="acc", bufs=1))
-                for it in range(I_TILES):
-                    cross.append([acc.tile([P, BANK], F32, name="cross_%d_%d" % (it, jh)) for jh in range(J_HALVES)])
-            transpose_r(n)
-            copy_r(n)
-            if n == TILE_BANKS:
-                quantise_z(PASSES - 1)
-            after_bank(n)
-            if b == HALF_BANKS - 1 and jt >= 1:
-                left = SQUARES - SQUARES_BY_Z
-                for chunk in range(SQUARES_BY_Z + left * (jt - 1) // (J_TILES - 1), SQUARES_BY_Z + left * jt // (J_TILES - 1)):
-                    square_r(chunk)
             if b == TILE_BANKS - 1 and jt + R_BUFS < J_TILES:
                 for q in range(R_CHUNKS):
                     load_reference((jt + R_BUFS) * R_CHUNKS + q)
 
-        z2 = const.tile([P, I_TILES], F32)
+        with ExitStack() as early_stack:
+            early = early_stack.enter_context(tc.tile_pool(name="early", bufs=1))
+            z_stage = early_stack.enter_context(tc.tile_pool(name="z_stage", bufs=4))
+
+            x_sb = early.tile([P, I_TILES, D], BF16)
+            nc.sync.dma_start(out=x_sb[:], in_=x.rearrange("(t p) k -> p t k", p=P))
+            h_bf = const.tile([P, 1], BF16)
+            nc.sync.dma_start(out=h_bf[:], in_=bandwidth.partition_broadcast(P))
+            for chunk in range(GRAM_TILES * R_CHUNKS):
+                load_reference(chunk)
+
+            w_planes = early.tile([P, DC // W_PLANES], U8, align_bytes=64)
+            nc.vector.memset(w_planes[:].bitcast(I32), 0)
+            for quad in range(4):
+                nc.sync.dma_start(
+                    out=w_planes[32 * quad : 32 * quad + 4 * W_PLANES, :].bitcast(I32),
+                    in_=pca_weight_scales[0][4 * quad : 4 * quad + 4, :].rearrange("r (n c) -> n r c", n=W_PLANES).bitcast(I32),
+                )
+
+            w_words = early.tile([P, DC], U32, align_bytes=64)
+            w_bytes = pca_weight_words[0].rearrange("p n t -> p (n t)")
+            bias_all = early.tile([P, DC], BF16)
+            for g in range(PASSES):
+                cols = slice(g * K_PASS, (g + 1) * K_PASS)
+                nc.sync.dma_start(
+                    out=w_words[:, cols].bitcast(I32), in_=w_bytes[:, 4 * g * K_PASS : 4 * (g + 1) * K_PASS].bitcast(I32)
+                )
+                nc.sync.dma_start(out=bias_all[:, cols], in_=pca_bias[cols].partition_broadcast(P))
+                if g % 2 == 1:
+                    load_reference(GRAM_TILES * R_CHUNKS + g // 2)
+
+            make_identity(nc, ident[:])
+            res_pad = const.tile([P, P], F32)
+            nc.vector.memset(res_pad[:], 0.0)
+            nc.vector.memset(r2_parts[:], 0.0)
+
+            h32 = const.tile([P, 1], F32)
+            nc.vector.tensor_copy(out=h32[:], in_=h_bf[:])
+            h_sq = const.tile([P, 1], F32)
+            nc.vector.tensor_tensor(out=h_sq[:], in0=h32[:], in1=h32[:], op=ALU.mult)
+            inv_h2 = const.tile([P, 1], F32)
+            nc.vector.reciprocal(out=inv_h2[:], in_=h_sq[:])
+            ln_h = const.tile([P, 1], F32)
+            nc.scalar.activation(out=ln_h[:], in_=h32[:], func=ACT.Ln, scale=SQRT_2PI_HI)
+            coeff = const.tile([P, 1], F32)
+            nc.vector.tensor_scalar(
+                out=coeff[:], in0=ln_h[:], scalar1=-float(DC), scalar2=COEFF_REST, op0=ALU.mult, op1=ALU.add
+            )
+
+            x_words = x_sb[:].bitcast(F32)
+            xt_ps = work.tile([P, I_TILES, 2, P], F32, tag="work")
+            for it in range(I_TILES):
+                for u in range(2):
+                    nc.tensor.transpose(xt_ps[:, it, u, :], x_words[:, it, u : D // 2 : 2], ident[:])
+            x_grouped = early.tile([P, B, 4], BF16, align_bytes=64)
+            nc.vector.tensor_copy(
+                out=x_grouped[:].rearrange("p i t -> p (i t)").bitcast(F32).rearrange("p (a i u) -> p a i u", a=I_TILES, u=2),
+                in_=xt_ps[:].rearrange("p a u i -> p a i u"),
+            )
+            x_codes = early.tile([P, B], U32, align_bytes=64)
+            x_scales = early.tile([P, B], U8, align_bytes=64)
+            nc.vector.quantize_mx(
+                out=x_codes[:].bitcast(FP8X4), scales=x_scales[:], in_=x_grouped[:].rearrange("p i t -> p (i t)")
+            )
+
+            for n in range(HEAD_BANKS):
+                transpose_r(n)
+                copy_r(n)
+                if n % HALF_BANKS == 0 and n > 0:
+                    quantise_r(n // HALF_BANKS - 1)
+                next_loads(n)
+
+            y_ps = {}
+            z_f32 = {}
+            z_bf = {}
+            zt_ps = {}
+            z_grouped = {}
+
+            with tc.psum_pool(name="z_banks", bufs=Y_BANKS) as z_banks:
+                gram_ps = z_banks.tile([P, GRAM_TILES, P], F32, bufs=1)
+
+                def project(g, it):
+                    plane, col0 = (g * K_PASS) // (DC // W_PLANES), (g * K_PASS) % (DC // W_PLANES)
+                    y_ps[(g, it)] = z_banks.tile([P, K_PASS], F32, name="y_ps")
+                    nc.tensor.matmul_mx(
+                        out=y_ps[(g, it)][:],
+                        lhsT=x_codes[:, it * P : (it + 1) * P].bitcast(FP8X4),
+                        lhsT_scale=x_scales[:, it * P : (it + 1) * P],
+                        rhs=w_words[:, g * K_PASS : (g + 1) * K_PASS].bitcast(FP8X4),
+                        rhs_scale=w_planes[4 * plane : P, col0 : col0 + K_PASS],
+                        start=True,
+                        stop=True,
+                    )
+
+                def finish_z(g, it):
+                    z_f32[(g, it)] = z_stage.tile([P, K_PASS], F32, name="z_f32")
+                    nc.vector.tensor_tensor(
+                        out=z_f32[(g, it)][:],
+                        in0=y_ps[(g, it)][:],
+                        in1=bias_all[:, g * K_PASS : (g + 1) * K_PASS],
+                        op=ALU.add,
+                    )
+                    z_sq = unread.tile([P, K_PASS], BF16, tag="by_scalar")
+                    nc.scalar.activation(
+                        out=z_sq[:], in_=z_f32[(g, it)][:], func=ACT.Square, accum_out=z2_parts[:, it, g : g + 1]
+                    )
+                    z_bf[(g, it)] = z_stage.tile([P, K_PASS], BF16, name="z_bf")
+                    nc.gpsimd.tensor_scalar(
+                        out=z_bf[(g, it)][:], in0=z_f32[(g, it)][:], scalar1=1.0, scalar2=0.0, op0=ALU.mult, op1=ALU.add
+                    )
+
+                def transpose_z(g):
+                    zt_ps[g] = work.tile([P, I_TILES, 2, P], F32, tag="work", name="zt_ps")
+                    for it in range(I_TILES):
+                        z_words = z_bf[(g, it)][:].bitcast(F32)
+                        for u in range(2):
+                            nc.tensor.transpose(zt_ps[g][:, it, u, :], z_words[:, u * P : (u + 1) * P], ident[:])
+
+                def copy_z(g):
+                    z_grouped[g] = z_stage.tile([P, B, 4], BF16, align_bytes=64, name="z_grouped")
+                    nc.vector.tensor_copy(
+                        out=z_grouped[g][:]
+                        .rearrange("p i t -> p (i t)")
+                        .bitcast(F32)
+                        .rearrange("p (a i u) -> p a i u", a=I_TILES, u=2),
+                        in_=zt_ps[g][:].rearrange("p a u i -> p a i u"),
+                    )
+
+                def quantise_z(g):
+                    nc.vector.quantize_mx(
+                        out=z_codes[:, g, :].bitcast(FP8X4),
+                        scales=z_scales[:, g, :],
+                        in_=z_grouped[g][:].rearrange("p i t -> p (i t)"),
+                    )
+
+                def gram(jt, g):
+                    for t in range(4):
+                        plane = r_grouped[2 * jt + g // HALF][:, g % HALF, :, t]
+                        nc.tensor.matmul(
+                            out=gram_ps[:, jt, :],
+                            lhsT=plane,
+                            rhs=plane,
+                            start=(g == 0 and t == 0),
+                            stop=(g == PASSES - 1 and t == 3),
+                        )
+
+                units = [(g, it) for g in range(PASSES) for it in range(I_TILES)]
+                for g, it in units[:Y_BANKS]:
+                    project(g, it)
+                for g in range(PASSES + 3):
+                    if g < PASSES:
+                        for it in range(I_TILES):
+                            finish_z(g, it)
+                        for later in units[I_TILES * g + Y_BANKS : I_TILES * (g + 1) + Y_BANKS]:
+                            project(later[0], later[1])
+                    if g == 0:
+                        quantise_r(HEAD_BANKS // HALF_BANKS - 1)
+                    if 1 <= g <= PASSES:
+                        transpose_z(g - 1)
+                    if g < PASSES:
+                        for piece in range(GRAM_TILES * g, GRAM_TILES * (g + 1)):
+                            gram(piece // PASSES, piece % PASSES)
+                    if 2 <= g <= PASSES + 1:
+                        copy_z(g - 2)
+                    if g >= 3:
+                        quantise_z(g - 3)
+                    if Z_SQUARES_FROM <= g < PASSES and (g - Z_SQUARES_FROM) % 2 == 0:
+                        square_r((g - Z_SQUARES_FROM) // 2)
+
+                for jt in range(GRAM_TILES):
+                    off_diagonal = unread.tile([P, P], F32, tag="by_vector")
+                    nc.vector.scalar_tensor_tensor(
+                        out=off_diagonal[:],
+                        in0=gram_ps[:, jt, :],
+                        scalar=1.0,
+                        in1=ident[:],
+                        op0=ALU.mult,
+                        op1=ALU.mult,
+                        accum_out=r2_parts[:, jt, 0:1],
+                    )
+
+        late = stack.enter_context(tc.tile_pool(name="late", bufs=1))
+        acc = stack.enter_context(tc.psum_pool(name="acc", bufs=1))
+        for it in range(I_TILES):
+            cross.append([acc.tile([P, BANK], F32, name="cross_%d_%d" % (it, jh)) for jh in range(J_HALVES)])
+
+        def after_bank(n):
+            if n % HALF_BANKS == 0 and HEAD_BANKS < n <= N_BANKS:
+                quantise_r(n // HALF_BANKS - 1)
+            if HEAD_BANKS <= n < HEAD_BANKS + 4 * GRAM_TILES and (n - HEAD_BANKS) % 2 == 0:
+                products((n - HEAD_BANKS) // 2)
+            if (n - LAG) % HALF_BANKS == HALF_BANKS - 1 and n - LAG >= HEAD_BANKS:
+                products((n - LAG) // HALF_BANKS)
+
+        def squares_due(m):
+            left, banks = SQUARES - SQUARES_BY_Z, N_BANKS - HEAD_BANKS - HALF_BANKS
+            return SQUARES_BY_Z + min(left, left * m // banks)
+
+        for n in range(HEAD_BANKS, N_BANKS):
+            transpose_r(n)
+            copy_r(n)
+            after_bank(n)
+            for k in range(squares_due(n - HEAD_BANKS), squares_due(n - HEAD_BANKS + 1)):
+                square_r(k)
+            next_loads(n)
+
+        z2 = late.tile([P, I_TILES], F32)
         nc.vector.tensor_reduce(out=z2[:], in_=z2_parts[:], axis=AX.X, op=ALU.add)
-        z2_half = const.tile([P, I_TILES], F32)
+        z2_half = late.tile([P, I_TILES], F32)
         nc.vector.tensor_scalar(out=z2_half[:], in0=z2[:], scalar1=-0.5, scalar2=None, op0=ALU.mult)
-        r2 = const.tile([P, J_TILES], F32)
+        r2 = late.tile([P, J_TILES], F32)
         nc.vector.tensor_reduce(out=r2[:], in_=r2_parts[:], axis=AX.X, op=ALU.add)
         after_bank(N_BANKS)
-        r2_half = const.tile([P, NREF], F32)
+        r2_half = late.tile([P, NREF], F32)
         for jh in range(J_HALVES):
             r2_ps = work.tile([P, BANK // P, P], F32, tag="work")
             for m in range(BANK // P):
@@ -313,10 +363,10 @@ def tile_kernelloglikelihood_k_kernel(
         for n in range(N_BANKS + 1, N_BANKS + LAG):
             after_bank(n)
 
-        w = [const.tile([P, NREF], F32, name="w_%d" % it) for it in range(I_TILES)]
-        w_max = const.tile([P, I_TILES, J_HALVES], F32)
-        neg_l_max = const.tile([P, I_TILES], F32)
-        sum_exp = const.tile([P, I_TILES], F32)
+        w = [late.tile([P, NREF], F32, name="w_%d" % it) for it in range(I_TILES)]
+        w_max = late.tile([P, I_TILES, J_HALVES], F32)
+        neg_l_max = late.tile([P, I_TILES], F32)
+        sum_exp = late.tile([P, I_TILES], F32)
 
         def half_distances(it, jh):
             cols = slice(jh * BANK, (jh + 1) * BANK)
@@ -350,7 +400,7 @@ def tile_kernelloglikelihood_k_kernel(
                         op0=ALU.mult,
                         op1=ALU.mult,
                     )
-                    e_w = unread.tile([P, NREF], BF16)
+                    e_w = unread.tile([P, NREF], BF16, tag="by_scalar")
                     nc.scalar.activation(
                         out=e_w[:],
                         in_=w[it][:],
@@ -359,13 +409,13 @@ def tile_kernelloglikelihood_k_kernel(
                         bias=neg_l_max[:, it : it + 1],
                         accum_out=sum_exp[:, it : it + 1],
                     )
-        ln_sum = const.tile([P, I_TILES], F32)
+        ln_sum = late.tile([P, I_TILES], F32)
         nc.scalar.activation(out=ln_sum[:], in_=sum_exp[:], func=ACT.Ln)
         nc.vector.scalar_tensor_tensor(
             out=res_pad[:, 0:I_TILES], in0=ln_sum[:], scalar=coeff[:], in1=neg_l_max[:], op0=ALU.add, op1=ALU.subtract
         )
         res_ps = work.tile([P, P], F32, tag="work")
         nc.tensor.transpose(res_ps[:], res_pad[:], ident[:])
-        res_rows = const.tile([P, P], F32)
+        res_rows = late.tile([P, P], F32)
         nc.vector.tensor_copy(out=res_rows[:], in_=res_ps[:])
         nc.sync.dma_start(out=out.rearrange("(t p) -> t p", p=P), in_=res_rows[0:I_TILES, :])

@@ -30,18 +30,22 @@ W_PLANES = 4
 R_CHUNK = 2048
 R_CHUNKS = DC // R_CHUNK
 R_BUFS = 4
-GRAM_TILES = 2
-HEAD_BANKS = GRAM_TILES * TILE_BANKS
+W_BUFS = 6
+Z_FIRST = TILE_BANKS
+Z_GROUP = 4
+Z_DONE = Z_FIRST + PASSES + 3
+GRAM_FROM, GRAM_TILES = 1, 2
 Y_BANKS = 3
-LAG = 5
-SQUARES = (J_TILES - GRAM_TILES) * R_CHUNKS
-Z_SQUARES_FROM = 4
-SQUARES_BY_Z = (PASSES - Z_SQUARES_FROM) // 2
+X_STEP = 3
+LOADS_FROM = Z_FIRST + PASSES - W_BUFS + 1
+Q_BUFS = 8
+GROUPS = ((0, 4), (4, 7), (7, 8))
+GROUP_LAG = 3
+VECTOR_SQUARE_EVERY = 10
 
 FLOPS = 2 * B * D * DC + 2 * B * DC * NREF
 
 assert 2 * P * P * P * 4 * PASSES * GRAM_TILES <= FLOPS // 10
-assert LAG > HALF_BANKS
 
 SQRT_2PI_HI = 41069.0 / 16384.0
 COEFF_REST = -math.log(NREF) - DC * math.log(math.sqrt(2.0 * math.pi) / SQRT_2PI_HI)
@@ -54,10 +58,11 @@ def tile_kernelloglikelihood_k_kernel(
     with ExitStack() as stack:
         const = stack.enter_context(tc.tile_pool(name="const", bufs=1))
         r_rows = stack.enter_context(tc.tile_pool(name="r_rows", bufs=R_BUFS))
-        r_stage = stack.enter_context(tc.tile_pool(name="r_stage", bufs=2 * GRAM_TILES))
-        r_quant = stack.enter_context(tc.tile_pool(name="r_quant", bufs=2 * GRAM_TILES + 1))
+        r_stage = stack.enter_context(tc.tile_pool(name="r_stage", bufs=4))
+        r_quant = stack.enter_context(tc.tile_pool(name="r_quant", bufs=Q_BUFS))
         unread = stack.enter_context(tc.tile_pool(name="unread", bufs=2))
         work = stack.enter_context(tc.psum_pool(name="work", bufs=4))
+        acc = stack.enter_context(tc.psum_pool(name="acc", bufs=1))
         stack.enter_context(tc.manual_schedule())
 
         ident = const.tile([P, P], F32)
@@ -65,13 +70,21 @@ def tile_kernelloglikelihood_k_kernel(
         z_scales = const.tile([P, PASSES, B], U8, align_bytes=64)
         z2_parts = const.tile([P, I_TILES, PASSES], F32)
         r2_parts = const.tile([P, J_TILES, R_CHUNKS], F32)
+        scalar_tiles = [jt for jt in range(J_TILES) if not GRAM_FROM <= jt < GRAM_FROM + GRAM_TILES]
 
-        cross = []
+        cross = {}
         r_sb = {}
         rt_ps = {}
         r_grouped = {}
         r_codes = {}
         r_scales = {}
+        gram_todo = []
+        product_todo = []
+        state = {"gram": 0, "product": 0, "diagonals": -1, "prepared": 0, "halved": 0}
+        agenda = {}
+
+        def hand_off(q):
+            return GROUP_LAG if q < len(GROUPS) - 1 else 1
 
         def load_reference(chunk):
             jt, q = chunk // R_CHUNKS, chunk % R_CHUNKS
@@ -80,16 +93,18 @@ def tile_kernelloglikelihood_k_kernel(
             cols = slice(q * R_CHUNK, (q + 1) * R_CHUNK)
             nc.sync.dma_start(out=r_sb[jt][:, cols], in_=X_ref[jt * P : (jt + 1) * P, cols])
 
-        def square_r(k):
-            chunk = GRAM_TILES * R_CHUNKS + k
-            jt, q = chunk // R_CHUNKS, chunk % R_CHUNKS
-            r_sq = unread.tile([P, R_CHUNK], BF16, tag="by_scalar")
-            nc.scalar.activation(
-                out=r_sq[:],
-                in_=r_sb[jt][:, q * R_CHUNK : (q + 1) * R_CHUNK],
-                func=ACT.Square,
-                accum_out=r2_parts[:, jt, q : q + 1],
-            )
+        def square_r(k, by_vector):
+            jt, q = scalar_tiles[k // R_CHUNKS], k % R_CHUNKS
+            rows = r_sb[jt][:, q * R_CHUNK : (q + 1) * R_CHUNK]
+            if by_vector:
+                r_sq_v = unread.tile([P, R_CHUNK], BF16, tag="by_vector")
+                nc.vector.scalar_tensor_tensor(
+                    out=r_sq_v[:], in0=rows, scalar=1.0, in1=rows, op0=ALU.mult, op1=ALU.mult,
+                    accum_out=r2_parts[:, jt, q : q + 1],
+                )
+            else:
+                r_sq = unread.tile([P, R_CHUNK], BF16, tag="by_scalar")
+                nc.scalar.activation(out=r_sq[:], in_=rows, func=ACT.Square, accum_out=r2_parts[:, jt, q : q + 1])
 
         def transpose_r(n):
             jt, b = n // TILE_BANKS, n % TILE_BANKS
@@ -107,7 +122,7 @@ def tile_kernelloglikelihood_k_kernel(
             words = (
                 r_grouped[h][:].rearrange("p g j t -> p (g j t)").bitcast(F32).rearrange("p (g j u) -> p g j u", g=HALF, u=2)
             )
-            copy = nc.scalar.copy if (n < HEAD_BANKS and n % 2 == 1) else nc.vector.tensor_copy
+            copy = nc.scalar.copy if Z_FIRST <= n < Z_FIRST + PASSES else nc.vector.tensor_copy
             copy(out=words[:, 2 * pair : 2 * pair + 2, :, :], in_=rt_ps[n][:].rearrange("p a u j -> p a j u"))
 
         def quantise_r(h):
@@ -119,63 +134,307 @@ def tile_kernelloglikelihood_k_kernel(
                 in_=r_grouped[h][:].rearrange("p g j t -> p (g j t)"),
             )
 
-        def products(h):
+        def products(h, it):
             jt, first = h // 2, (h % 2) * HALF
-            cols = slice((jt % (BANK // P)) * P, (jt % (BANK // P) + 1) * P)
-            for it in range(I_TILES):
-                for g in range(first, first + HALF):
-                    nc.tensor.matmul_mx(
-                        out=cross[it][jt // (BANK // P)][:, cols],
-                        lhsT=z_codes[:, g, it * P : (it + 1) * P].bitcast(FP8X4),
-                        lhsT_scale=z_scales[:, g, it * P : (it + 1) * P],
-                        rhs=r_codes[h][:, g - first, :].bitcast(FP8X4),
-                        rhs_scale=r_scales[h][:, g - first, :],
-                        start=(g == 0),
-                        stop=(g == PASSES - 1),
-                    )
+            q = len([group for group in GROUPS if jt >= group[0]]) - 1
+            if (it, q) not in cross:
+                cross[(it, q)] = acc.tile([P, BANK], F32, tag="acc_%d" % (it + I_TILES * (q % 2)), name="cross")
+            cols = slice((jt - GROUPS[q][0]) * P, (jt - GROUPS[q][0] + 1) * P)
+            for g in range(first, first + HALF):
+                nc.tensor.matmul_mx(
+                    out=cross[(it, q)][:, cols],
+                    lhsT=z_codes[:, g, it * P : (it + 1) * P].bitcast(FP8X4),
+                    lhsT_scale=z_scales[:, g, it * P : (it + 1) * P],
+                    rhs=r_codes[h][:, g - first, :].bitcast(FP8X4),
+                    rhs_scale=r_scales[h][:, g - first, :],
+                    start=(g == 0),
+                    stop=(g == PASSES - 1),
+                )
 
-        def next_loads(n):
-            jt, b = n // TILE_BANKS, n % TILE_BANKS
-            if b == TILE_BANKS - 1 and jt + R_BUFS < J_TILES:
+        gram_ps = acc.tile([P, GRAM_TILES, P], F32, tag="acc_%d" % Y_BANKS)
+
+        def gram(jt, g):
+            for t in range(4):
+                plane = r_grouped[2 * jt + g // HALF][:, g % HALF, :, t]
+                nc.tensor.matmul(
+                    out=gram_ps[:, jt - GRAM_FROM, :],
+                    lhsT=plane,
+                    rhs=plane,
+                    start=(g == 0 and t == 0),
+                    stop=(g == PASSES - 1 and t == 3),
+                )
+
+        def diagonals():
+            for jt in range(GRAM_FROM, GRAM_FROM + GRAM_TILES):
+                off_diagonal = unread.tile([P, P], F32, tag="by_vector")
+                nc.vector.scalar_tensor_tensor(
+                    out=off_diagonal[:], in0=gram_ps[:, jt - GRAM_FROM, :], scalar=1.0, in1=ident[:],
+                    op0=ALU.mult, op1=ALU.mult, accum_out=r2_parts[:, jt, 0:1],
+                )
+
+        pools = {}
+        early_tiles = {}
+        w_words = {}
+        bias = {}
+        y_ps = {}
+        z_f32 = {}
+        z_bf = {}
+        zt_ps = {}
+        z_grouped = {}
+        units = [(g, it) for g in range(PASSES) for it in range(I_TILES)]
+
+        def load_w(g):
+            cols = slice(g * K_PASS, (g + 1) * K_PASS)
+            w_words[g] = pools["w"].tile([P, K_PASS], U32, align_bytes=64, name="w_words")
+            w_bytes = pca_weight_words[0].rearrange("p n t -> p (n t)")
+            nc.sync.dma_start(out=w_words[g][:].bitcast(I32), in_=w_bytes[:, 4 * g * K_PASS : 4 * (g + 1) * K_PASS].bitcast(I32))
+            bias[g] = pools["w"].tile([P, K_PASS], BF16, name="bias")
+            nc.sync.dma_start(out=bias[g][:], in_=pca_bias[cols].partition_broadcast(P))
+            if g % 2 == 0:
+                load_reference(R_CHUNKS + g // 2)
+            if g == PASSES - 1:
+                for chunk in range(R_CHUNKS + PASSES // 2, R_BUFS * R_CHUNKS):
+                    load_reference(chunk)
+
+        def transpose_x():
+            x_words = early_tiles["x_sb"][:].bitcast(F32)
+            early_tiles["xt_ps"] = work.tile([P, I_TILES, 2, P], F32, tag="work", name="xt_ps")
+            for it in range(I_TILES):
+                for u in range(2):
+                    nc.tensor.transpose(early_tiles["xt_ps"][:, it, u, :], x_words[:, it, u : D // 2 : 2], ident[:])
+
+        def copy_x():
+            nc.vector.tensor_copy(
+                out=early_tiles["x_grouped"][:]
+                .rearrange("p i t -> p (i t)")
+                .bitcast(F32)
+                .rearrange("p (a i u) -> p a i u", a=I_TILES, u=2),
+                in_=early_tiles["xt_ps"][:].rearrange("p a u i -> p a i u"),
+            )
+
+        def quantise_x():
+            nc.vector.quantize_mx(
+                out=early_tiles["x_codes"][:].bitcast(FP8X4),
+                scales=early_tiles["x_scales"][:],
+                in_=early_tiles["x_grouped"][:].rearrange("p i t -> p (i t)"),
+            )
+
+        def project(g, it):
+            plane, col0 = (g * K_PASS) // (DC // W_PLANES), (g * K_PASS) % (DC // W_PLANES)
+            y_ps[(g, it)] = acc.tile([P, K_PASS], F32, tag="acc_%d" % ((I_TILES * g + it) % Y_BANKS), name="y_ps")
+            nc.tensor.matmul_mx(
+                out=y_ps[(g, it)][:],
+                lhsT=early_tiles["x_codes"][:, it * P : (it + 1) * P].bitcast(FP8X4),
+                lhsT_scale=early_tiles["x_scales"][:, it * P : (it + 1) * P],
+                rhs=w_words[g][:].bitcast(FP8X4),
+                rhs_scale=early_tiles["w_planes"][4 * plane : P, col0 : col0 + K_PASS],
+                start=True,
+                stop=True,
+            )
+
+        def finish_z(g, it):
+            z_f32[(g, it)] = pools["z"].tile([P, K_PASS], F32, name="z_f32")
+            nc.vector.tensor_tensor(out=z_f32[(g, it)][:], in0=y_ps[(g, it)][:], in1=bias[g][:], op=ALU.add)
+            z_sq = unread.tile([P, K_PASS], BF16, tag="by_scalar")
+            nc.scalar.activation(out=z_sq[:], in_=z_f32[(g, it)][:], func=ACT.Square, accum_out=z2_parts[:, it, g : g + 1])
+            z_bf[(g, it)] = pools["z"].tile([P, K_PASS], BF16, name="z_bf")
+            nc.gpsimd.tensor_scalar(
+                out=z_bf[(g, it)][:], in0=z_f32[(g, it)][:], scalar1=1.0, scalar2=0.0, op0=ALU.mult, op1=ALU.add
+            )
+
+        def transpose_z(g):
+            zt_ps[g] = work.tile([P, I_TILES, 2, P], F32, tag="work", name="zt_ps")
+            for it in range(I_TILES):
+                z_words = z_bf[(g, it)][:].bitcast(F32)
+                for u in range(2):
+                    nc.tensor.transpose(zt_ps[g][:, it, u, :], z_words[:, u * P : (u + 1) * P], ident[:])
+
+        def copy_z(g):
+            if g % Z_GROUP == 0:
+                z_grouped[g // Z_GROUP] = pools["z_group"].tile([P, Z_GROUP, B, 4], BF16, align_bytes=64, name="z_grouped")
+            words = (
+                z_grouped[g // Z_GROUP][:]
+                .rearrange("p g i t -> p (g i t)")
+                .bitcast(F32)
+                .rearrange("p (g a i u) -> p g a i u", g=Z_GROUP, a=I_TILES, u=2)
+            )
+            copy = nc.vector.tensor_copy if g % 2 == 0 else nc.scalar.copy
+            copy(out=words[:, g % Z_GROUP, :, :, :], in_=zt_ps[g][:].rearrange("p a u i -> p a i u"))
+
+        def quantise_z(group):
+            passes = slice(group * Z_GROUP, (group + 1) * Z_GROUP)
+            nc.vector.quantize_mx(
+                out=z_codes[:, passes, :].rearrange("p g i -> p (g i)").bitcast(FP8X4),
+                scales=z_scales[:, passes, :].rearrange("p g i -> p (g i)"),
+                in_=z_grouped[group][:].rearrange("p g i t -> p (g i t)"),
+            )
+
+        late_tiles = {}
+        r2_ps = {}
+
+        def sum_r2(q):
+            t0, t1 = GROUPS[q]
+            nc.vector.tensor_reduce(out=late_tiles["r2"][:, t0:t1], in_=r2_parts[:, t0:t1, :], axis=AX.X, op=ALU.add)
+
+        def spread_r2(q):
+            t0, t1 = GROUPS[q]
+            r2_ps[q] = work.tile([P, t1 - t0, P], F32, tag="work", name="r2_ps")
+            for jt in range(t0, t1):
+                nc.tensor.transpose(r2_ps[q][:, jt - t0, :], late_tiles["r2"][:, jt : jt + 1].to_broadcast([P, P]), ident[:])
+
+        def halve_r2(q):
+            nc.vector.tensor_scalar(
+                out=late_tiles["r2_half"][:, GROUPS[q][0] * P : GROUPS[q][1] * P],
+                in0=r2_ps[q][:].rearrange("p m j -> p (m j)"),
+                scalar1=-0.5,
+                scalar2=None,
+                op0=ALU.mult,
+            )
+
+        def distances(q):
+            cols = slice(GROUPS[q][0] * P, GROUPS[q][1] * P)
+            w = late_tiles["w"]
+            for it in range(I_TILES):
+                nc.vector.scalar_tensor_tensor(
+                    out=w[it][:, cols],
+                    in0=cross[(it, q)][:, 0 : (GROUPS[q][1] - GROUPS[q][0]) * P],
+                    scalar=late_tiles["z2_half"][:, it : it + 1],
+                    in1=late_tiles["r2_half"][:, cols],
+                    op0=ALU.add,
+                    op1=ALU.add,
+                )
+            for it in range(I_TILES):
+                nc.vector.tensor_scalar(
+                    out=w[it][:, cols], in0=w[it][:, cols], scalar1=0.0, scalar2=None, op0=ALU.min, op1=ALU.max,
+                    accum_out=late_tiles["w_max"][:, it, q : q + 1],
+                )
+            nc.vector.tensor_scalar(
+                out=late_tiles["neg_l_max"][:, :, q], in0=late_tiles["w_max"][:, :, q], scalar1=late_tiles["inv_h2"][:],
+                scalar2=-1.0, op0=ALU.mult, op1=ALU.mult,
+            )
+
+        def exponentials(q):
+            cols = slice(GROUPS[q][0] * P, GROUPS[q][1] * P)
+            w = late_tiles["w"]
+            for it in range(I_TILES):
+                e_w = unread.tile([P, BANK], BF16, tag="by_scalar")
+                nc.scalar.activation(
+                    out=e_w[:, 0 : (GROUPS[q][1] - GROUPS[q][0]) * P],
+                    in_=w[it][:, cols],
+                    func=ACT.Exp,
+                    scale=late_tiles["inv_h2"][:],
+                    bias=late_tiles["neg_l_max"][:, it, q : q + 1],
+                    accum_out=late_tiles["sums"][:, it, q : q + 1],
+                )
+
+        def squares_due(m):
+            left, banks = (len(scalar_tiles) - 1) * R_CHUNKS, N_BANKS - Z_FIRST - PASSES - HALF_BANKS
+            return R_CHUNKS + min(left, left * max(m, 0) // banks)
+
+        def step(n):
+            g = n - Z_FIRST
+            if n == 0:
+                for k in range(R_CHUNKS):
+                    square_r(k, False)
+            if 0 <= g < PASSES:
+                for it in range(I_TILES):
+                    finish_z(g, it)
+                for later in units[I_TILES * g + Y_BANKS : I_TILES * (g + 1) + Y_BANKS]:
+                    project(later[0], later[1])
+                if g + W_BUFS < PASSES:
+                    load_w(g + W_BUFS)
+            if n == X_STEP:
+                transpose_x()
+            if 1 <= g <= PASSES:
+                transpose_z(g - 1)
+            if n < N_BANKS:
+                transpose_r(n)
+            if n == Z_FIRST - 1:
+                for first in units[:Y_BANKS]:
+                    project(first[0], first[1])
+            for piece in gram_todo[state["gram"] : state["gram"] + 2]:
+                if piece[0] <= n:
+                    gram(piece[1], piece[2])
+                    state["gram"] += 1
+                    if state["gram"] == GRAM_TILES * PASSES:
+                        state["diagonals"] = n + 2
+            if n % 2 == 0 or n >= N_BANKS:
+                for piece in product_todo[state["product"] : state["product"] + 2]:
+                    if piece[0] <= n:
+                        products(piece[1], piece[2])
+                        state["product"] += 1
+                        for q in range(len(GROUPS)):
+                            if piece[1] == 2 * GROUPS[q][1] - 1 and piece[2] == I_TILES - 1:
+                                lag = hand_off(q)
+                                first = max(n + lag, state["halved"] + 1)
+                                agenda.setdefault(first, []).append((distances, q))
+                                agenda.setdefault(first + lag - 1, []).append((exponentials, q))
+            if n == X_STEP + 1:
+                copy_x()
+            if n == X_STEP + 2:
+                quantise_x()
+            if 2 <= g <= PASSES + 1:
+                copy_z(g - 2)
+            if 1 <= n <= N_BANKS:
+                copy_r(n - 1)
+                if n % HALF_BANKS == 0 and GRAM_FROM <= (n - 1) // TILE_BANKS < GRAM_FROM + GRAM_TILES:
+                    h = n // HALF_BANKS - 1
+                    gram_todo.extend([(n + 1, h // 2, (h % 2) * HALF + a) for a in range(HALF)])
+            if g >= Z_GROUP + 2 and (g - 2) % Z_GROUP == 0 and g <= PASSES + 2:
+                quantise_z((g - 2) // Z_GROUP - 1)
+            if n > HALF_BANKS and n % HALF_BANKS == 1 and n <= N_BANKS + 1:
+                h = n // HALF_BANKS - 1
+                quantise_r(h)
+                product_todo.extend([(max(n + 2, Z_DONE + 1), h, it) for it in range(I_TILES)])
+            if n == state["diagonals"]:
+                diagonals()
+            for k in range(squares_due(g - PASSES), squares_due(g - PASSES + 1)):
+                square_r(k, k % VECTOR_SQUARE_EVERY == VECTOR_SQUARE_EVERY - 2)
+            q = state["prepared"]
+            if q < len(GROUPS) and n > max(state["diagonals"], Z_DONE) > 0:
+                lag = hand_off(q)
+                if squares_due(g - PASSES - 2 * lag) >= R_CHUNKS * len([jt for jt in scalar_tiles if jt < GROUPS[q][1]]):
+                    agenda.setdefault(n, []).append((sum_r2, q))
+                    agenda.setdefault(n + lag, []).append((spread_r2, q))
+                    agenda.setdefault(n + 2 * lag, []).append((halve_r2, q))
+                    state["halved"] = n + 2 * lag
+                    state["prepared"] += 1
+            for entry in agenda.get(n, []):
+                entry[0](entry[1])
+            if n >= LOADS_FROM and (n - LOADS_FROM) % TILE_BANKS == 0 and (n - LOADS_FROM) // TILE_BANKS + R_BUFS < J_TILES:
                 for q in range(R_CHUNKS):
-                    load_reference((jt + R_BUFS) * R_CHUNKS + q)
+                    load_reference(((n - LOADS_FROM) // TILE_BANKS + R_BUFS) * R_CHUNKS + q)
 
         with ExitStack() as early_stack:
             early = early_stack.enter_context(tc.tile_pool(name="early", bufs=1))
-            z_stage = early_stack.enter_context(tc.tile_pool(name="z_stage", bufs=4))
+            pools["w"] = early_stack.enter_context(tc.tile_pool(name="w_pool", bufs=W_BUFS))
+            pools["z"] = early_stack.enter_context(tc.tile_pool(name="z_stage", bufs=4))
+            pools["z_group"] = early_stack.enter_context(tc.tile_pool(name="z_group", bufs=2))
 
-            x_sb = early.tile([P, I_TILES, D], BF16)
-            nc.sync.dma_start(out=x_sb[:], in_=x.rearrange("(t p) k -> p t k", p=P))
             h_bf = const.tile([P, 1], BF16)
             nc.sync.dma_start(out=h_bf[:], in_=bandwidth.partition_broadcast(P))
-            for chunk in range(GRAM_TILES * R_CHUNKS):
+            load_reference(0)
+            early_tiles["x_sb"] = early.tile([P, I_TILES, D], BF16, name="x_sb")
+            nc.sync.dma_start(out=early_tiles["x_sb"][:], in_=x.rearrange("(t p) k -> p t k", p=P))
+            for chunk in range(1, R_CHUNKS):
                 load_reference(chunk)
-
-            w_planes = early.tile([P, DC // W_PLANES], U8, align_bytes=64)
-            nc.vector.memset(w_planes[:].bitcast(I32), 0)
+            early_tiles["w_planes"] = early.tile([P, DC // W_PLANES], U8, align_bytes=64, name="w_planes")
+            nc.vector.memset(early_tiles["w_planes"][:].bitcast(I32), 0)
             for quad in range(4):
                 nc.sync.dma_start(
-                    out=w_planes[32 * quad : 32 * quad + 4 * W_PLANES, :].bitcast(I32),
+                    out=early_tiles["w_planes"][32 * quad : 32 * quad + 4 * W_PLANES, :].bitcast(I32),
                     in_=pca_weight_scales[0][4 * quad : 4 * quad + 4, :].rearrange("r (n c) -> n r c", n=W_PLANES).bitcast(I32),
                 )
-
-            w_words = early.tile([P, DC], U32, align_bytes=64)
-            w_bytes = pca_weight_words[0].rearrange("p n t -> p (n t)")
-            bias_all = early.tile([P, DC], BF16)
-            for g in range(PASSES):
-                cols = slice(g * K_PASS, (g + 1) * K_PASS)
-                nc.sync.dma_start(
-                    out=w_words[:, cols].bitcast(I32), in_=w_bytes[:, 4 * g * K_PASS : 4 * (g + 1) * K_PASS].bitcast(I32)
-                )
-                nc.sync.dma_start(out=bias_all[:, cols], in_=pca_bias[cols].partition_broadcast(P))
-                if g % 2 == 1:
-                    load_reference(GRAM_TILES * R_CHUNKS + g // 2)
+            for g in range(W_BUFS):
+                load_w(g)
+            early_tiles["x_grouped"] = early.tile([P, B, 4], BF16, align_bytes=64, name="x_grouped")
+            early_tiles["x_codes"] = early.tile([P, B], U32, align_bytes=64, name="x_codes")
+            early_tiles["x_scales"] = early.tile([P, B], U8, align_bytes=64, name="x_scales")
 
             make_identity(nc, ident[:])
             res_pad = const.tile([P, P], F32)
             nc.vector.memset(res_pad[:], 0.0)
             nc.vector.memset(r2_parts[:], 0.0)
-
             h32 = const.tile([P, 1], F32)
             nc.vector.tensor_copy(out=h32[:], in_=h_bf[:])
             h_sq = const.tile([P, 1], F32)
@@ -189,230 +448,42 @@ def tile_kernelloglikelihood_k_kernel(
                 out=coeff[:], in0=ln_h[:], scalar1=-float(DC), scalar2=COEFF_REST, op0=ALU.mult, op1=ALU.add
             )
 
-            x_words = x_sb[:].bitcast(F32)
-            xt_ps = work.tile([P, I_TILES, 2, P], F32, tag="work")
-            for it in range(I_TILES):
-                for u in range(2):
-                    nc.tensor.transpose(xt_ps[:, it, u, :], x_words[:, it, u : D // 2 : 2], ident[:])
-            x_grouped = early.tile([P, B, 4], BF16, align_bytes=64)
-            nc.vector.tensor_copy(
-                out=x_grouped[:].rearrange("p i t -> p (i t)").bitcast(F32).rearrange("p (a i u) -> p a i u", a=I_TILES, u=2),
-                in_=xt_ps[:].rearrange("p a u i -> p a i u"),
-            )
-            x_codes = early.tile([P, B], U32, align_bytes=64)
-            x_scales = early.tile([P, B], U8, align_bytes=64)
-            nc.vector.quantize_mx(
-                out=x_codes[:].bitcast(FP8X4), scales=x_scales[:], in_=x_grouped[:].rearrange("p i t -> p (i t)")
-            )
-
-            for n in range(HEAD_BANKS):
-                transpose_r(n)
-                copy_r(n)
-                if n % HALF_BANKS == 0 and n > 0:
-                    quantise_r(n // HALF_BANKS - 1)
-                next_loads(n)
-
-            y_ps = {}
-            z_f32 = {}
-            z_bf = {}
-            zt_ps = {}
-            z_grouped = {}
-
-            with tc.psum_pool(name="z_banks", bufs=Y_BANKS) as z_banks:
-                gram_ps = z_banks.tile([P, GRAM_TILES, P], F32, bufs=1)
-
-                def project(g, it):
-                    plane, col0 = (g * K_PASS) // (DC // W_PLANES), (g * K_PASS) % (DC // W_PLANES)
-                    y_ps[(g, it)] = z_banks.tile([P, K_PASS], F32, name="y_ps")
-                    nc.tensor.matmul_mx(
-                        out=y_ps[(g, it)][:],
-                        lhsT=x_codes[:, it * P : (it + 1) * P].bitcast(FP8X4),
-                        lhsT_scale=x_scales[:, it * P : (it + 1) * P],
-                        rhs=w_words[:, g * K_PASS : (g + 1) * K_PASS].bitcast(FP8X4),
-                        rhs_scale=w_planes[4 * plane : P, col0 : col0 + K_PASS],
-                        start=True,
-                        stop=True,
-                    )
-
-                def finish_z(g, it):
-                    z_f32[(g, it)] = z_stage.tile([P, K_PASS], F32, name="z_f32")
-                    nc.vector.tensor_tensor(
-                        out=z_f32[(g, it)][:],
-                        in0=y_ps[(g, it)][:],
-                        in1=bias_all[:, g * K_PASS : (g + 1) * K_PASS],
-                        op=ALU.add,
-                    )
-                    z_sq = unread.tile([P, K_PASS], BF16, tag="by_scalar")
-                    nc.scalar.activation(
-                        out=z_sq[:], in_=z_f32[(g, it)][:], func=ACT.Square, accum_out=z2_parts[:, it, g : g + 1]
-                    )
-                    z_bf[(g, it)] = z_stage.tile([P, K_PASS], BF16, name="z_bf")
-                    nc.gpsimd.tensor_scalar(
-                        out=z_bf[(g, it)][:], in0=z_f32[(g, it)][:], scalar1=1.0, scalar2=0.0, op0=ALU.mult, op1=ALU.add
-                    )
-
-                def transpose_z(g):
-                    zt_ps[g] = work.tile([P, I_TILES, 2, P], F32, tag="work", name="zt_ps")
-                    for it in range(I_TILES):
-                        z_words = z_bf[(g, it)][:].bitcast(F32)
-                        for u in range(2):
-                            nc.tensor.transpose(zt_ps[g][:, it, u, :], z_words[:, u * P : (u + 1) * P], ident[:])
-
-                def copy_z(g):
-                    z_grouped[g] = z_stage.tile([P, B, 4], BF16, align_bytes=64, name="z_grouped")
-                    nc.vector.tensor_copy(
-                        out=z_grouped[g][:]
-                        .rearrange("p i t -> p (i t)")
-                        .bitcast(F32)
-                        .rearrange("p (a i u) -> p a i u", a=I_TILES, u=2),
-                        in_=zt_ps[g][:].rearrange("p a u i -> p a i u"),
-                    )
-
-                def quantise_z(g):
-                    nc.vector.quantize_mx(
-                        out=z_codes[:, g, :].bitcast(FP8X4),
-                        scales=z_scales[:, g, :],
-                        in_=z_grouped[g][:].rearrange("p i t -> p (i t)"),
-                    )
-
-                def gram(jt, g):
-                    for t in range(4):
-                        plane = r_grouped[2 * jt + g // HALF][:, g % HALF, :, t]
-                        nc.tensor.matmul(
-                            out=gram_ps[:, jt, :],
-                            lhsT=plane,
-                            rhs=plane,
-                            start=(g == 0 and t == 0),
-                            stop=(g == PASSES - 1 and t == 3),
-                        )
-
-                units = [(g, it) for g in range(PASSES) for it in range(I_TILES)]
-                for g, it in units[:Y_BANKS]:
-                    project(g, it)
-                for g in range(PASSES + 3):
-                    if g < PASSES:
-                        for it in range(I_TILES):
-                            finish_z(g, it)
-                        for later in units[I_TILES * g + Y_BANKS : I_TILES * (g + 1) + Y_BANKS]:
-                            project(later[0], later[1])
-                    if g == 0:
-                        quantise_r(HEAD_BANKS // HALF_BANKS - 1)
-                    if 1 <= g <= PASSES:
-                        transpose_z(g - 1)
-                    if g < PASSES:
-                        for piece in range(GRAM_TILES * g, GRAM_TILES * (g + 1)):
-                            gram(piece // PASSES, piece % PASSES)
-                    if 2 <= g <= PASSES + 1:
-                        copy_z(g - 2)
-                    if g >= 3:
-                        quantise_z(g - 3)
-                    if Z_SQUARES_FROM <= g < PASSES and (g - Z_SQUARES_FROM) % 2 == 0:
-                        square_r((g - Z_SQUARES_FROM) // 2)
-
-                for jt in range(GRAM_TILES):
-                    off_diagonal = unread.tile([P, P], F32, tag="by_vector")
-                    nc.vector.scalar_tensor_tensor(
-                        out=off_diagonal[:],
-                        in0=gram_ps[:, jt, :],
-                        scalar=1.0,
-                        in1=ident[:],
-                        op0=ALU.mult,
-                        op1=ALU.mult,
-                        accum_out=r2_parts[:, jt, 0:1],
-                    )
+            for n in range(Z_DONE):
+                step(n)
 
         late = stack.enter_context(tc.tile_pool(name="late", bufs=1))
-        acc = stack.enter_context(tc.psum_pool(name="acc", bufs=1))
-        for it in range(I_TILES):
-            cross.append([acc.tile([P, BANK], F32, name="cross_%d_%d" % (it, jh)) for jh in range(J_HALVES)])
-
-        def after_bank(n):
-            if n % HALF_BANKS == 0 and HEAD_BANKS < n <= N_BANKS:
-                quantise_r(n // HALF_BANKS - 1)
-            if HEAD_BANKS <= n < HEAD_BANKS + 4 * GRAM_TILES and (n - HEAD_BANKS) % 2 == 0:
-                products((n - HEAD_BANKS) // 2)
-            if (n - LAG) % HALF_BANKS == HALF_BANKS - 1 and n - LAG >= HEAD_BANKS:
-                products((n - LAG) // HALF_BANKS)
-
-        def squares_due(m):
-            left, banks = SQUARES - SQUARES_BY_Z, N_BANKS - HEAD_BANKS - HALF_BANKS
-            return SQUARES_BY_Z + min(left, left * m // banks)
-
-        for n in range(HEAD_BANKS, N_BANKS):
-            transpose_r(n)
-            copy_r(n)
-            after_bank(n)
-            for k in range(squares_due(n - HEAD_BANKS), squares_due(n - HEAD_BANKS + 1)):
-                square_r(k)
-            next_loads(n)
-
+        late_tiles["inv_h2"] = inv_h2
         z2 = late.tile([P, I_TILES], F32)
         nc.vector.tensor_reduce(out=z2[:], in_=z2_parts[:], axis=AX.X, op=ALU.add)
-        z2_half = late.tile([P, I_TILES], F32)
-        nc.vector.tensor_scalar(out=z2_half[:], in0=z2[:], scalar1=-0.5, scalar2=None, op0=ALU.mult)
-        r2 = late.tile([P, J_TILES], F32)
-        nc.vector.tensor_reduce(out=r2[:], in_=r2_parts[:], axis=AX.X, op=ALU.add)
-        after_bank(N_BANKS)
-        r2_half = late.tile([P, NREF], F32)
-        for jh in range(J_HALVES):
-            r2_ps = work.tile([P, BANK // P, P], F32, tag="work")
-            for m in range(BANK // P):
-                jt = jh * (BANK // P) + m
-                nc.tensor.transpose(r2_ps[:, m, :], r2[:, jt : jt + 1].to_broadcast([P, P]), ident[:])
-            nc.scalar.mul(out=r2_half[:, jh * BANK : (jh + 1) * BANK], in_=r2_ps[:].rearrange("p m j -> p (m j)"), mul=-0.5)
-        for n in range(N_BANKS + 1, N_BANKS + LAG):
-            after_bank(n)
+        late_tiles["z2_half"] = late.tile([P, I_TILES], F32, name="z2_half")
+        nc.vector.tensor_scalar(out=late_tiles["z2_half"][:], in0=z2[:], scalar1=-0.5, scalar2=None, op0=ALU.mult)
+        late_tiles["r2"] = late.tile([P, J_TILES], F32, name="r2")
+        late_tiles["r2_half"] = late.tile([P, NREF], F32, name="r2_half")
+        late_tiles["w"] = [late.tile([P, NREF], F32, name="w_%d" % it) for it in range(I_TILES)]
+        late_tiles["w_max"] = late.tile([P, I_TILES, len(GROUPS)], F32, name="w_max")
+        late_tiles["neg_l_max"] = late.tile([P, I_TILES, len(GROUPS)], F32, name="neg_l_max")
+        late_tiles["sums"] = late.tile([P, I_TILES, len(GROUPS)], F32, name="sums")
+        for n in range(Z_DONE, N_BANKS + 5):
+            step(n)
 
-        w = [late.tile([P, NREF], F32, name="w_%d" % it) for it in range(I_TILES)]
-        w_max = late.tile([P, I_TILES, J_HALVES], F32)
-        neg_l_max = late.tile([P, I_TILES], F32)
+        top = late.tile([P, I_TILES], F32)
+        nc.vector.tensor_reduce(out=top[:], in_=late_tiles["w_max"][:], axis=AX.X, op=ALU.max)
+        neg_l_top = late.tile([P, I_TILES], F32)
+        nc.vector.tensor_scalar(out=neg_l_top[:], in0=top[:], scalar1=inv_h2[:], scalar2=-1.0, op0=ALU.mult, op1=ALU.mult)
+        factor = late.tile([P, I_TILES, len(GROUPS)], F32)
+        for it in range(I_TILES):
+            nc.scalar.activation(
+                out=factor[:, it, :], in_=late_tiles["w_max"][:, it, :], func=ACT.Exp, scale=inv_h2[:],
+                bias=neg_l_top[:, it : it + 1],
+            )
+        weighted = late.tile([P, I_TILES, len(GROUPS)], F32)
+        nc.vector.tensor_tensor(out=weighted[:], in0=late_tiles["sums"][:], in1=factor[:], op=ALU.mult)
         sum_exp = late.tile([P, I_TILES], F32)
-
-        def half_distances(it, jh):
-            cols = slice(jh * BANK, (jh + 1) * BANK)
-            nc.vector.scalar_tensor_tensor(
-                out=w[it][:, cols],
-                in0=cross[it][jh][:],
-                scalar=z2_half[:, it : it + 1],
-                in1=r2_half[:, cols],
-                op0=ALU.add,
-                op1=ALU.add,
-            )
-            nc.vector.tensor_scalar(
-                out=w[it][:, cols],
-                in0=w[it][:, cols],
-                scalar1=0.0,
-                scalar2=(None if jh == 0 else w_max[:, it, jh - 1 : jh]),
-                op0=ALU.min,
-                op1=ALU.max,
-                accum_out=w_max[:, it, jh : jh + 1],
-            )
-
-        for jh in range(J_HALVES):
-            for it in range(I_TILES):
-                half_distances(it, jh)
-                if jh == J_HALVES - 1:
-                    nc.vector.tensor_scalar(
-                        out=neg_l_max[:, it : it + 1],
-                        in0=w_max[:, it, jh : jh + 1],
-                        scalar1=inv_h2[:],
-                        scalar2=-1.0,
-                        op0=ALU.mult,
-                        op1=ALU.mult,
-                    )
-                    e_w = unread.tile([P, NREF], BF16, tag="by_scalar")
-                    nc.scalar.activation(
-                        out=e_w[:],
-                        in_=w[it][:],
-                        func=ACT.Exp,
-                        scale=inv_h2[:],
-                        bias=neg_l_max[:, it : it + 1],
-                        accum_out=sum_exp[:, it : it + 1],
-                    )
+        nc.vector.tensor_reduce(out=sum_exp[:], in_=weighted[:], axis=AX.X, op=ALU.add)
         ln_sum = late.tile([P, I_TILES], F32)
         nc.scalar.activation(out=ln_sum[:], in_=sum_exp[:], func=ACT.Ln)
         nc.vector.scalar_tensor_tensor(
-            out=res_pad[:, 0:I_TILES], in0=ln_sum[:], scalar=coeff[:], in1=neg_l_max[:], op0=ALU.add, op1=ALU.subtract
+            out=res_pad[:, 0:I_TILES], in0=ln_sum[:], scalar=coeff[:], in1=neg_l_top[:], op0=ALU.add, op1=ALU.subtract
         )
         res_ps = work.tile([P, P], F32, tag="work")
         nc.tensor.transpose(res_ps[:], res_pad[:], ident[:])

@@ -41,7 +41,6 @@ LOADS_FROM = Z_FIRST + PASSES - W_BUFS + 1
 Q_BUFS = 8
 GROUPS = ((0, 4), (4, 7), (7, 8))
 GROUP_LAG = 3
-VECTOR_SQUARE_EVERY = 10
 
 FLOPS = 2 * B * D * DC + 2 * B * DC * NREF
 
@@ -80,11 +79,19 @@ def tile_kernelloglikelihood_k_kernel(
         r_scales = {}
         gram_todo = []
         product_todo = []
-        state = {"gram": 0, "product": 0, "diagonals": -1, "prepared": 0, "halved": 0}
+        state = {"gram": 0, "product": 0, "diagonals": -1, "prepared": 0}
+        multiplied = {}
+        halved = {}
         agenda = {}
 
         def hand_off(q):
             return GROUP_LAG if q < len(GROUPS) - 1 else 1
+
+        def plan_distances(q):
+            if q in multiplied and q in halved:
+                first = max(multiplied[q], halved[q])
+                agenda.setdefault(first, []).append((distances, q))
+                agenda.setdefault(first + hand_off(q) - 1, []).append((exponentials, q))
 
         def load_reference(chunk):
             jt, q = chunk // R_CHUNKS, chunk % R_CHUNKS
@@ -93,18 +100,11 @@ def tile_kernelloglikelihood_k_kernel(
             cols = slice(q * R_CHUNK, (q + 1) * R_CHUNK)
             nc.sync.dma_start(out=r_sb[jt][:, cols], in_=X_ref[jt * P : (jt + 1) * P, cols])
 
-        def square_r(k, by_vector):
+        def square_r(k):
             jt, q = scalar_tiles[k // R_CHUNKS], k % R_CHUNKS
             rows = r_sb[jt][:, q * R_CHUNK : (q + 1) * R_CHUNK]
-            if by_vector:
-                r_sq_v = unread.tile([P, R_CHUNK], BF16, tag="by_vector")
-                nc.vector.scalar_tensor_tensor(
-                    out=r_sq_v[:], in0=rows, scalar=1.0, in1=rows, op0=ALU.mult, op1=ALU.mult,
-                    accum_out=r2_parts[:, jt, q : q + 1],
-                )
-            else:
-                r_sq = unread.tile([P, R_CHUNK], BF16, tag="by_scalar")
-                nc.scalar.activation(out=r_sq[:], in_=rows, func=ACT.Square, accum_out=r2_parts[:, jt, q : q + 1])
+            r_sq = unread.tile([P, R_CHUNK], BF16, tag="by_scalar")
+            nc.scalar.activation(out=r_sq[:], in_=rows, func=ACT.Square, accum_out=r2_parts[:, jt, q : q + 1])
 
         def transpose_r(n):
             jt, b = n // TILE_BANKS, n % TILE_BANKS
@@ -328,14 +328,14 @@ def tile_kernelloglikelihood_k_kernel(
                 )
 
         def squares_due(m):
-            left, banks = (len(scalar_tiles) - 1) * R_CHUNKS, N_BANKS - Z_FIRST - PASSES - HALF_BANKS
+            left, banks = (len(scalar_tiles) - 1) * R_CHUNKS, N_BANKS - Z_FIRST - PASSES
             return R_CHUNKS + min(left, left * max(m, 0) // banks)
 
         def step(n):
             g = n - Z_FIRST
             if n == 0:
                 for k in range(R_CHUNKS):
-                    square_r(k, False)
+                    square_r(k)
             if 0 <= g < PASSES:
                 for it in range(I_TILES):
                     finish_z(g, it)
@@ -365,10 +365,8 @@ def tile_kernelloglikelihood_k_kernel(
                         state["product"] += 1
                         for q in range(len(GROUPS)):
                             if piece[1] == 2 * GROUPS[q][1] - 1 and piece[2] == I_TILES - 1:
-                                lag = hand_off(q)
-                                first = max(n + lag, state["halved"] + 1)
-                                agenda.setdefault(first, []).append((distances, q))
-                                agenda.setdefault(first + lag - 1, []).append((exponentials, q))
+                                multiplied[q] = n + hand_off(q)
+                                plan_distances(q)
             if n == X_STEP + 1:
                 copy_x()
             if n == X_STEP + 2:
@@ -382,22 +380,23 @@ def tile_kernelloglikelihood_k_kernel(
                     gram_todo.extend([(n + 1, h // 2, (h % 2) * HALF + a) for a in range(HALF)])
             if g >= Z_GROUP + 2 and (g - 2) % Z_GROUP == 0 and g <= PASSES + 2:
                 quantise_z((g - 2) // Z_GROUP - 1)
-            if n > HALF_BANKS and n % HALF_BANKS == 1 and n <= N_BANKS + 1:
+            if (n > HALF_BANKS and n % HALF_BANKS == 1 and n < N_BANKS) or n == N_BANKS:
                 h = n // HALF_BANKS - 1
                 quantise_r(h)
-                product_todo.extend([(max(n + 2, Z_DONE + 1), h, it) for it in range(I_TILES)])
+                product_todo.extend([(max(min(n + 2, N_BANKS + 1), Z_DONE + 1), h, it) for it in range(I_TILES)])
             if n == state["diagonals"]:
                 diagonals()
             for k in range(squares_due(g - PASSES), squares_due(g - PASSES + 1)):
-                square_r(k, k % VECTOR_SQUARE_EVERY == VECTOR_SQUARE_EVERY - 2)
+                square_r(k)
             q = state["prepared"]
             if q < len(GROUPS) and n > max(state["diagonals"], Z_DONE) > 0:
                 lag = hand_off(q)
-                if squares_due(g - PASSES - 2 * lag) >= R_CHUNKS * len([jt for jt in scalar_tiles if jt < GROUPS[q][1]]):
+                if squares_due(g - PASSES - 1) >= R_CHUNKS * len([jt for jt in scalar_tiles if jt < GROUPS[q][1]]):
                     agenda.setdefault(n, []).append((sum_r2, q))
                     agenda.setdefault(n + lag, []).append((spread_r2, q))
                     agenda.setdefault(n + 2 * lag, []).append((halve_r2, q))
-                    state["halved"] = n + 2 * lag
+                    halved[q] = n + 2 * lag + 1
+                    plan_distances(q)
                     state["prepared"] += 1
             for entry in agenda.get(n, []):
                 entry[0](entry[1])
@@ -463,8 +462,9 @@ def tile_kernelloglikelihood_k_kernel(
         late_tiles["w_max"] = late.tile([P, I_TILES, len(GROUPS)], F32, name="w_max")
         late_tiles["neg_l_max"] = late.tile([P, I_TILES, len(GROUPS)], F32, name="neg_l_max")
         late_tiles["sums"] = late.tile([P, I_TILES, len(GROUPS)], F32, name="sums")
-        for n in range(Z_DONE, N_BANKS + 5):
+        for n in range(Z_DONE, N_BANKS + 6):
             step(n)
+        assert max(agenda) < N_BANKS + 6 and state["product"] == 2 * J_TILES * I_TILES
 
         top = late.tile([P, I_TILES], F32)
         nc.vector.tensor_reduce(out=top[:], in_=late_tiles["w_max"][:], axis=AX.X, op=ALU.max)

@@ -62,7 +62,6 @@ def tile_kernelloglikelihood_k_kernel(
         unread = stack.enter_context(tc.tile_pool(name="unread", bufs=2))
         work = stack.enter_context(tc.psum_pool(name="work", bufs=4))
         acc = stack.enter_context(tc.psum_pool(name="acc", bufs=1))
-        stack.enter_context(tc.manual_schedule())
 
         ident = const.tile([P, P], F32)
         z_codes = const.tile([P, PASSES, B], U32, align_bytes=64)

@@ -20,31 +20,28 @@ K_PASS = 4 * P
 BANK = 512
 I_TILES = B // P
 J_TILES = NREF // P
-J_HALVES = NREF // BANK
 PASSES = DC // K_PASS
-HALF = PASSES // 2
-TILE_BANKS = PASSES // 2
-HALF_BANKS = TILE_BANKS // 2
-N_BANKS = J_TILES * TILE_BANKS
+GROUPS = ((0, 4), (4, 6), (6, 8))
+UNIT_COLS = 4 * BANK
+CHUNK_UNITS = 2
 W_PLANES = 4
-R_CHUNK = 2048
-R_CHUNKS = DC // R_CHUNK
-R_BUFS = 4
+R_BUFS = 7
 W_BUFS = 6
-Z_FIRST = TILE_BANKS
-Z_GROUP = 4
-Z_DONE = Z_FIRST + PASSES + 3
-GRAM_FROM, GRAM_TILES = 1, 2
-Y_BANKS = 3
-X_STEP = 3
-LOADS_FROM = Z_FIRST + PASSES - W_BUFS + 1
-Q_BUFS = 8
-GROUPS = ((0, 4), (4, 7), (7, 8))
-GROUP_LAG = 3
+Q_BUFS = 12
+Z_LAG = 2
+Z_PAIR = 2
+GRAM_CHUNKS = (8, 3, 2)
+STEPS_BEHIND = 4
 
 FLOPS = 2 * B * D * DC + 2 * B * DC * NREF
 
-assert 2 * P * P * P * 4 * PASSES * GRAM_TILES <= FLOPS // 10
+UNITS = [
+    (q, t0, t1 - t0, g, 4 // (t1 - t0))
+    for q, (t0, t1) in enumerate(GROUPS)
+    for g in range(0, PASSES, 4 // (t1 - t0))
+]
+LAST = [max(n for n, unit in enumerate(UNITS) if unit[0] == q) for q in range(len(GROUPS))]
+FIRST = [min(n for n, unit in enumerate(UNITS) if unit[0] == q) for q in range(len(GROUPS))]
 
 SQRT_2PI_HI = 41069.0 / 16384.0
 COEFF_REST = -math.log(NREF) - DC * math.log(math.sqrt(2.0 * math.pi) / SQRT_2PI_HI)
@@ -57,122 +54,127 @@ def tile_kernelloglikelihood_k_kernel(
     with ExitStack() as stack:
         const = stack.enter_context(tc.tile_pool(name="const", bufs=1))
         r_rows = stack.enter_context(tc.tile_pool(name="r_rows", bufs=R_BUFS))
-        r_stage = stack.enter_context(tc.tile_pool(name="r_stage", bufs=4))
+        r_stage = stack.enter_context(tc.tile_pool(name="r_stage", bufs=5))
         r_quant = stack.enter_context(tc.tile_pool(name="r_quant", bufs=Q_BUFS))
+        w_pool = stack.enter_context(tc.tile_pool(name="w_pool", bufs=W_BUFS))
+        z_stage = stack.enter_context(tc.tile_pool(name="z_stage", bufs=4))
+        z_group = stack.enter_context(tc.tile_pool(name="z_group", bufs=2))
         unread = stack.enter_context(tc.tile_pool(name="unread", bufs=2))
-        work = stack.enter_context(tc.psum_pool(name="work", bufs=4))
+        work = stack.enter_context(tc.psum_pool(name="work", bufs=3))
         acc = stack.enter_context(tc.psum_pool(name="acc", bufs=1))
 
         ident = const.tile([P, P], F32)
         z_codes = const.tile([P, PASSES, B], U32, align_bytes=64)
         z_scales = const.tile([P, PASSES, B], U8, align_bytes=64)
         z2_parts = const.tile([P, I_TILES, PASSES], F32)
-        r2_parts = const.tile([P, J_TILES, R_CHUNKS], F32)
-        scalar_tiles = [jt for jt in range(J_TILES) if not GRAM_FROM <= jt < GRAM_FROM + GRAM_TILES]
+        r2_parts = const.tile([P, J_TILES, 8], F32)
 
-        cross = {}
         r_sb = {}
         rt_ps = {}
         r_grouped = {}
         r_codes = {}
         r_scales = {}
-        gram_todo = []
-        product_todo = []
-        state = {"gram": 0, "product": 0, "diagonals": -1, "prepared": 0}
-        multiplied = {}
-        halved = {}
-        agenda = {}
+        cross = {}
+        gram_ps = {}
 
-        def hand_off(q):
-            return GROUP_LAG if q < len(GROUPS) - 1 else 1
+        def chunk_cols(k):
+            q, t0, nt, g0, np_ = UNITS[k * CHUNK_UNITS]
+            return g0 * K_PASS, CHUNK_UNITS * np_ * K_PASS
 
-        def plan_distances(q):
-            if q in multiplied and q in halved:
-                first = max(multiplied[q], halved[q])
-                agenda.setdefault(first, []).append((distances, q))
-                agenda.setdefault(first + hand_off(q) - 1, []).append((exponentials, q))
+        def load_reference(k, part=0, parts=1):
+            q, t0, nt, g0, np_ = UNITS[k * CHUNK_UNITS]
+            c0, width = chunk_cols(k)
+            if part == 0:
+                r_sb[k] = r_rows.tile([P, nt, width], BF16, name="r_sb")
+            lo, hi = part * width // parts, (part + 1) * width // parts
+            nc.sync.dma_start(
+                out=r_sb[k][:, :, lo:hi],
+                in_=X_ref[t0 * P : (t0 + nt) * P, c0 + lo : c0 + hi].rearrange("(t p) c -> p t c", p=P),
+            )
 
-        def load_reference(chunk):
-            jt, q = chunk // R_CHUNKS, chunk % R_CHUNKS
-            if q == 0:
-                r_sb[jt] = r_rows.tile([P, DC], BF16, name="r_sb")
-            cols = slice(q * R_CHUNK, (q + 1) * R_CHUNK)
-            nc.sync.dma_start(out=r_sb[jt][:, cols], in_=X_ref[jt * P : (jt + 1) * P, cols])
+        def chunk_index(k):
+            return k - FIRST[UNITS[k * CHUNK_UNITS][0]] // CHUNK_UNITS
 
-        def square_r(k):
-            jt, q = scalar_tiles[k // R_CHUNKS], k % R_CHUNKS
-            rows = r_sb[jt][:, q * R_CHUNK : (q + 1) * R_CHUNK]
-            r_sq = unread.tile([P, R_CHUNK], BF16, tag="by_scalar")
-            nc.scalar.activation(out=r_sq[:], in_=rows, func=ACT.Square, accum_out=r2_parts[:, jt, q : q + 1])
+        def gram_units(q):
+            first = FIRST[q] + (0 if q == 0 else CHUNK_UNITS)
+            return range(first, first + GRAM_CHUNKS[q] * CHUNK_UNITS)
 
-        def transpose_r(n):
-            jt, b = n // TILE_BANKS, n % TILE_BANKS
-            r_words = r_sb[jt][:].bitcast(F32)
-            rt_ps[n] = work.tile([P, 2, 2, P], F32, tag="work", name="rt_ps")
+        def by_gram(k, a):
+            return a == 0 and k * CHUNK_UNITS in gram_units(UNITS[k * CHUNK_UNITS][0])
+
+        def square_r(k, a):
+            t0 = UNITS[k * CHUNK_UNITS][1]
+            c0, width = chunk_cols(k)
+            r_sq = unread.tile([P, UNIT_COLS], BF16, tag="by_scalar")
+            nc.scalar.activation(
+                out=r_sq[:, 0:width], in_=r_sb[k][:, a, :], func=ACT.Square,
+                accum_out=r2_parts[:, t0 + a, chunk_index(k) : chunk_index(k) + 1],
+            )
+
+        def transpose_r(n, b):
+            q, t0, nt, g0, np_ = UNITS[n]
+            k = n // CHUNK_UNITS
+            a0, g = (2 * b, g0) if np_ == 1 else (0, g0 + b)
+            rt_ps[(n, b)] = work.tile([P, 2, 2, P], F32, tag="work", name="rt_ps")
             for a in range(2):
+                words = r_sb[k][:, a0 + a, :].bitcast(F32)
                 for u in range(2):
-                    w0 = (2 * b + a) * (K_PASS // 2) + u * P
-                    nc.tensor.transpose(rt_ps[n][:, a, u, :], r_words[:, w0 : w0 + P], ident[:])
+                    w0 = (g * K_PASS - chunk_cols(k)[0]) // 2 + u * P
+                    nc.tensor.transpose(rt_ps[(n, b)][:, a, u, :], words[:, w0 : w0 + P], ident[:])
 
-        def copy_r(n):
-            h, pair = n // HALF_BANKS, n % HALF_BANKS
-            if pair == 0:
-                r_grouped[h] = r_stage.tile([P, HALF, P, 4], BF16, align_bytes=64, name="r_grouped")
-            words = (
-                r_grouped[h][:].rearrange("p g j t -> p (g j t)").bitcast(F32).rearrange("p (g j u) -> p g j u", g=HALF, u=2)
+        def copy_r(n, b):
+            if b == 0:
+                r_grouped[n] = r_stage.tile([P, UNIT_COLS], BF16, align_bytes=64, name="r_grouped")
+            words = r_grouped[n][:].bitcast(F32).rearrange("p (b a j u) -> p b a j u", b=2, a=2, u=2)
+            copy = nc.scalar.copy if n > LAST[0] and n % 3 == 0 and b == 1 else nc.vector.tensor_copy
+            copy(out=words[:, b, :, :, :], in_=rt_ps[(n, b)][:].rearrange("p a u j -> p a j u"))
+
+        def quantise_r(n):
+            r_codes[n] = r_quant.tile([P, BANK], U32, align_bytes=64, name="r_codes")
+            r_scales[n] = r_quant.tile([P, BANK], U8, align_bytes=64, name="r_scales")
+            nc.vector.quantize_mx(out=r_codes[n][:].bitcast(FP8X4), scales=r_scales[n][:], in_=r_grouped[n][:])
+
+        def products(n):
+            q, t0, nt, g0, np_ = UNITS[n]
+            for b in range(np_):
+                cols = slice(b * nt * P, (b + 1) * nt * P)
+                for it in range(I_TILES):
+                    if (it, q) not in cross:
+                        cross[(it, q)] = acc.tile([P, BANK], F32, tag="acc_%d" % (it + I_TILES * (q % 2)), name="cross")
+                    nc.tensor.matmul_mx(
+                        out=cross[(it, q)][:, 0 : nt * P],
+                        lhsT=z_codes[:, g0 + b, it * P : (it + 1) * P].bitcast(FP8X4),
+                        lhsT_scale=z_scales[:, g0 + b, it * P : (it + 1) * P],
+                        rhs=r_codes[n][:, cols].bitcast(FP8X4),
+                        rhs_scale=r_scales[n][:, cols],
+                        start=(g0 + b == 0),
+                        stop=(g0 + b == PASSES - 1),
+                    )
+
+        def gram(n):
+            q, t0, nt, g0, np_ = UNITS[n]
+            if q not in gram_ps:
+                gram_ps[q] = acc.tile([P, P], F32, tag="gram", name="gram_ps")
+            columns = r_grouped[n][:].rearrange("p (j t) -> p j t", t=4)
+            for b in range(np_):
+                for t in range(4):
+                    plane = columns[:, b * nt * P : b * nt * P + P, t]
+                    nc.tensor.matmul(
+                        out=gram_ps[q][:],
+                        lhsT=plane,
+                        rhs=plane,
+                        start=(n == gram_units(q)[0] and b == 0 and t == 0),
+                        stop=(n == gram_units(q)[-1] and b == np_ - 1 and t == 3),
+                    )
+
+        def diagonal(q):
+            off_diagonal = unread.tile([P, P], F32, tag="by_vector")
+            nc.vector.scalar_tensor_tensor(
+                out=off_diagonal[:], in0=gram_ps[q][:], scalar=1.0, in1=ident[:], op0=ALU.mult, op1=ALU.mult,
+                accum_out=r2_parts[:, GROUPS[q][0], 7:8],
             )
-            copy = nc.scalar.copy if Z_FIRST <= n < Z_FIRST + PASSES else nc.vector.tensor_copy
-            copy(out=words[:, 2 * pair : 2 * pair + 2, :, :], in_=rt_ps[n][:].rearrange("p a u j -> p a j u"))
 
-        def quantise_r(h):
-            r_codes[h] = r_quant.tile([P, HALF, P], U32, align_bytes=64, name="r_codes")
-            r_scales[h] = r_quant.tile([P, HALF, P], U8, align_bytes=64, name="r_scales")
-            nc.vector.quantize_mx(
-                out=r_codes[h][:].rearrange("p g j -> p (g j)").bitcast(FP8X4),
-                scales=r_scales[h][:].rearrange("p g j -> p (g j)"),
-                in_=r_grouped[h][:].rearrange("p g j t -> p (g j t)"),
-            )
-
-        def products(h, it):
-            jt, first = h // 2, (h % 2) * HALF
-            q = len([group for group in GROUPS if jt >= group[0]]) - 1
-            if (it, q) not in cross:
-                cross[(it, q)] = acc.tile([P, BANK], F32, tag="acc_%d" % (it + I_TILES * (q % 2)), name="cross")
-            cols = slice((jt - GROUPS[q][0]) * P, (jt - GROUPS[q][0] + 1) * P)
-            for g in range(first, first + HALF):
-                nc.tensor.matmul_mx(
-                    out=cross[(it, q)][:, cols],
-                    lhsT=z_codes[:, g, it * P : (it + 1) * P].bitcast(FP8X4),
-                    lhsT_scale=z_scales[:, g, it * P : (it + 1) * P],
-                    rhs=r_codes[h][:, g - first, :].bitcast(FP8X4),
-                    rhs_scale=r_scales[h][:, g - first, :],
-                    start=(g == 0),
-                    stop=(g == PASSES - 1),
-                )
-
-        gram_ps = acc.tile([P, GRAM_TILES, P], F32, tag="acc_%d" % Y_BANKS)
-
-        def gram(jt, g):
-            for t in range(4):
-                plane = r_grouped[2 * jt + g // HALF][:, g % HALF, :, t]
-                nc.tensor.matmul(
-                    out=gram_ps[:, jt - GRAM_FROM, :],
-                    lhsT=plane,
-                    rhs=plane,
-                    start=(g == 0 and t == 0),
-                    stop=(g == PASSES - 1 and t == 3),
-                )
-
-        def diagonals():
-            for jt in range(GRAM_FROM, GRAM_FROM + GRAM_TILES):
-                off_diagonal = unread.tile([P, P], F32, tag="by_vector")
-                nc.vector.scalar_tensor_tensor(
-                    out=off_diagonal[:], in0=gram_ps[:, jt - GRAM_FROM, :], scalar=1.0, in1=ident[:],
-                    op0=ALU.mult, op1=ALU.mult, accum_out=r2_parts[:, jt, 0:1],
-                )
-
-        pools = {}
-        early_tiles = {}
+        early = {}
         w_words = {}
         bias = {}
         y_ps = {}
@@ -180,66 +182,62 @@ def tile_kernelloglikelihood_k_kernel(
         z_bf = {}
         zt_ps = {}
         z_grouped = {}
-        units = [(g, it) for g in range(PASSES) for it in range(I_TILES)]
 
         def load_w(g):
-            cols = slice(g * K_PASS, (g + 1) * K_PASS)
-            w_words[g] = pools["w"].tile([P, K_PASS], U32, align_bytes=64, name="w_words")
+            w_words[g] = w_pool.tile([P, K_PASS], U32, align_bytes=64, name="w_words")
             w_bytes = pca_weight_words[0].rearrange("p n t -> p (n t)")
             nc.sync.dma_start(out=w_words[g][:].bitcast(I32), in_=w_bytes[:, 4 * g * K_PASS : 4 * (g + 1) * K_PASS].bitcast(I32))
-            bias[g] = pools["w"].tile([P, K_PASS], BF16, name="bias")
-            nc.sync.dma_start(out=bias[g][:], in_=pca_bias[cols].partition_broadcast(P))
-            if g % 2 == 0:
-                load_reference(R_CHUNKS + g // 2)
-            if g == PASSES - 1:
-                for chunk in range(R_CHUNKS + PASSES // 2, R_BUFS * R_CHUNKS):
-                    load_reference(chunk)
+            bias[g] = w_pool.tile([P, K_PASS], BF16, name="bias")
+            nc.sync.dma_start(out=bias[g][:], in_=pca_bias[g * K_PASS : (g + 1) * K_PASS].partition_broadcast(P))
 
         def transpose_x():
-            x_words = early_tiles["x_sb"][:].bitcast(F32)
-            early_tiles["xt_ps"] = work.tile([P, I_TILES, 2, P], F32, tag="work", name="xt_ps")
+            x_words = early["x_sb"][:].bitcast(F32)
+            early["xt_ps"] = work.tile([P, I_TILES, 2, P], F32, tag="work", name="xt_ps")
             for it in range(I_TILES):
                 for u in range(2):
-                    nc.tensor.transpose(early_tiles["xt_ps"][:, it, u, :], x_words[:, it, u : D // 2 : 2], ident[:])
+                    nc.tensor.transpose(early["xt_ps"][:, it, u, :], x_words[:, it, u : D // 2 : 2], ident[:])
 
         def copy_x():
             nc.vector.tensor_copy(
-                out=early_tiles["x_grouped"][:]
-                .rearrange("p i t -> p (i t)")
-                .bitcast(F32)
-                .rearrange("p (a i u) -> p a i u", a=I_TILES, u=2),
-                in_=early_tiles["xt_ps"][:].rearrange("p a u i -> p a i u"),
+                out=early["x_grouped"][:].bitcast(F32).rearrange("p (a i u) -> p a i u", a=I_TILES, u=2),
+                in_=early["xt_ps"][:].rearrange("p a u i -> p a i u"),
             )
 
         def quantise_x():
-            nc.vector.quantize_mx(
-                out=early_tiles["x_codes"][:].bitcast(FP8X4),
-                scales=early_tiles["x_scales"][:],
-                in_=early_tiles["x_grouped"][:].rearrange("p i t -> p (i t)"),
-            )
+            nc.vector.quantize_mx(out=early["x_codes"][:].bitcast(FP8X4), scales=early["x_scales"][:], in_=early["x_grouped"][:])
 
-        def project(g, it):
+        def project(g):
             plane, col0 = (g * K_PASS) // (DC // W_PLANES), (g * K_PASS) % (DC // W_PLANES)
-            y_ps[(g, it)] = acc.tile([P, K_PASS], F32, tag="acc_%d" % ((I_TILES * g + it) % Y_BANKS), name="y_ps")
-            nc.tensor.matmul_mx(
-                out=y_ps[(g, it)][:],
-                lhsT=early_tiles["x_codes"][:, it * P : (it + 1) * P].bitcast(FP8X4),
-                lhsT_scale=early_tiles["x_scales"][:, it * P : (it + 1) * P],
-                rhs=w_words[g][:].bitcast(FP8X4),
-                rhs_scale=early_tiles["w_planes"][4 * plane : P, col0 : col0 + K_PASS],
-                start=True,
-                stop=True,
-            )
+            for it in range(I_TILES):
+                y_ps[(g, it)] = acc.tile([P, K_PASS], F32, tag="acc_%d" % (I_TILES + it), name="y_ps")
+                nc.tensor.matmul_mx(
+                    out=y_ps[(g, it)][:],
+                    lhsT=early["x_codes"][:, it * P : (it + 1) * P].bitcast(FP8X4),
+                    lhsT_scale=early["x_scales"][:, it * P : (it + 1) * P],
+                    rhs=w_words[g][:].bitcast(FP8X4),
+                    rhs_scale=early["w_planes"][4 * plane : P, col0 : col0 + K_PASS],
+                    start=True,
+                    stop=True,
+                )
 
-        def finish_z(g, it):
-            z_f32[(g, it)] = pools["z"].tile([P, K_PASS], F32, name="z_f32")
-            nc.vector.tensor_tensor(out=z_f32[(g, it)][:], in0=y_ps[(g, it)][:], in1=bias[g][:], op=ALU.add)
-            z_sq = unread.tile([P, K_PASS], BF16, tag="by_scalar")
-            nc.scalar.activation(out=z_sq[:], in_=z_f32[(g, it)][:], func=ACT.Square, accum_out=z2_parts[:, it, g : g + 1])
-            z_bf[(g, it)] = pools["z"].tile([P, K_PASS], BF16, name="z_bf")
-            nc.gpsimd.tensor_scalar(
-                out=z_bf[(g, it)][:], in0=z_f32[(g, it)][:], scalar1=1.0, scalar2=0.0, op0=ALU.mult, op1=ALU.add
-            )
+        def add_bias(g):
+            for it in range(I_TILES):
+                z_f32[(g, it)] = z_stage.tile([P, K_PASS], F32, name="z_f32")
+                nc.vector.tensor_tensor(out=z_f32[(g, it)][:], in0=y_ps[(g, it)][:], in1=bias[g][:], op=ALU.add)
+
+        def round_z(g):
+            for it in range(I_TILES):
+                z_bf[(g, it)] = z_stage.tile([P, K_PASS], BF16, name="z_bf")
+                nc.gpsimd.tensor_scalar(
+                    out=z_bf[(g, it)][:], in0=z_f32[(g, it)][:], scalar1=1.0, scalar2=0.0, op0=ALU.mult, op1=ALU.add
+                )
+
+        def square_z(g):
+            for it in range(I_TILES):
+                z_sq = unread.tile([P, UNIT_COLS], BF16, tag="by_scalar")
+                nc.scalar.activation(
+                    out=z_sq[:, 0:K_PASS], in_=z_f32[(g, it)][:], func=ACT.Square, accum_out=z2_parts[:, it, g : g + 1]
+                )
 
         def transpose_z(g):
             zt_ps[g] = work.tile([P, I_TILES, 2, P], F32, tag="work", name="zt_ps")
@@ -249,41 +247,42 @@ def tile_kernelloglikelihood_k_kernel(
                     nc.tensor.transpose(zt_ps[g][:, it, u, :], z_words[:, u * P : (u + 1) * P], ident[:])
 
         def copy_z(g):
-            if g % Z_GROUP == 0:
-                z_grouped[g // Z_GROUP] = pools["z_group"].tile([P, Z_GROUP, B, 4], BF16, align_bytes=64, name="z_grouped")
-            words = (
-                z_grouped[g // Z_GROUP][:]
-                .rearrange("p g i t -> p (g i t)")
-                .bitcast(F32)
-                .rearrange("p (g a i u) -> p g a i u", g=Z_GROUP, a=I_TILES, u=2)
-            )
-            copy = nc.vector.tensor_copy if g % 2 == 0 else nc.scalar.copy
-            copy(out=words[:, g % Z_GROUP, :, :, :], in_=zt_ps[g][:].rearrange("p a u i -> p a i u"))
+            if g % Z_PAIR == 0:
+                z_grouped[g // Z_PAIR] = z_group.tile([P, Z_PAIR * B * 4], BF16, align_bytes=64, name="z_grouped")
+            words = z_grouped[g // Z_PAIR][:].bitcast(F32).rearrange("p (g a i u) -> p g a i u", g=Z_PAIR, a=I_TILES, u=2)
+            copy = nc.vector.tensor_copy if g % 4 == 1 else nc.scalar.copy
+            copy(out=words[:, g % Z_PAIR, :, :, :], in_=zt_ps[g][:].rearrange("p a u i -> p a i u"))
 
-        def quantise_z(group):
-            passes = slice(group * Z_GROUP, (group + 1) * Z_GROUP)
+        def quantise_z(pair):
+            passes = slice(pair * Z_PAIR, (pair + 1) * Z_PAIR)
             nc.vector.quantize_mx(
                 out=z_codes[:, passes, :].rearrange("p g i -> p (g i)").bitcast(FP8X4),
                 scales=z_scales[:, passes, :].rearrange("p g i -> p (g i)"),
-                in_=z_grouped[group][:].rearrange("p g i t -> p (g i t)"),
+                in_=z_grouped[pair][:],
             )
 
-        late_tiles = {}
+        late = {}
         r2_ps = {}
+
+        def sum_z2():
+            nc.vector.tensor_reduce(out=late["z2"][:], in_=z2_parts[:], axis=AX.X, op=ALU.add)
+
+        def halve_z2():
+            nc.vector.tensor_scalar(out=late["z2_half"][:], in0=late["z2"][:], scalar1=-0.5, scalar2=None, op0=ALU.mult)
 
         def sum_r2(q):
             t0, t1 = GROUPS[q]
-            nc.vector.tensor_reduce(out=late_tiles["r2"][:, t0:t1], in_=r2_parts[:, t0:t1, :], axis=AX.X, op=ALU.add)
+            nc.vector.tensor_reduce(out=late["r2"][:, t0:t1], in_=r2_parts[:, t0:t1, :], axis=AX.X, op=ALU.add)
 
         def spread_r2(q):
             t0, t1 = GROUPS[q]
             r2_ps[q] = work.tile([P, t1 - t0, P], F32, tag="work", name="r2_ps")
             for jt in range(t0, t1):
-                nc.tensor.transpose(r2_ps[q][:, jt - t0, :], late_tiles["r2"][:, jt : jt + 1].to_broadcast([P, P]), ident[:])
+                nc.tensor.transpose(r2_ps[q][:, jt - t0, :], late["r2"][:, jt : jt + 1].to_broadcast([P, P]), ident[:])
 
         def halve_r2(q):
             nc.vector.tensor_scalar(
-                out=late_tiles["r2_half"][:, GROUPS[q][0] * P : GROUPS[q][1] * P],
+                out=late["r2_half"][:, GROUPS[q][0] * P : GROUPS[q][1] * P],
                 in0=r2_ps[q][:].rearrange("p m j -> p (m j)"),
                 scalar1=-0.5,
                 scalar2=None,
@@ -292,200 +291,221 @@ def tile_kernelloglikelihood_k_kernel(
 
         def distances(q):
             cols = slice(GROUPS[q][0] * P, GROUPS[q][1] * P)
-            w = late_tiles["w"]
+            w = late["w"]
             for it in range(I_TILES):
                 nc.vector.scalar_tensor_tensor(
                     out=w[it][:, cols],
                     in0=cross[(it, q)][:, 0 : (GROUPS[q][1] - GROUPS[q][0]) * P],
-                    scalar=late_tiles["z2_half"][:, it : it + 1],
-                    in1=late_tiles["r2_half"][:, cols],
+                    scalar=late["z2_half"][:, it : it + 1],
+                    in1=late["r2_half"][:, cols],
                     op0=ALU.add,
                     op1=ALU.add,
                 )
             for it in range(I_TILES):
                 nc.vector.tensor_scalar(
                     out=w[it][:, cols], in0=w[it][:, cols], scalar1=0.0, scalar2=None, op0=ALU.min, op1=ALU.max,
-                    accum_out=late_tiles["w_max"][:, it, q : q + 1],
+                    accum_out=late["w_max"][:, it, q : q + 1],
                 )
-            nc.vector.tensor_scalar(
-                out=late_tiles["neg_l_max"][:, :, q], in0=late_tiles["w_max"][:, :, q], scalar1=late_tiles["inv_h2"][:],
-                scalar2=-1.0, op0=ALU.mult, op1=ALU.mult,
-            )
+            if q < len(GROUPS) - 1:
+                nc.vector.tensor_scalar(
+                    out=late["neg_l_max"][:, :, q], in0=late["w_max"][:, :, q], scalar1=late["inv_h2"][:],
+                    scalar2=-1.0, op0=ALU.mult, op1=ALU.mult,
+                )
 
         def exponentials(q):
             cols = slice(GROUPS[q][0] * P, GROUPS[q][1] * P)
-            w = late_tiles["w"]
+            w = late["w"]
             for it in range(I_TILES):
-                e_w = unread.tile([P, BANK], BF16, tag="by_scalar")
+                e_w = unread.tile([P, UNIT_COLS], BF16, tag="by_scalar")
                 nc.scalar.activation(
                     out=e_w[:, 0 : (GROUPS[q][1] - GROUPS[q][0]) * P],
                     in_=w[it][:, cols],
                     func=ACT.Exp,
-                    scale=late_tiles["inv_h2"][:],
-                    bias=late_tiles["neg_l_max"][:, it, q : q + 1],
-                    accum_out=late_tiles["sums"][:, it, q : q + 1],
+                    scale=late["inv_h2"][:],
+                    bias=late["neg_l_max"][:, it, q : q + 1],
+                    accum_out=late["sums"][:, it, q : q + 1],
                 )
 
-        def squares_due(m):
-            left, banks = (len(scalar_tiles) - 1) * R_CHUNKS, N_BANKS - Z_FIRST - PASSES
-            return R_CHUNKS + min(left, left * max(m, 0) // banks)
+        n_units = len(UNITS)
+        product_todo = []
+        early_agenda = {}
+        agenda = {}
+
+        def plan(step_, function, *args):
+            agenda.setdefault(step_, []).append((function, args))
+
+        def plan_early(step_, function, *args):
+            early_agenda.setdefault(step_, []).append((function, args))
+
+        def squares_of(n):
+            k = n // CHUNK_UNITS
+            tiles = [a for a in range(UNITS[n][2]) if not by_gram(k, a)]
+            cut = (len(tiles) + 1) // 2 if n < len(UNITS) - CHUNK_UNITS else len(tiles)
+            return [(k, a) for a in (tiles[:cut] if n % CHUNK_UNITS == 0 else tiles[cut:])]
 
         def step(n):
-            g = n - Z_FIRST
-            if n == 0:
-                for k in range(R_CHUNKS):
-                    square_r(k)
+            g = n - Z_LAG
             if 0 <= g < PASSES:
-                for it in range(I_TILES):
-                    finish_z(g, it)
-                for later in units[I_TILES * g + Y_BANKS : I_TILES * (g + 1) + Y_BANKS]:
-                    project(later[0], later[1])
-                if g + W_BUFS < PASSES:
-                    load_w(g + W_BUFS)
-            if n == X_STEP:
+                add_bias(g)
+                round_z(g)
+            for entry in early_agenda.get(n, []):
+                entry[0](*entry[1])
+            if n < n_units:
+                for b in range(2):
+                    transpose_r(n, b)
+            if n == 0:
                 transpose_x()
+                copy_x()
+                quantise_x()
             if 1 <= g <= PASSES:
                 transpose_z(g - 1)
-            if n < N_BANKS:
-                transpose_r(n)
-            if n == Z_FIRST - 1:
-                for first in units[:Y_BANKS]:
-                    project(first[0], first[1])
-            for piece in gram_todo[state["gram"] : state["gram"] + 2]:
-                if piece[0] <= n:
-                    gram(piece[1], piece[2])
-                    state["gram"] += 1
-                    if state["gram"] == GRAM_TILES * PASSES:
-                        state["diagonals"] = n + 2
-            if n % 2 == 0 or n >= N_BANKS:
-                for piece in product_todo[state["product"] : state["product"] + 2]:
-                    if piece[0] <= n:
-                        products(piece[1], piece[2])
-                        state["product"] += 1
-                        for q in range(len(GROUPS)):
-                            if piece[1] == 2 * GROUPS[q][1] - 1 and piece[2] == I_TILES - 1:
-                                multiplied[q] = n + hand_off(q)
-                                plan_distances(q)
-            if n == X_STEP + 1:
-                copy_x()
-            if n == X_STEP + 2:
-                quantise_x()
-            if 2 <= g <= PASSES + 1:
-                copy_z(g - 2)
-            if 1 <= n <= N_BANKS:
-                copy_r(n - 1)
-                if n % HALF_BANKS == 0 and GRAM_FROM <= (n - 1) // TILE_BANKS < GRAM_FROM + GRAM_TILES:
-                    h = n // HALF_BANKS - 1
-                    gram_todo.extend([(n + 1, h // 2, (h % 2) * HALF + a) for a in range(HALF)])
-            if g >= Z_GROUP + 2 and (g - 2) % Z_GROUP == 0 and g <= PASSES + 2:
-                quantise_z((g - 2) // Z_GROUP - 1)
-            if (n > HALF_BANKS and n % HALF_BANKS == 1 and n < N_BANKS) or n == N_BANKS:
-                h = n // HALF_BANKS - 1
-                quantise_r(h)
-                product_todo.extend([(max(min(n + 2, N_BANKS + 1), Z_DONE + 1), h, it) for it in range(I_TILES)])
-            if n == state["diagonals"]:
-                diagonals()
-            for k in range(squares_due(g - PASSES), squares_due(g - PASSES + 1)):
-                square_r(k)
-            q = state["prepared"]
-            if q < len(GROUPS) and n > max(state["diagonals"], Z_DONE) > 0:
-                lag = hand_off(q)
-                if squares_due(g - PASSES - 1) >= R_CHUNKS * len([jt for jt in scalar_tiles if jt < GROUPS[q][1]]):
-                    agenda.setdefault(n, []).append((sum_r2, q))
-                    agenda.setdefault(n + lag, []).append((spread_r2, q))
-                    agenda.setdefault(n + 2 * lag, []).append((halve_r2, q))
-                    halved[q] = n + 2 * lag + 1
-                    plan_distances(q)
-                    state["prepared"] += 1
+            if 0 <= g + 1 < PASSES:
+                project(g + 1)
+            if n % 2 == 0 or n >= n_units:
+                count = 0
+                while product_todo and product_todo[0][0] <= n and count < 3:
+                    unit = product_todo[0][1]
+                    products(unit)
+                    product_todo.remove(product_todo[0])
+                    count += 1
+                    for q in range(len(GROUPS)):
+                        if unit == LAST[q]:
+                            if q < len(GROUPS) - 1:
+                                plan(n + 2, distances, q)
+                                plan(n + 3, exponentials, q)
+                            else:
+                                plan(n + 1, distances, q)
+            if 1 <= n <= n_units and n - 1 in gram_units(UNITS[n - 1][0]):
+                gram(n - 1)
+            if n < n_units:
+                for b in range(2):
+                    copy_r(n, b)
+            if 1 <= g <= PASSES:
+                square_z(g - 1)
+                copy_z(g - 1)
+            if n < n_units:
+                for piece in squares_of(n):
+                    square_r(piece[0], piece[1])
+            if 1 <= n < n_units:
+                quantise_r(n - 1)
+            if n == n_units - 1:
+                quantise_r(n)
+            if g >= Z_PAIR + 1 and (g - 1) % Z_PAIR == 0 and (g - 1) // Z_PAIR <= PASSES // Z_PAIR:
+                quantise_z((g - 1) // Z_PAIR - 1)
             for entry in agenda.get(n, []):
-                entry[0](entry[1])
-            if n >= LOADS_FROM and (n - LOADS_FROM) % TILE_BANKS == 0 and (n - LOADS_FROM) // TILE_BANKS + R_BUFS < J_TILES:
-                for q in range(R_CHUNKS):
-                    load_reference(((n - LOADS_FROM) // TILE_BANKS + R_BUFS) * R_CHUNKS + q)
+                entry[0](*entry[1])
+            if 0 <= g and g + W_BUFS < PASSES:
+                load_w(g + W_BUFS)
+            k = n // CHUNK_UNITS + R_BUFS
+            if n % CHUNK_UNITS == 1 and k * CHUNK_UNITS < n_units:
+                load_reference(k)
 
-        with ExitStack() as early_stack:
-            early = early_stack.enter_context(tc.tile_pool(name="early", bufs=1))
-            pools["w"] = early_stack.enter_context(tc.tile_pool(name="w_pool", bufs=W_BUFS))
-            pools["z"] = early_stack.enter_context(tc.tile_pool(name="z_stage", bufs=4))
-            pools["z_group"] = early_stack.enter_context(tc.tile_pool(name="z_group", bufs=2))
-
-            h_bf = const.tile([P, 1], BF16)
-            nc.sync.dma_start(out=h_bf[:], in_=bandwidth.partition_broadcast(P))
-            load_reference(0)
-            early_tiles["x_sb"] = early.tile([P, I_TILES, D], BF16, name="x_sb")
-            nc.sync.dma_start(out=early_tiles["x_sb"][:], in_=x.rearrange("(t p) k -> p t k", p=P))
-            for chunk in range(1, R_CHUNKS):
-                load_reference(chunk)
-            early_tiles["w_planes"] = early.tile([P, DC // W_PLANES], U8, align_bytes=64, name="w_planes")
-            nc.vector.memset(early_tiles["w_planes"][:].bitcast(I32), 0)
-            for quad in range(4):
-                nc.sync.dma_start(
-                    out=early_tiles["w_planes"][32 * quad : 32 * quad + 4 * W_PLANES, :].bitcast(I32),
-                    in_=pca_weight_scales[0][4 * quad : 4 * quad + 4, :].rearrange("r (n c) -> n r c", n=W_PLANES).bitcast(I32),
-                )
-            for g in range(W_BUFS):
-                load_w(g)
-            early_tiles["x_grouped"] = early.tile([P, B, 4], BF16, align_bytes=64, name="x_grouped")
-            early_tiles["x_codes"] = early.tile([P, B], U32, align_bytes=64, name="x_codes")
-            early_tiles["x_scales"] = early.tile([P, B], U8, align_bytes=64, name="x_scales")
-
-            make_identity(nc, ident[:])
-            res_pad = const.tile([P, P], F32)
-            nc.vector.memset(res_pad[:], 0.0)
-            nc.vector.memset(r2_parts[:], 0.0)
-            h32 = const.tile([P, 1], F32)
-            nc.vector.tensor_copy(out=h32[:], in_=h_bf[:])
-            h_sq = const.tile([P, 1], F32)
-            nc.vector.tensor_tensor(out=h_sq[:], in0=h32[:], in1=h32[:], op=ALU.mult)
-            inv_h2 = const.tile([P, 1], F32)
-            nc.vector.reciprocal(out=inv_h2[:], in_=h_sq[:])
-            ln_h = const.tile([P, 1], F32)
-            nc.scalar.activation(out=ln_h[:], in_=h32[:], func=ACT.Ln, scale=SQRT_2PI_HI)
-            coeff = const.tile([P, 1], F32)
-            nc.vector.tensor_scalar(
-                out=coeff[:], in0=ln_h[:], scalar1=-float(DC), scalar2=COEFF_REST, op0=ALU.mult, op1=ALU.add
+        h_bf = const.tile([P, 1], BF16)
+        nc.sync.dma_start(out=h_bf[:], in_=bandwidth.partition_broadcast(P))
+        load_reference(0, 0, 2)
+        early["x_sb"] = const.tile([P, I_TILES, D], BF16, name="x_sb")
+        nc.sync.dma_start(out=early["x_sb"][:], in_=x.rearrange("(t p) k -> p t k", p=P))
+        load_reference(0, 1, 2)
+        early["w_planes"] = const.tile([P, DC // W_PLANES], U8, align_bytes=64, name="w_planes")
+        nc.vector.memset(early["w_planes"][:].bitcast(I32), 0)
+        for quad in range(4):
+            nc.sync.dma_start(
+                out=early["w_planes"][32 * quad : 32 * quad + 4 * W_PLANES, :].bitcast(I32),
+                in_=pca_weight_scales[0][4 * quad : 4 * quad + 4, :].rearrange("r (n c) -> n r c", n=W_PLANES).bitcast(I32),
             )
+        load_w(0)
+        load_reference(1)
+        load_w(1)
+        for k in range(2, R_BUFS):
+            if 2 * k - 2 < W_BUFS:
+                load_w(2 * k - 2)
+                load_w(2 * k - 1)
+            load_reference(k)
+        early["x_grouped"] = const.tile([P, B * 4], BF16, align_bytes=64, name="x_grouped")
+        early["x_codes"] = const.tile([P, B], U32, align_bytes=64, name="x_codes")
+        early["x_scales"] = const.tile([P, B], U8, align_bytes=64, name="x_scales")
 
-            for n in range(Z_DONE):
+        make_identity(nc, ident[:])
+        res_pad = const.tile([P, P], F32)
+        nc.vector.memset(res_pad[:], 0.0)
+        nc.vector.memset(r2_parts[:], 0.0)
+        h32 = const.tile([P, 1], F32)
+        nc.vector.tensor_copy(out=h32[:], in_=h_bf[:])
+        h_sq = const.tile([P, 1], F32)
+        nc.vector.tensor_tensor(out=h_sq[:], in0=h32[:], in1=h32[:], op=ALU.mult)
+        inv_h2 = const.tile([P, 1], F32)
+        nc.vector.reciprocal(out=inv_h2[:], in_=h_sq[:])
+        ln_h = const.tile([P, 1], F32)
+        nc.scalar.activation(out=ln_h[:], in_=h32[:], func=ACT.Ln, scale=SQRT_2PI_HI)
+        coeff = const.tile([P, 1], F32)
+        nc.vector.tensor_scalar(
+            out=coeff[:], in0=ln_h[:], scalar1=-float(DC), scalar2=COEFF_REST, op0=ALU.mult, op1=ALU.add
+        )
+        late["inv_h2"] = inv_h2
+        late["z2"] = const.tile([P, I_TILES], F32, name="z2")
+        late["z2_half"] = const.tile([P, I_TILES], F32, name="z2_half")
+        late["r2"] = const.tile([P, J_TILES], F32, name="r2")
+        late["r2_half"] = const.tile([P, NREF], F32, name="r2_half")
+        late["w"] = [const.tile([P, NREF], F32, name="w_%d" % it) for it in range(I_TILES)]
+        late["w_max"] = const.tile([P, I_TILES, len(GROUPS)], F32, name="w_max")
+        late["neg_l_max"] = const.tile([P, I_TILES, len(GROUPS)], F32, name="neg_l_max")
+        late["sums"] = const.tile([P, I_TILES, len(GROUPS)], F32, name="sums")
+
+        for n, unit in enumerate(UNITS):
+            ready = n + 2 if n < n_units - 1 else n + 1
+            if unit[0] == 0:
+                ready = max(ready, (unit[3] // Z_PAIR * Z_PAIR + Z_PAIR - 1) + Z_LAG + 3)
+            product_todo.append((ready, n))
+        z_end = Z_LAG + PASSES
+        plan(z_end + 1, sum_z2)
+        plan(z_end + 2, halve_z2)
+        for q in range(len(GROUPS)):
+            end = LAST[q] + 1 if q < len(GROUPS) - 1 else LAST[q]
+            gram_end = gram_units(q)[-1] + 2
+            plan(gram_end, diagonal, q)
+            end = max(end, gram_end)
+            hurry = q == len(GROUPS) - 1
+            plan(end + 1 - hurry, sum_r2, q)
+            plan(end + 2 - hurry, spread_r2, q)
+            plan_early(end + 3 - hurry, halve_r2, q)
+
+        with tc.manual_schedule():
+            for n in range(n_units + STEPS_BEHIND):
                 step(n)
+        assert not product_todo and max(agenda) < n_units + STEPS_BEHIND
 
-        late = stack.enter_context(tc.tile_pool(name="late", bufs=1))
-        late_tiles["inv_h2"] = inv_h2
-        z2 = late.tile([P, I_TILES], F32)
-        nc.vector.tensor_reduce(out=z2[:], in_=z2_parts[:], axis=AX.X, op=ALU.add)
-        late_tiles["z2_half"] = late.tile([P, I_TILES], F32, name="z2_half")
-        nc.vector.tensor_scalar(out=late_tiles["z2_half"][:], in0=z2[:], scalar1=-0.5, scalar2=None, op0=ALU.mult)
-        late_tiles["r2"] = late.tile([P, J_TILES], F32, name="r2")
-        late_tiles["r2_half"] = late.tile([P, NREF], F32, name="r2_half")
-        late_tiles["w"] = [late.tile([P, NREF], F32, name="w_%d" % it) for it in range(I_TILES)]
-        late_tiles["w_max"] = late.tile([P, I_TILES, len(GROUPS)], F32, name="w_max")
-        late_tiles["neg_l_max"] = late.tile([P, I_TILES, len(GROUPS)], F32, name="neg_l_max")
-        late_tiles["sums"] = late.tile([P, I_TILES, len(GROUPS)], F32, name="sums")
-        for n in range(Z_DONE, N_BANKS + 6):
-            step(n)
-        assert max(agenda) < N_BANKS + 6 and state["product"] == 2 * J_TILES * I_TILES
-
-        top = late.tile([P, I_TILES], F32)
-        nc.vector.tensor_reduce(out=top[:], in_=late_tiles["w_max"][:], axis=AX.X, op=ALU.max)
-        neg_l_top = late.tile([P, I_TILES], F32)
+        last = len(GROUPS) - 1
+        top = const.tile([P, I_TILES], F32)
+        nc.vector.tensor_reduce(out=top[:], in_=late["w_max"][:], axis=AX.X, op=ALU.max)
+        neg_l_top = const.tile([P, I_TILES], F32)
         nc.vector.tensor_scalar(out=neg_l_top[:], in0=top[:], scalar1=inv_h2[:], scalar2=-1.0, op0=ALU.mult, op1=ALU.mult)
-        factor = late.tile([P, I_TILES, len(GROUPS)], F32)
+        factor = const.tile([P, I_TILES, last], F32)
         for it in range(I_TILES):
             nc.scalar.activation(
-                out=factor[:, it, :], in_=late_tiles["w_max"][:, it, :], func=ACT.Exp, scale=inv_h2[:],
+                out=factor[:, it, :], in_=late["w_max"][:, it, 0:last], func=ACT.Exp, scale=inv_h2[:],
                 bias=neg_l_top[:, it : it + 1],
             )
-        weighted = late.tile([P, I_TILES, len(GROUPS)], F32)
-        nc.vector.tensor_tensor(out=weighted[:], in0=late_tiles["sums"][:], in1=factor[:], op=ALU.mult)
-        sum_exp = late.tile([P, I_TILES], F32)
+        weighted = const.tile([P, I_TILES, len(GROUPS)], F32)
+        nc.vector.tensor_tensor(out=weighted[:, :, 0:last], in0=late["sums"][:, :, 0:last], in1=factor[:], op=ALU.mult)
+        for it in range(I_TILES):
+            e_w = unread.tile([P, UNIT_COLS], BF16, tag="by_scalar")
+            nc.scalar.activation(
+                out=e_w[:, 0 : (GROUPS[last][1] - GROUPS[last][0]) * P],
+                in_=late["w"][it][:, GROUPS[last][0] * P : GROUPS[last][1] * P],
+                func=ACT.Exp,
+                scale=inv_h2[:],
+                bias=neg_l_top[:, it : it + 1],
+                accum_out=weighted[:, it, last : last + 1],
+            )
+        sum_exp = const.tile([P, I_TILES], F32)
         nc.vector.tensor_reduce(out=sum_exp[:], in_=weighted[:], axis=AX.X, op=ALU.add)
-        ln_sum = late.tile([P, I_TILES], F32)
+        ln_sum = const.tile([P, I_TILES], F32)
         nc.scalar.activation(out=ln_sum[:], in_=sum_exp[:], func=ACT.Ln)
         nc.vector.scalar_tensor_tensor(
             out=res_pad[:, 0:I_TILES], in0=ln_sum[:], scalar=coeff[:], in1=neg_l_top[:], op0=ALU.add, op1=ALU.subtract
         )
         res_ps = work.tile([P, P], F32, tag="work")
         nc.tensor.transpose(res_ps[:], res_pad[:], ident[:])
-        res_rows = late.tile([P, P], F32)
+        res_rows = const.tile([P, P], F32)
         nc.vector.tensor_copy(out=res_rows[:], in_=res_ps[:])
         nc.sync.dma_start(out=out.rearrange("(t p) -> t p", p=P), in_=res_rows[0:I_TILES, :])

@@ -21,16 +21,18 @@ BANK = 512
 I_TILES = B // P
 J_TILES = NREF // P
 PASSES = DC // K_PASS
-GROUPS = ((0, 4), (4, 6), (6, 8))
+GROUPS = ((0, 4), (4, 6), (6, 7), (7, 8))
 UNIT_COLS = 4 * BANK
 CHUNK_UNITS = 2
 W_PLANES = 4
-R_BUFS = 7
+R_BUFS = 6
 W_BUFS = 6
 Q_BUFS = 12
 Z_LAG = 2
 Z_PAIR = 2
-GRAM_CHUNKS = (8, 3, 2)
+SQUARES_BEHIND = 19
+SQUARE_COLS = 2048
+GRAM_CHUNKS = (8, 3, 0, 1)
 STEPS_BEHIND = 4
 
 FLOPS = 2 * B * D * DC + 2 * B * DC * NREF
@@ -96,28 +98,31 @@ def tile_kernelloglikelihood_k_kernel(
             return k - FIRST[UNITS[k * CHUNK_UNITS][0]] // CHUNK_UNITS
 
         def gram_units(q):
-            first = FIRST[q] + (0 if q == 0 else CHUNK_UNITS)
+            first = FIRST[q] + (CHUNK_UNITS if q == 1 else 0)
             return range(first, first + GRAM_CHUNKS[q] * CHUNK_UNITS)
 
         def by_gram(k, a):
             return a == 0 and k * CHUNK_UNITS in gram_units(UNITS[k * CHUNK_UNITS][0])
 
-        def square_r(k, a):
+        def square_r(k, a, part):
             t0 = UNITS[k * CHUNK_UNITS][1]
             c0, width = chunk_cols(k)
-            r_sq = unread.tile([P, UNIT_COLS], BF16, tag="by_scalar")
+            parts = max(1, width // SQUARE_COLS)
+            entry = chunk_index(k) * parts + part
+            cols = slice(part * width // parts, (part + 1) * width // parts)
+            r_sq = unread.tile([P, SQUARE_COLS], BF16, tag="by_scalar")
             nc.scalar.activation(
-                out=r_sq[:, 0:width], in_=r_sb[k][:, a, :], func=ACT.Square,
-                accum_out=r2_parts[:, t0 + a, chunk_index(k) : chunk_index(k) + 1],
+                out=r_sq[:, 0 : width // parts], in_=r_sb[k][:, a, cols], func=ACT.Square,
+                accum_out=r2_parts[:, t0 + a, entry : entry + 1],
             )
 
         def transpose_r(n, b):
             q, t0, nt, g0, np_ = UNITS[n]
             k = n // CHUNK_UNITS
-            a0, g = (2 * b, g0) if np_ == 1 else (0, g0 + b)
             rt_ps[(n, b)] = work.tile([P, 2, 2, P], F32, tag="work", name="rt_ps")
             for a in range(2):
-                words = r_sb[k][:, a0 + a, :].bitcast(F32)
+                g = g0 + (2 * b + a) // nt
+                words = r_sb[k][:, (2 * b + a) % nt, :].bitcast(F32)
                 for u in range(2):
                     w0 = (g * K_PASS - chunk_cols(k)[0]) // 2 + u * P
                     nc.tensor.transpose(rt_ps[(n, b)][:, a, u, :], words[:, w0 : w0 + P], ident[:])
@@ -126,13 +131,19 @@ def tile_kernelloglikelihood_k_kernel(
             if b == 0:
                 r_grouped[n] = r_stage.tile([P, UNIT_COLS], BF16, align_bytes=64, name="r_grouped")
             words = r_grouped[n][:].bitcast(F32).rearrange("p (b a j u) -> p b a j u", b=2, a=2, u=2)
-            copy = nc.scalar.copy if n > LAST[0] and n % 3 == 0 and b == 1 else nc.vector.tensor_copy
+            copy = nc.scalar.copy if n == len(UNITS) - 1 and b == 1 else nc.vector.tensor_copy
             copy(out=words[:, b, :, :, :], in_=rt_ps[(n, b)][:].rearrange("p a u j -> p a j u"))
 
-        def quantise_r(n):
+        def quantise_r(n, parts=1):
             r_codes[n] = r_quant.tile([P, BANK], U32, align_bytes=64, name="r_codes")
             r_scales[n] = r_quant.tile([P, BANK], U8, align_bytes=64, name="r_scales")
-            nc.vector.quantize_mx(out=r_codes[n][:].bitcast(FP8X4), scales=r_scales[n][:], in_=r_grouped[n][:])
+            for part in range(parts):
+                cols = slice(part * BANK // parts, (part + 1) * BANK // parts)
+                nc.vector.quantize_mx(
+                    out=r_codes[n][:, cols].bitcast(FP8X4),
+                    scales=r_scales[n][:, cols],
+                    in_=r_grouped[n][:, 4 * cols.start : 4 * cols.stop],
+                )
 
         def products(n):
             q, t0, nt, g0, np_ = UNITS[n]
@@ -234,7 +245,7 @@ def tile_kernelloglikelihood_k_kernel(
 
         def square_z(g):
             for it in range(I_TILES):
-                z_sq = unread.tile([P, UNIT_COLS], BF16, tag="by_scalar")
+                z_sq = unread.tile([P, SQUARE_COLS], BF16, tag="by_scalar")
                 nc.scalar.activation(
                     out=z_sq[:, 0:K_PASS], in_=z_f32[(g, it)][:], func=ACT.Square, accum_out=z2_parts[:, it, g : g + 1]
                 )
@@ -250,8 +261,7 @@ def tile_kernelloglikelihood_k_kernel(
             if g % Z_PAIR == 0:
                 z_grouped[g // Z_PAIR] = z_group.tile([P, Z_PAIR * B * 4], BF16, align_bytes=64, name="z_grouped")
             words = z_grouped[g // Z_PAIR][:].bitcast(F32).rearrange("p (g a i u) -> p g a i u", g=Z_PAIR, a=I_TILES, u=2)
-            copy = nc.vector.tensor_copy if g % 4 == 1 else nc.scalar.copy
-            copy(out=words[:, g % Z_PAIR, :, :, :], in_=zt_ps[g][:].rearrange("p a u i -> p a i u"))
+            nc.scalar.copy(out=words[:, g % Z_PAIR, :, :, :], in_=zt_ps[g][:].rearrange("p a u i -> p a i u"))
 
         def quantise_z(pair):
             passes = slice(pair * Z_PAIR, (pair + 1) * Z_PAIR)
@@ -316,7 +326,7 @@ def tile_kernelloglikelihood_k_kernel(
             cols = slice(GROUPS[q][0] * P, GROUPS[q][1] * P)
             w = late["w"]
             for it in range(I_TILES):
-                e_w = unread.tile([P, UNIT_COLS], BF16, tag="by_scalar")
+                e_w = unread.tile([P, SQUARE_COLS], BF16, tag="by_scalar")
                 nc.scalar.activation(
                     out=e_w[:, 0 : (GROUPS[q][1] - GROUPS[q][0]) * P],
                     in_=w[it][:, cols],
@@ -330,6 +340,7 @@ def tile_kernelloglikelihood_k_kernel(
         product_todo = []
         early_agenda = {}
         agenda = {}
+        halved = {}
 
         def plan(step_, function, *args):
             agenda.setdefault(step_, []).append((function, args))
@@ -337,11 +348,22 @@ def tile_kernelloglikelihood_k_kernel(
         def plan_early(step_, function, *args):
             early_agenda.setdefault(step_, []).append((function, args))
 
-        def squares_of(n):
-            k = n // CHUNK_UNITS
-            tiles = [a for a in range(UNITS[n][2]) if not by_gram(k, a)]
-            cut = (len(tiles) + 1) // 2 if n < len(UNITS) - CHUNK_UNITS else len(tiles)
-            return [(k, a) for a in (tiles[:cut] if n % CHUNK_UNITS == 0 else tiles[cut:])]
+        def pieces(group_range):
+            return [
+                (k, a, part)
+                for k in range(n_units // CHUNK_UNITS)
+                if UNITS[k * CHUNK_UNITS][0] in group_range
+                for a in range(UNITS[k * CHUNK_UNITS][2])
+                if not by_gram(k, a)
+                for part in range(max(1, chunk_cols(k)[1] // SQUARE_COLS))
+            ]
+
+        squares = {}
+        first_pieces, other_pieces = pieces([0]), pieces(range(1, len(GROUPS)))
+        for i, piece in enumerate(first_pieces):
+            squares.setdefault(i * SQUARES_BEHIND // len(first_pieces), []).append(piece)
+        for i, piece in enumerate(other_pieces):
+            squares.setdefault(SQUARES_BEHIND + i * (n_units - 2 - SQUARES_BEHIND) // len(other_pieces), []).append(piece)
 
         def step(n):
             g = n - Z_LAG
@@ -352,52 +374,49 @@ def tile_kernelloglikelihood_k_kernel(
                 entry[0](*entry[1])
             if n < n_units:
                 for b in range(2):
-                    transpose_r(n, b)
-            if n == 0:
-                transpose_x()
-                copy_x()
-                quantise_x()
+                    copy_r(n, b)
             if 1 <= g <= PASSES:
                 transpose_z(g - 1)
-            if 0 <= g + 1 < PASSES:
-                project(g + 1)
-            if n % 2 == 0 or n >= n_units:
-                count = 0
-                while product_todo and product_todo[0][0] <= n and count < 3:
-                    unit = product_todo[0][1]
-                    products(unit)
-                    product_todo.remove(product_todo[0])
-                    count += 1
-                    for q in range(len(GROUPS)):
-                        if unit == LAST[q]:
-                            if q < len(GROUPS) - 1:
-                                plan(n + 2, distances, q)
-                                plan(n + 3, exponentials, q)
-                            else:
-                                plan(n + 1, distances, q)
             if 1 <= n <= n_units and n - 1 in gram_units(UNITS[n - 1][0]):
                 gram(n - 1)
-            if n < n_units:
+            limit = len(UNITS) if n >= n_units else 1 if n < FIRST[1] + 5 else 2
+            while product_todo and product_todo[0][0] <= n and limit > 0:
+                unit = product_todo[0][1]
+                products(unit)
+                product_todo.remove(product_todo[0])
+                limit -= 1
+                for q in range(len(GROUPS)):
+                    if unit == LAST[q]:
+                        if q < len(GROUPS) - 1:
+                            plan(max(n + 2, halved[q]), distances, q)
+                            plan(max(n + 2, halved[q]) + 1, exponentials, q)
+                        else:
+                            plan(max(n + 1, halved[q]), distances, q)
+            if 0 <= g + 1 < PASSES:
+                project(g + 1)
+            if n + 1 < n_units:
                 for b in range(2):
-                    copy_r(n, b)
+                    transpose_r(n + 1, b)
             if 1 <= g <= PASSES:
                 square_z(g - 1)
                 copy_z(g - 1)
-            if n < n_units:
-                for piece in squares_of(n):
-                    square_r(piece[0], piece[1])
+            for piece in squares.get(n, []):
+                square_r(*piece)
+            if n == 0:
+                copy_x()
+                quantise_x()
             if 1 <= n < n_units:
                 quantise_r(n - 1)
             if n == n_units - 1:
-                quantise_r(n)
+                quantise_r(n, 2)
             if g >= Z_PAIR + 1 and (g - 1) % Z_PAIR == 0 and (g - 1) // Z_PAIR <= PASSES // Z_PAIR:
                 quantise_z((g - 1) // Z_PAIR - 1)
             for entry in agenda.get(n, []):
                 entry[0](*entry[1])
             if 0 <= g and g + W_BUFS < PASSES:
                 load_w(g + W_BUFS)
-            k = n // CHUNK_UNITS + R_BUFS
-            if n % CHUNK_UNITS == 1 and k * CHUNK_UNITS < n_units:
+            k = (g + W_BUFS) // 2 + 1
+            if g >= 0 and g % 2 == 0 and k * CHUNK_UNITS < n_units:
                 load_reference(k)
 
         h_bf = const.tile([P, 1], BF16)
@@ -414,13 +433,14 @@ def tile_kernelloglikelihood_k_kernel(
                 in_=pca_weight_scales[0][4 * quad : 4 * quad + 4, :].rearrange("r (n c) -> n r c", n=W_PLANES).bitcast(I32),
             )
         load_w(0)
-        load_reference(1)
+        load_reference(1, 0, 2)
         load_w(1)
-        for k in range(2, R_BUFS):
-            if 2 * k - 2 < W_BUFS:
-                load_w(2 * k - 2)
-                load_w(2 * k - 1)
+        load_reference(1, 1, 2)
+        load_w(2)
+        for k in range(2, W_BUFS // 2 + 1):
             load_reference(k)
+            for g in range(2 * k - 1, min(2 * k + 1, W_BUFS)):
+                load_w(g)
         early["x_grouped"] = const.tile([P, B * 4], BF16, align_bytes=64, name="x_grouped")
         early["x_codes"] = const.tile([P, B], U32, align_bytes=64, name="x_codes")
         early["x_scales"] = const.tile([P, B], U8, align_bytes=64, name="x_scales")
@@ -435,12 +455,8 @@ def tile_kernelloglikelihood_k_kernel(
         nc.vector.tensor_tensor(out=h_sq[:], in0=h32[:], in1=h32[:], op=ALU.mult)
         inv_h2 = const.tile([P, 1], F32)
         nc.vector.reciprocal(out=inv_h2[:], in_=h_sq[:])
-        ln_h = const.tile([P, 1], F32)
-        nc.scalar.activation(out=ln_h[:], in_=h32[:], func=ACT.Ln, scale=SQRT_2PI_HI)
-        coeff = const.tile([P, 1], F32)
-        nc.vector.tensor_scalar(
-            out=coeff[:], in0=ln_h[:], scalar1=-float(DC), scalar2=COEFF_REST, op0=ALU.mult, op1=ALU.add
-        )
+        log_in = const.tile([P, I_TILES + 1], F32)
+        nc.vector.tensor_scalar(out=log_in[:, I_TILES :], in0=h32[:], scalar1=SQRT_2PI_HI, scalar2=None, op0=ALU.mult)
         late["inv_h2"] = inv_h2
         late["z2"] = const.tile([P, I_TILES], F32, name="z2")
         late["z2_half"] = const.tile([P, I_TILES], F32, name="z2_half")
@@ -461,15 +477,20 @@ def tile_kernelloglikelihood_k_kernel(
         plan(z_end + 2, halve_z2)
         for q in range(len(GROUPS)):
             end = LAST[q] + 1 if q < len(GROUPS) - 1 else LAST[q]
-            gram_end = gram_units(q)[-1] + 2
-            plan(gram_end, diagonal, q)
-            end = max(end, gram_end)
+            end = max(end, SQUARES_BEHIND - 1)
+            if GRAM_CHUNKS[q]:
+                plan(gram_units(q)[-1] + 2, diagonal, q)
+                end = max(end, gram_units(q)[-1] + 2)
             hurry = q == len(GROUPS) - 1
             plan(end + 1 - hurry, sum_r2, q)
             plan(end + 2 - hurry, spread_r2, q)
             plan_early(end + 3 - hurry, halve_r2, q)
+            halved[q] = end + 3 - hurry
 
         with tc.manual_schedule():
+            for b in range(2):
+                transpose_r(0, b)
+            transpose_x()
             for n in range(n_units + STEPS_BEHIND):
                 step(n)
         assert not product_todo and max(agenda) < n_units + STEPS_BEHIND
@@ -488,7 +509,7 @@ def tile_kernelloglikelihood_k_kernel(
         weighted = const.tile([P, I_TILES, len(GROUPS)], F32)
         nc.vector.tensor_tensor(out=weighted[:, :, 0:last], in0=late["sums"][:, :, 0:last], in1=factor[:], op=ALU.mult)
         for it in range(I_TILES):
-            e_w = unread.tile([P, UNIT_COLS], BF16, tag="by_scalar")
+            e_w = unread.tile([P, SQUARE_COLS], BF16, tag="by_scalar")
             nc.scalar.activation(
                 out=e_w[:, 0 : (GROUPS[last][1] - GROUPS[last][0]) * P],
                 in_=late["w"][it][:, GROUPS[last][0] * P : GROUPS[last][1] * P],
@@ -497,12 +518,15 @@ def tile_kernelloglikelihood_k_kernel(
                 bias=neg_l_top[:, it : it + 1],
                 accum_out=weighted[:, it, last : last + 1],
             )
-        sum_exp = const.tile([P, I_TILES], F32)
-        nc.vector.tensor_reduce(out=sum_exp[:], in_=weighted[:], axis=AX.X, op=ALU.add)
-        ln_sum = const.tile([P, I_TILES], F32)
-        nc.scalar.activation(out=ln_sum[:], in_=sum_exp[:], func=ACT.Ln)
+        rest = const.tile([P, I_TILES], F32)
+        nc.vector.tensor_scalar(out=rest[:], in0=neg_l_top[:], scalar1=-1.0, scalar2=COEFF_REST, op0=ALU.mult, op1=ALU.add)
+        nc.vector.tensor_reduce(out=log_in[:, 0:I_TILES], in_=weighted[:], axis=AX.X, op=ALU.add)
+        logs = const.tile([P, I_TILES + 1], F32)
+        nc.scalar.activation(out=logs[:], in_=log_in[:], func=ACT.Ln)
+        coeff = const.tile([P, 1], F32)
+        nc.vector.tensor_scalar(out=coeff[:], in0=logs[:, I_TILES :], scalar1=-float(DC), scalar2=None, op0=ALU.mult)
         nc.vector.scalar_tensor_tensor(
-            out=res_pad[:, 0:I_TILES], in0=ln_sum[:], scalar=coeff[:], in1=neg_l_top[:], op0=ALU.add, op1=ALU.subtract
+            out=res_pad[:, 0:I_TILES], in0=logs[:, 0:I_TILES], scalar=coeff[:], in1=rest[:], op0=ALU.add, op1=ALU.add
         )
         res_ps = work.tile([P, P], F32, tag="work")
         nc.tensor.transpose(res_ps[:], res_pad[:], ident[:])

@@ -23,16 +23,19 @@ J_TILES = NREF // P
 PASSES = DC // K_PASS
 GROUPS = ((0, 4), (4, 6), (6, 7), (7, 8))
 UNIT_COLS = 4 * BANK
-CHUNK_UNITS = 2
+CHUNK_UNITS = 4
+LOAD_UNITS = 2
+LOAD_AHEAD = 6
+PAIR = 2
 W_PLANES = 4
-R_BUFS = 6
+R_BUFS = 3
 W_BUFS = 6
-Q_BUFS = 12
+Q_BUFS = 6
 Z_LAG = 2
 Z_PAIR = 2
 SQUARES_BEHIND = 19
 SQUARE_COLS = 2048
-GRAM_CHUNKS = (8, 3, 0, 1)
+GRAM_UNITS = (range(0, 16), range(18, 24), range(0), range(28, 30))
 STEPS_BEHIND = 4
 
 FLOPS = 2 * B * D * DC + 2 * B * DC * NREF
@@ -56,12 +59,13 @@ def tile_kernelloglikelihood_k_kernel(
     with ExitStack() as stack:
         const = stack.enter_context(tc.tile_pool(name="const", bufs=1))
         r_rows = stack.enter_context(tc.tile_pool(name="r_rows", bufs=R_BUFS))
-        r_stage = stack.enter_context(tc.tile_pool(name="r_stage", bufs=5))
+        r_stage = stack.enter_context(tc.tile_pool(name="r_stage", bufs=3))
         r_quant = stack.enter_context(tc.tile_pool(name="r_quant", bufs=Q_BUFS))
         w_pool = stack.enter_context(tc.tile_pool(name="w_pool", bufs=W_BUFS))
-        z_stage = stack.enter_context(tc.tile_pool(name="z_stage", bufs=4))
+        b_pool = stack.enter_context(tc.tile_pool(name="b_pool", bufs=4))
+        z_stage = stack.enter_context(tc.tile_pool(name="z_stage", bufs=8))
         z_group = stack.enter_context(tc.tile_pool(name="z_group", bufs=2))
-        unread = stack.enter_context(tc.tile_pool(name="unread", bufs=2))
+        unread = stack.enter_context(tc.tile_pool(name="unread", bufs=4))
         work = stack.enter_context(tc.psum_pool(name="work", bufs=3))
         acc = stack.enter_context(tc.psum_pool(name="acc", bufs=1))
 
@@ -69,7 +73,7 @@ def tile_kernelloglikelihood_k_kernel(
         z_codes = const.tile([P, PASSES, B], U32, align_bytes=64)
         z_scales = const.tile([P, PASSES, B], U8, align_bytes=64)
         z2_parts = const.tile([P, I_TILES, PASSES], F32)
-        r2_parts = const.tile([P, J_TILES, 8], F32)
+        r2_parts = const.tile([P, J_TILES, 1 + 2 * DC // SQUARE_COLS], F32)
 
         r_sb = {}
         rt_ps = {}
@@ -83,36 +87,36 @@ def tile_kernelloglikelihood_k_kernel(
             q, t0, nt, g0, np_ = UNITS[k * CHUNK_UNITS]
             return g0 * K_PASS, CHUNK_UNITS * np_ * K_PASS
 
-        def load_reference(k, part=0, parts=1):
+        def load_reference(n, count):
+            k = n // CHUNK_UNITS
             q, t0, nt, g0, np_ = UNITS[k * CHUNK_UNITS]
             c0, width = chunk_cols(k)
-            if part == 0:
+            if n % CHUNK_UNITS == 0:
                 r_sb[k] = r_rows.tile([P, nt, width], BF16, name="r_sb")
-            lo, hi = part * width // parts, (part + 1) * width // parts
+            lo = (n % CHUNK_UNITS) * np_ * K_PASS
+            hi = lo + count * np_ * K_PASS
             nc.sync.dma_start(
                 out=r_sb[k][:, :, lo:hi],
                 in_=X_ref[t0 * P : (t0 + nt) * P, c0 + lo : c0 + hi].rearrange("(t p) c -> p t c", p=P),
             )
 
-        def chunk_index(k):
-            return k - FIRST[UNITS[k * CHUNK_UNITS][0]] // CHUNK_UNITS
+        def pieces(groups):
+            result = []
+            for k in range(len(UNITS) // CHUNK_UNITS):
+                q, t0, nt, g0, np_ = UNITS[k * CHUNK_UNITS]
+                width = SQUARE_COLS if q > 0 else SQUARE_COLS // 2
+                for part in range(chunk_cols(k)[1] // width):
+                    for a in range(nt):
+                        if q in groups and (a > 0 or k * CHUNK_UNITS + part * width // (np_ * K_PASS) not in GRAM_UNITS[q]):
+                            result.append((k, a, part * width, (part + 1) * width))
+            return result
 
-        def gram_units(q):
-            first = FIRST[q] + (CHUNK_UNITS if q == 1 else 0)
-            return range(first, first + GRAM_CHUNKS[q] * CHUNK_UNITS)
-
-        def by_gram(k, a):
-            return a == 0 and k * CHUNK_UNITS in gram_units(UNITS[k * CHUNK_UNITS][0])
-
-        def square_r(k, a, part):
-            t0 = UNITS[k * CHUNK_UNITS][1]
-            c0, width = chunk_cols(k)
-            parts = max(1, width // SQUARE_COLS)
-            entry = chunk_index(k) * parts + part
-            cols = slice(part * width // parts, (part + 1) * width // parts)
-            r_sq = unread.tile([P, SQUARE_COLS], BF16, tag="by_scalar")
+        def square_r(k, a, lo, hi):
+            q, t0, nt, g0, np_ = UNITS[k * CHUNK_UNITS]
+            entry = 2 * (g0 * K_PASS + lo) // SQUARE_COLS
+            r_sq = unread.tile([P, SQUARE_COLS], BF16, name="r_sq")
             nc.scalar.activation(
-                out=r_sq[:, 0 : width // parts], in_=r_sb[k][:, a, cols], func=ACT.Square,
+                out=r_sq[:, 0 : hi - lo], in_=r_sb[k][:, a, lo:hi], func=ACT.Square,
                 accum_out=r2_parts[:, t0 + a, entry : entry + 1],
             )
 
@@ -128,27 +132,25 @@ def tile_kernelloglikelihood_k_kernel(
                     nc.tensor.transpose(rt_ps[(n, b)][:, a, u, :], words[:, w0 : w0 + P], ident[:])
 
         def copy_r(n, b):
-            if b == 0:
-                r_grouped[n] = r_stage.tile([P, UNIT_COLS], BF16, align_bytes=64, name="r_grouped")
-            words = r_grouped[n][:].bitcast(F32).rearrange("p (b a j u) -> p b a j u", b=2, a=2, u=2)
+            if n % PAIR == 0 and b == 0:
+                r_grouped[n // PAIR] = r_stage.tile([P, PAIR * UNIT_COLS], BF16, align_bytes=64, name="r_grouped")
+            words = r_grouped[n // PAIR][:].bitcast(F32).rearrange("p (b a j u) -> p b a j u", b=2 * PAIR, a=2, u=2)
             copy = nc.scalar.copy if n == len(UNITS) - 1 and b == 1 else nc.vector.tensor_copy
-            copy(out=words[:, b, :, :, :], in_=rt_ps[(n, b)][:].rearrange("p a u j -> p a j u"))
+            copy(out=words[:, 2 * (n % PAIR) + b, :, :, :], in_=rt_ps[(n, b)][:].rearrange("p a u j -> p a j u"))
 
-        def quantise_r(n, parts=1):
-            r_codes[n] = r_quant.tile([P, BANK], U32, align_bytes=64, name="r_codes")
-            r_scales[n] = r_quant.tile([P, BANK], U8, align_bytes=64, name="r_scales")
-            for part in range(parts):
-                cols = slice(part * BANK // parts, (part + 1) * BANK // parts)
-                nc.vector.quantize_mx(
-                    out=r_codes[n][:, cols].bitcast(FP8X4),
-                    scales=r_scales[n][:, cols],
-                    in_=r_grouped[n][:, 4 * cols.start : 4 * cols.stop],
-                )
+        def quantise_r(m, lo=0, hi=PAIR * BANK):
+            if lo == 0:
+                r_codes[m] = r_quant.tile([P, PAIR * BANK], U32, align_bytes=64, name="r_codes")
+                r_scales[m] = r_quant.tile([P, PAIR * BANK], U8, align_bytes=64, name="r_scales")
+            nc.vector.quantize_mx(
+                out=r_codes[m][:, lo:hi].bitcast(FP8X4), scales=r_scales[m][:, lo:hi], in_=r_grouped[m][:, 4 * lo : 4 * hi]
+            )
 
         def products(n):
             q, t0, nt, g0, np_ = UNITS[n]
             for b in range(np_):
-                cols = slice(b * nt * P, (b + 1) * nt * P)
+                first = (n % PAIR) * BANK + b * nt * P
+                cols = slice(first, first + nt * P)
                 for it in range(I_TILES):
                     if (it, q) not in cross:
                         cross[(it, q)] = acc.tile([P, BANK], F32, tag="acc_%d" % (it + I_TILES * (q % 2)), name="cross")
@@ -156,8 +158,8 @@ def tile_kernelloglikelihood_k_kernel(
                         out=cross[(it, q)][:, 0 : nt * P],
                         lhsT=z_codes[:, g0 + b, it * P : (it + 1) * P].bitcast(FP8X4),
                         lhsT_scale=z_scales[:, g0 + b, it * P : (it + 1) * P],
-                        rhs=r_codes[n][:, cols].bitcast(FP8X4),
-                        rhs_scale=r_scales[n][:, cols],
+                        rhs=r_codes[n // PAIR][:, cols].bitcast(FP8X4),
+                        rhs_scale=r_scales[n // PAIR][:, cols],
                         start=(g0 + b == 0),
                         stop=(g0 + b == PASSES - 1),
                     )
@@ -166,23 +168,24 @@ def tile_kernelloglikelihood_k_kernel(
             q, t0, nt, g0, np_ = UNITS[n]
             if q not in gram_ps:
                 gram_ps[q] = acc.tile([P, P], F32, tag="gram", name="gram_ps")
-            columns = r_grouped[n][:].rearrange("p (j t) -> p j t", t=4)
+            columns = r_grouped[n // PAIR][:].rearrange("p (j t) -> p j t", t=4)
             for b in range(np_):
                 for t in range(4):
-                    plane = columns[:, b * nt * P : b * nt * P + P, t]
+                    first = (n % PAIR) * BANK + b * nt * P
+                    plane = columns[:, first : first + P, t]
                     nc.tensor.matmul(
                         out=gram_ps[q][:],
                         lhsT=plane,
                         rhs=plane,
-                        start=(n == gram_units(q)[0] and b == 0 and t == 0),
-                        stop=(n == gram_units(q)[-1] and b == np_ - 1 and t == 3),
+                        start=(n == GRAM_UNITS[q][0] and b == 0 and t == 0),
+                        stop=(n == GRAM_UNITS[q][-1] and b == np_ - 1 and t == 3),
                     )
 
         def diagonal(q):
             off_diagonal = unread.tile([P, P], F32, tag="by_vector")
             nc.vector.scalar_tensor_tensor(
                 out=off_diagonal[:], in0=gram_ps[q][:], scalar=1.0, in1=ident[:], op0=ALU.mult, op1=ALU.mult,
-                accum_out=r2_parts[:, GROUPS[q][0], 7:8],
+                accum_out=r2_parts[:, GROUPS[q][0], 2 * DC // SQUARE_COLS :],
             )
 
         early = {}
@@ -198,8 +201,11 @@ def tile_kernelloglikelihood_k_kernel(
             w_words[g] = w_pool.tile([P, K_PASS], U32, align_bytes=64, name="w_words")
             w_bytes = pca_weight_words[0].rearrange("p n t -> p (n t)")
             nc.sync.dma_start(out=w_words[g][:].bitcast(I32), in_=w_bytes[:, 4 * g * K_PASS : 4 * (g + 1) * K_PASS].bitcast(I32))
-            bias[g] = w_pool.tile([P, K_PASS], BF16, name="bias")
-            nc.sync.dma_start(out=bias[g][:], in_=pca_bias[g * K_PASS : (g + 1) * K_PASS].partition_broadcast(P))
+            if g % Z_PAIR == 0:
+                bias[g // Z_PAIR] = b_pool.tile([P, Z_PAIR * K_PASS], BF16, name="bias")
+                nc.sync.dma_start(
+                    out=bias[g // Z_PAIR][:], in_=pca_bias[g * K_PASS : (g + Z_PAIR) * K_PASS].partition_broadcast(P)
+                )
 
         def transpose_x():
             x_words = early["x_sb"][:].bitcast(F32)
@@ -232,9 +238,10 @@ def tile_kernelloglikelihood_k_kernel(
                 )
 
         def add_bias(g):
+            bias_cols = bias[g // Z_PAIR][:, (g % Z_PAIR) * K_PASS : (g % Z_PAIR + 1) * K_PASS]
             for it in range(I_TILES):
                 z_f32[(g, it)] = z_stage.tile([P, K_PASS], F32, name="z_f32")
-                nc.vector.tensor_tensor(out=z_f32[(g, it)][:], in0=y_ps[(g, it)][:], in1=bias[g][:], op=ALU.add)
+                nc.vector.tensor_tensor(out=z_f32[(g, it)][:], in0=y_ps[(g, it)][:], in1=bias_cols, op=ALU.add)
 
         def round_z(g):
             for it in range(I_TILES):
@@ -245,9 +252,9 @@ def tile_kernelloglikelihood_k_kernel(
 
         def square_z(g):
             for it in range(I_TILES):
-                z_sq = unread.tile([P, SQUARE_COLS], BF16, tag="by_scalar")
+                z_sq = unread.tile([P, BANK], BF16, bufs=10, tag="z_sq")
                 nc.scalar.activation(
-                    out=z_sq[:, 0:K_PASS], in_=z_f32[(g, it)][:], func=ACT.Square, accum_out=z2_parts[:, it, g : g + 1]
+                    out=z_sq[:], in_=z_f32[(g, it)][:], func=ACT.Square, accum_out=z2_parts[:, it, g : g + 1]
                 )
 
         def transpose_z(g):
@@ -326,7 +333,7 @@ def tile_kernelloglikelihood_k_kernel(
             cols = slice(GROUPS[q][0] * P, GROUPS[q][1] * P)
             w = late["w"]
             for it in range(I_TILES):
-                e_w = unread.tile([P, SQUARE_COLS], BF16, tag="by_scalar")
+                e_w = unread.tile([P, BANK], BF16, bufs=10, tag="z_sq")
                 nc.scalar.activation(
                     out=e_w[:, 0 : (GROUPS[q][1] - GROUPS[q][0]) * P],
                     in_=w[it][:, cols],
@@ -348,16 +355,6 @@ def tile_kernelloglikelihood_k_kernel(
         def plan_early(step_, function, *args):
             early_agenda.setdefault(step_, []).append((function, args))
 
-        def pieces(group_range):
-            return [
-                (k, a, part)
-                for k in range(n_units // CHUNK_UNITS)
-                if UNITS[k * CHUNK_UNITS][0] in group_range
-                for a in range(UNITS[k * CHUNK_UNITS][2])
-                if not by_gram(k, a)
-                for part in range(max(1, chunk_cols(k)[1] // SQUARE_COLS))
-            ]
-
         squares = {}
         first_pieces, other_pieces = pieces([0]), pieces(range(1, len(GROUPS)))
         for i, piece in enumerate(first_pieces):
@@ -377,9 +374,9 @@ def tile_kernelloglikelihood_k_kernel(
                     copy_r(n, b)
             if 1 <= g <= PASSES:
                 transpose_z(g - 1)
-            if 1 <= n <= n_units and n - 1 in gram_units(UNITS[n - 1][0]):
+            if 1 <= n <= n_units and n - 1 in GRAM_UNITS[UNITS[n - 1][0]]:
                 gram(n - 1)
-            limit = len(UNITS) if n >= n_units else 1 if n < FIRST[1] + 5 else 2
+            limit = len(UNITS) if n >= n_units else 1 if n < FIRST[1] + 5 or n % 2 == 1 else 3
             while product_todo and product_todo[0][0] <= n and limit > 0:
                 unit = product_todo[0][1]
                 products(unit)
@@ -405,26 +402,27 @@ def tile_kernelloglikelihood_k_kernel(
             if n == 0:
                 copy_x()
                 quantise_x()
-            if 1 <= n < n_units:
-                quantise_r(n - 1)
+            if n % PAIR == 0 and PAIR <= n < n_units:
+                quantise_r(n // PAIR - 1)
             if n == n_units - 1:
-                quantise_r(n, 2)
+                for lo, hi in ((0, BANK), (BANK, BANK + BANK // 2), (BANK + BANK // 2, 2 * BANK)):
+                    quantise_r(n // PAIR, lo, hi)
             if g >= Z_PAIR + 1 and (g - 1) % Z_PAIR == 0 and (g - 1) // Z_PAIR <= PASSES // Z_PAIR:
                 quantise_z((g - 1) // Z_PAIR - 1)
             for entry in agenda.get(n, []):
                 entry[0](*entry[1])
             if 0 <= g and g + W_BUFS < PASSES:
                 load_w(g + W_BUFS)
-            k = (g + W_BUFS) // 2 + 1
-            if g >= 0 and g % 2 == 0 and k * CHUNK_UNITS < n_units:
-                load_reference(k)
+            ahead = n + LOAD_AHEAD
+            if g >= 0 and g % LOAD_UNITS == 0 and ahead < n_units:
+                load_reference(ahead, LOAD_UNITS)
 
         h_bf = const.tile([P, 1], BF16)
         nc.sync.dma_start(out=h_bf[:], in_=bandwidth.partition_broadcast(P))
-        load_reference(0, 0, 2)
+        load_reference(0, 1)
         early["x_sb"] = const.tile([P, I_TILES, D], BF16, name="x_sb")
         nc.sync.dma_start(out=early["x_sb"][:], in_=x.rearrange("(t p) k -> p t k", p=P))
-        load_reference(0, 1, 2)
+        load_reference(1, 1)
         early["w_planes"] = const.tile([P, DC // W_PLANES], U8, align_bytes=64, name="w_planes")
         nc.vector.memset(early["w_planes"][:].bitcast(I32), 0)
         for quad in range(4):
@@ -433,13 +431,13 @@ def tile_kernelloglikelihood_k_kernel(
                 in_=pca_weight_scales[0][4 * quad : 4 * quad + 4, :].rearrange("r (n c) -> n r c", n=W_PLANES).bitcast(I32),
             )
         load_w(0)
-        load_reference(1, 0, 2)
+        load_reference(2, 1)
         load_w(1)
-        load_reference(1, 1, 2)
+        load_reference(3, 1)
         load_w(2)
-        for k in range(2, W_BUFS // 2 + 1):
-            load_reference(k)
-            for g in range(2 * k - 1, min(2 * k + 1, W_BUFS)):
+        for n in range(4, W_BUFS + 2, LOAD_UNITS):
+            load_reference(n, LOAD_UNITS)
+            for g in range(n - 1, min(n + 1, W_BUFS)):
                 load_w(g)
         early["x_grouped"] = const.tile([P, B * 4], BF16, align_bytes=64, name="x_grouped")
         early["x_codes"] = const.tile([P, B], U32, align_bytes=64, name="x_codes")
@@ -468,7 +466,7 @@ def tile_kernelloglikelihood_k_kernel(
         late["sums"] = const.tile([P, I_TILES, len(GROUPS)], F32, name="sums")
 
         for n, unit in enumerate(UNITS):
-            ready = n + 2 if n < n_units - 1 else n + 1
+            ready = (n // PAIR + 1) * PAIR + 1 if n < n_units - PAIR else n_units
             if unit[0] == 0:
                 ready = max(ready, (unit[3] // Z_PAIR * Z_PAIR + Z_PAIR - 1) + Z_LAG + 3)
             product_todo.append((ready, n))
@@ -478,9 +476,9 @@ def tile_kernelloglikelihood_k_kernel(
         for q in range(len(GROUPS)):
             end = LAST[q] + 1 if q < len(GROUPS) - 1 else LAST[q]
             end = max(end, SQUARES_BEHIND - 1)
-            if GRAM_CHUNKS[q]:
-                plan(gram_units(q)[-1] + 2, diagonal, q)
-                end = max(end, gram_units(q)[-1] + 2)
+            if len(GRAM_UNITS[q]):
+                plan(GRAM_UNITS[q][-1] + 2, diagonal, q)
+                end = max(end, GRAM_UNITS[q][-1] + 2)
             hurry = q == len(GROUPS) - 1
             plan(end + 1 - hurry, sum_r2, q)
             plan(end + 2 - hurry, spread_r2, q)
@@ -509,7 +507,7 @@ def tile_kernelloglikelihood_k_kernel(
         weighted = const.tile([P, I_TILES, len(GROUPS)], F32)
         nc.vector.tensor_tensor(out=weighted[:, :, 0:last], in0=late["sums"][:, :, 0:last], in1=factor[:], op=ALU.mult)
         for it in range(I_TILES):
-            e_w = unread.tile([P, SQUARE_COLS], BF16, tag="by_scalar")
+            e_w = unread.tile([P, BANK], BF16, bufs=10, tag="z_sq")
             nc.scalar.activation(
                 out=e_w[:, 0 : (GROUPS[last][1] - GROUPS[last][0]) * P],
                 in_=late["w"][it][:, GROUPS[last][0] * P : GROUPS[last][1] * P],

@@ -23,16 +23,15 @@ J_TILES = NREF // P
 PASSES = DC // K_PASS
 GROUPS = ((0, 4), (4, 6), (6, 7), (7, 8))
 UNIT_COLS = 4 * BANK
-CHUNK_UNITS = 4
-LOAD_UNITS = 2
 LOAD_AHEAD = 6
 PAIR = 2
 W_PLANES = 4
-R_BUFS = 3
+R_BUFS = 6
 W_BUFS = 6
 Q_BUFS = 6
 Z_LAG = 2
 Z_PAIR = 2
+EARLY_UNITS = 3
 SQUARES_BEHIND = 19
 SQUARE_COLS = 2048
 GRAM_UNITS = (range(0, 16), range(18, 24), range(0), range(28, 30))
@@ -45,6 +44,7 @@ UNITS = [
     for q, (t0, t1) in enumerate(GROUPS)
     for g in range(0, PASSES, 4 // (t1 - t0))
 ]
+LOADS = [0, 1, 2, 3] + list(range(4, len(UNITS), 2))
 LAST = [max(n for n, unit in enumerate(UNITS) if unit[0] == q) for q in range(len(GROUPS))]
 FIRST = [min(n for n, unit in enumerate(UNITS) if unit[0] == q) for q in range(len(GROUPS))]
 
@@ -73,7 +73,7 @@ def tile_kernelloglikelihood_k_kernel(
         z_codes = const.tile([P, PASSES, B], U32, align_bytes=64)
         z_scales = const.tile([P, PASSES, B], U8, align_bytes=64)
         z2_parts = const.tile([P, I_TILES, PASSES], F32)
-        r2_parts = const.tile([P, J_TILES, 1 + 2 * DC // SQUARE_COLS], F32)
+        r2_parts = const.tile([P, J_TILES, 1 + PASSES], F32)
 
         r_sb = {}
         rt_ps = {}
@@ -83,37 +83,35 @@ def tile_kernelloglikelihood_k_kernel(
         cross = {}
         gram_ps = {}
 
-        def chunk_cols(k):
-            q, t0, nt, g0, np_ = UNITS[k * CHUNK_UNITS]
-            return g0 * K_PASS, CHUNK_UNITS * np_ * K_PASS
+        def load_of(n):
+            return max(k for k in range(len(LOADS)) if LOADS[k] <= n)
 
-        def load_reference(n, count):
-            k = n // CHUNK_UNITS
-            q, t0, nt, g0, np_ = UNITS[k * CHUNK_UNITS]
-            c0, width = chunk_cols(k)
-            if n % CHUNK_UNITS == 0:
-                r_sb[k] = r_rows.tile([P, nt, width], BF16, name="r_sb")
-            lo = (n % CHUNK_UNITS) * np_ * K_PASS
-            hi = lo + count * np_ * K_PASS
+        def load_cols(k):
+            units = (LOADS + [len(UNITS)])[k + 1] - LOADS[k]
+            return UNITS[LOADS[k]][3] * K_PASS, units * UNITS[LOADS[k]][4] * K_PASS
+
+        def load_reference(k):
+            q, t0, nt, g0, np_ = UNITS[LOADS[k]]
+            c0, width = load_cols(k)
+            r_sb[k] = r_rows.tile([P, nt, width], BF16, name="r_sb")
             nc.sync.dma_start(
-                out=r_sb[k][:, :, lo:hi],
-                in_=X_ref[t0 * P : (t0 + nt) * P, c0 + lo : c0 + hi].rearrange("(t p) c -> p t c", p=P),
+                out=r_sb[k][:], in_=X_ref[t0 * P : (t0 + nt) * P, c0 : c0 + width].rearrange("(t p) c -> p t c", p=P)
             )
 
         def pieces(groups):
             result = []
-            for k in range(len(UNITS) // CHUNK_UNITS):
-                q, t0, nt, g0, np_ = UNITS[k * CHUNK_UNITS]
-                width = SQUARE_COLS if q > 0 else SQUARE_COLS // 2
-                for part in range(chunk_cols(k)[1] // width):
+            for k, n in enumerate(LOADS):
+                q, t0, nt, g0, np_ = UNITS[n]
+                width = min(SQUARE_COLS, load_cols(k)[1])
+                for part in range(load_cols(k)[1] // width):
                     for a in range(nt):
-                        if q in groups and (a > 0 or k * CHUNK_UNITS + part * width // (np_ * K_PASS) not in GRAM_UNITS[q]):
+                        if q in groups and (a > 0 or n + part * width // (np_ * K_PASS) not in GRAM_UNITS[q]):
                             result.append((k, a, part * width, (part + 1) * width))
             return result
 
         def square_r(k, a, lo, hi):
-            q, t0, nt, g0, np_ = UNITS[k * CHUNK_UNITS]
-            entry = 2 * (g0 * K_PASS + lo) // SQUARE_COLS
+            q, t0, nt, g0, np_ = UNITS[LOADS[k]]
+            entry = (g0 * K_PASS + lo) // K_PASS
             r_sq = unread.tile([P, SQUARE_COLS], BF16, name="r_sq")
             nc.scalar.activation(
                 out=r_sq[:, 0 : hi - lo], in_=r_sb[k][:, a, lo:hi], func=ACT.Square,
@@ -122,13 +120,13 @@ def tile_kernelloglikelihood_k_kernel(
 
         def transpose_r(n, b):
             q, t0, nt, g0, np_ = UNITS[n]
-            k = n // CHUNK_UNITS
+            k = load_of(n)
             rt_ps[(n, b)] = work.tile([P, 2, 2, P], F32, tag="work", name="rt_ps")
             for a in range(2):
                 g = g0 + (2 * b + a) // nt
                 words = r_sb[k][:, (2 * b + a) % nt, :].bitcast(F32)
                 for u in range(2):
-                    w0 = (g * K_PASS - chunk_cols(k)[0]) // 2 + u * P
+                    w0 = (g * K_PASS - load_cols(k)[0]) // 2 + u * P
                     nc.tensor.transpose(rt_ps[(n, b)][:, a, u, :], words[:, w0 : w0 + P], ident[:])
 
         def copy_r(n, b):
@@ -185,7 +183,7 @@ def tile_kernelloglikelihood_k_kernel(
             off_diagonal = unread.tile([P, P], F32, tag="by_vector")
             nc.vector.scalar_tensor_tensor(
                 out=off_diagonal[:], in0=gram_ps[q][:], scalar=1.0, in1=ident[:], op0=ALU.mult, op1=ALU.mult,
-                accum_out=r2_parts[:, GROUPS[q][0], 2 * DC // SQUARE_COLS :],
+                accum_out=r2_parts[:, GROUPS[q][0], PASSES:],
             )
 
         early = {}
@@ -357,8 +355,12 @@ def tile_kernelloglikelihood_k_kernel(
 
         squares = {}
         first_pieces, other_pieces = pieces([0]), pieces(range(1, len(GROUPS)))
-        for i, piece in enumerate(first_pieces):
-            squares.setdefault(i * SQUARES_BEHIND // len(first_pieces), []).append(piece)
+        early_count = EARLY_UNITS * (UNITS[0][2] - 1)
+        for i, piece in enumerate(first_pieces[:early_count]):
+            squares.setdefault(i // (UNITS[0][2] - 1), []).append(piece)
+        for i, piece in enumerate(first_pieces[early_count:]):
+            spread = (SQUARES_BEHIND - EARLY_UNITS) / len(first_pieces[early_count:])
+            squares.setdefault(max(EARLY_UNITS + int(i * spread), LOADS[piece[0]]), []).append(piece)
         for i, piece in enumerate(other_pieces):
             squares.setdefault(SQUARES_BEHIND + i * (n_units - 2 - SQUARES_BEHIND) // len(other_pieces), []).append(piece)
 
@@ -413,16 +415,15 @@ def tile_kernelloglikelihood_k_kernel(
                 entry[0](*entry[1])
             if 0 <= g and g + W_BUFS < PASSES:
                 load_w(g + W_BUFS)
-            ahead = n + LOAD_AHEAD
-            if g >= 0 and g % LOAD_UNITS == 0 and ahead < n_units:
-                load_reference(ahead, LOAD_UNITS)
+            if g >= 0 and n + LOAD_AHEAD in LOADS:
+                load_reference(load_of(n + LOAD_AHEAD))
 
         h_bf = const.tile([P, 1], BF16)
         nc.sync.dma_start(out=h_bf[:], in_=bandwidth.partition_broadcast(P))
-        load_reference(0, 1)
+        load_reference(0)
         early["x_sb"] = const.tile([P, I_TILES, D], BF16, name="x_sb")
         nc.sync.dma_start(out=early["x_sb"][:], in_=x.rearrange("(t p) k -> p t k", p=P))
-        load_reference(1, 1)
+        load_reference(1)
         early["w_planes"] = const.tile([P, DC // W_PLANES], U8, align_bytes=64, name="w_planes")
         nc.vector.memset(early["w_planes"][:].bitcast(I32), 0)
         for quad in range(4):
@@ -431,21 +432,21 @@ def tile_kernelloglikelihood_k_kernel(
                 in_=pca_weight_scales[0][4 * quad : 4 * quad + 4, :].rearrange("r (n c) -> n r c", n=W_PLANES).bitcast(I32),
             )
         load_w(0)
-        load_reference(2, 1)
+        load_reference(2)
         load_w(1)
-        load_reference(3, 1)
+        load_reference(3)
         load_w(2)
-        for n in range(4, W_BUFS + 2, LOAD_UNITS):
-            load_reference(n, LOAD_UNITS)
-            for g in range(n - 1, min(n + 1, W_BUFS)):
+        for k in range(4, 6):
+            load_reference(k)
+            for g in range(LOADS[k] - 1, min(LOADS[k] + 1, W_BUFS)):
                 load_w(g)
         early["x_grouped"] = const.tile([P, B * 4], BF16, align_bytes=64, name="x_grouped")
         early["x_codes"] = const.tile([P, B], U32, align_bytes=64, name="x_codes")
         early["x_scales"] = const.tile([P, B], U8, align_bytes=64, name="x_scales")
 
         make_identity(nc, ident[:])
-        res_pad = const.tile([P, P], F32)
-        nc.vector.memset(res_pad[:], 0.0)
+        pads = const.tile([P, 2, P], F32)
+        nc.vector.memset(pads[:], 0.0)
         nc.vector.memset(r2_parts[:], 0.0)
         h32 = const.tile([P, 1], F32)
         nc.vector.tensor_copy(out=h32[:], in_=h_bf[:])
@@ -453,8 +454,6 @@ def tile_kernelloglikelihood_k_kernel(
         nc.vector.tensor_tensor(out=h_sq[:], in0=h32[:], in1=h32[:], op=ALU.mult)
         inv_h2 = const.tile([P, 1], F32)
         nc.vector.reciprocal(out=inv_h2[:], in_=h_sq[:])
-        log_in = const.tile([P, I_TILES + 1], F32)
-        nc.vector.tensor_scalar(out=log_in[:, I_TILES :], in0=h32[:], scalar1=SQRT_2PI_HI, scalar2=None, op0=ALU.mult)
         late["inv_h2"] = inv_h2
         late["z2"] = const.tile([P, I_TILES], F32, name="z2")
         late["z2_half"] = const.tile([P, I_TILES], F32, name="z2_half")
@@ -491,43 +490,46 @@ def tile_kernelloglikelihood_k_kernel(
             transpose_x()
             for n in range(n_units + STEPS_BEHIND):
                 step(n)
-        assert not product_todo and max(agenda) < n_units + STEPS_BEHIND
+            assert not product_todo and max(agenda) < n_units + STEPS_BEHIND
 
-        last = len(GROUPS) - 1
-        top = const.tile([P, I_TILES], F32)
-        nc.vector.tensor_reduce(out=top[:], in_=late["w_max"][:], axis=AX.X, op=ALU.max)
-        neg_l_top = const.tile([P, I_TILES], F32)
-        nc.vector.tensor_scalar(out=neg_l_top[:], in0=top[:], scalar1=inv_h2[:], scalar2=-1.0, op0=ALU.mult, op1=ALU.mult)
-        factor = const.tile([P, I_TILES, last], F32)
-        for it in range(I_TILES):
-            nc.scalar.activation(
-                out=factor[:, it, :], in_=late["w_max"][:, it, 0:last], func=ACT.Exp, scale=inv_h2[:],
-                bias=neg_l_top[:, it : it + 1],
+            last = len(GROUPS) - 1
+            top = const.tile([P, I_TILES], F32)
+            nc.vector.tensor_reduce(out=top[:], in_=late["w_max"][:], axis=AX.X, op=ALU.max)
+            neg_l_top = pads[:, 1, 0:I_TILES]
+            nc.vector.tensor_scalar(out=neg_l_top, in0=top[:], scalar1=inv_h2[:], scalar2=-1.0, op0=ALU.mult, op1=ALU.mult)
+            factor = const.tile([P, I_TILES, last], F32)
+            for it in range(I_TILES):
+                nc.scalar.activation(
+                    out=factor[:, it, :], in_=late["w_max"][:, it, 0:last], func=ACT.Exp, scale=inv_h2[:],
+                    bias=pads[:, 1, it : it + 1],
+                )
+            weighted = const.tile([P, I_TILES, len(GROUPS)], F32)
+            nc.vector.tensor_tensor(out=weighted[:, :, 0:last], in0=late["sums"][:, :, 0:last], in1=factor[:], op=ALU.mult)
+            for it in range(I_TILES):
+                e_w = unread.tile([P, BANK], BF16, bufs=10, tag="z_sq")
+                nc.scalar.activation(
+                    out=e_w[:, 0 : (GROUPS[last][1] - GROUPS[last][0]) * P],
+                    in_=late["w"][it][:, GROUPS[last][0] * P : GROUPS[last][1] * P],
+                    func=ACT.Exp,
+                    scale=inv_h2[:],
+                    bias=pads[:, 1, it : it + 1],
+                    accum_out=weighted[:, it, last : last + 1],
+                )
+            ln_h = const.tile([P, 1], F32)
+            nc.scalar.activation(out=ln_h[:], in_=h32[:], func=ACT.Ln, scale=SQRT_2PI_HI)
+            coeff = const.tile([P, 1], F32)
+            nc.vector.tensor_reduce(out=pads[:, 0, 0:I_TILES], in_=weighted[:], axis=AX.X, op=ALU.add)
+            nc.vector.tensor_scalar(
+                out=coeff[:], in0=ln_h[:], scalar1=-float(DC), scalar2=COEFF_REST, op0=ALU.mult, op1=ALU.add
             )
-        weighted = const.tile([P, I_TILES, len(GROUPS)], F32)
-        nc.vector.tensor_tensor(out=weighted[:, :, 0:last], in0=late["sums"][:, :, 0:last], in1=factor[:], op=ALU.mult)
-        for it in range(I_TILES):
-            e_w = unread.tile([P, BANK], BF16, bufs=10, tag="z_sq")
-            nc.scalar.activation(
-                out=e_w[:, 0 : (GROUPS[last][1] - GROUPS[last][0]) * P],
-                in_=late["w"][it][:, GROUPS[last][0] * P : GROUPS[last][1] * P],
-                func=ACT.Exp,
-                scale=inv_h2[:],
-                bias=neg_l_top[:, it : it + 1],
-                accum_out=weighted[:, it, last : last + 1],
+            rows_ps = work.tile([P, 2, P], F32, tag="work")
+            for i in (1, 0):
+                nc.tensor.transpose(rows_ps[:, i, :], pads[:, i, :], ident[:])
+            ln_sum = const.tile([P, P], F32)
+            nc.scalar.activation(out=ln_sum[0:I_TILES, :], in_=rows_ps[0:I_TILES, 0, :], func=ACT.Ln)
+            res_rows = const.tile([P, P], F32)
+            nc.vector.scalar_tensor_tensor(
+                out=res_rows[0:I_TILES, :], in0=ln_sum[0:I_TILES, :], scalar=coeff[0:I_TILES, :],
+                in1=rows_ps[0:I_TILES, 1, :], op0=ALU.add, op1=ALU.subtract,
             )
-        rest = const.tile([P, I_TILES], F32)
-        nc.vector.tensor_scalar(out=rest[:], in0=neg_l_top[:], scalar1=-1.0, scalar2=COEFF_REST, op0=ALU.mult, op1=ALU.add)
-        nc.vector.tensor_reduce(out=log_in[:, 0:I_TILES], in_=weighted[:], axis=AX.X, op=ALU.add)
-        logs = const.tile([P, I_TILES + 1], F32)
-        nc.scalar.activation(out=logs[:], in_=log_in[:], func=ACT.Ln)
-        coeff = const.tile([P, 1], F32)
-        nc.vector.tensor_scalar(out=coeff[:], in0=logs[:, I_TILES :], scalar1=-float(DC), scalar2=None, op0=ALU.mult)
-        nc.vector.scalar_tensor_tensor(
-            out=res_pad[:, 0:I_TILES], in0=logs[:, 0:I_TILES], scalar=coeff[:], in1=rest[:], op0=ALU.add, op1=ALU.add
-        )
-        res_ps = work.tile([P, P], F32, tag="work")
-        nc.tensor.transpose(res_ps[:], res_pad[:], ident[:])
-        res_rows = const.tile([P, P], F32)
-        nc.vector.tensor_copy(out=res_rows[:], in_=res_ps[:])
-        nc.sync.dma_start(out=out.rearrange("(t p) -> t p", p=P), in_=res_rows[0:I_TILES, :])
+            nc.sync.dma_start(out=out.rearrange("(t p) -> t p", p=P), in_=res_rows[0:I_TILES, :])

@@ -133,7 +133,7 @@ def tile_kernelloglikelihood_k_kernel(
             if n % PAIR == 0 and b == 0:
                 r_grouped[n // PAIR] = r_stage.tile([P, PAIR * UNIT_COLS], BF16, align_bytes=64, name="r_grouped")
             words = r_grouped[n // PAIR][:].bitcast(F32).rearrange("p (b a j u) -> p b a j u", b=2 * PAIR, a=2, u=2)
-            copy = nc.scalar.copy if n == len(UNITS) - 1 and b == 1 else nc.vector.tensor_copy
+            copy = nc.scalar.copy if b == 1 and (n >= 30) else nc.vector.tensor_copy
             copy(out=words[:, 2 * (n % PAIR) + b, :, :, :], in_=rt_ps[(n, b)][:].rearrange("p a u j -> p a j u"))
 
         def quantise_r(m, lo=0, hi=PAIR * BANK):
@@ -296,12 +296,11 @@ def tile_kernelloglikelihood_k_kernel(
                 nc.tensor.transpose(r2_ps[q][:, jt - t0, :], late["r2"][:, jt : jt + 1].to_broadcast([P, P]), ident[:])
 
         def halve_r2(q):
-            nc.vector.tensor_scalar(
+            nc.scalar.activation(
                 out=late["r2_half"][:, GROUPS[q][0] * P : GROUPS[q][1] * P],
-                in0=r2_ps[q][:].rearrange("p m j -> p (m j)"),
-                scalar1=-0.5,
-                scalar2=None,
-                op0=ALU.mult,
+                in_=r2_ps[q][:].rearrange("p m j -> p (m j)"),
+                func=ACT.Copy,
+                scale=-0.5,
             )
 
         def distances(q):
@@ -378,7 +377,7 @@ def tile_kernelloglikelihood_k_kernel(
                 transpose_z(g - 1)
             if 1 <= n <= n_units and n - 1 in GRAM_UNITS[UNITS[n - 1][0]]:
                 gram(n - 1)
-            limit = len(UNITS) if n >= n_units else 1 if n < FIRST[1] + 5 or n % 2 == 1 else 3
+            limit = len(UNITS) if n >= n_units else 1 if n < FIRST[1] + 5 else 2 if n % 2 == 0 or n > 24 else 1
             while product_todo and product_todo[0][0] <= n and limit > 0:
                 unit = product_todo[0][1]
                 products(unit)

@@ -133,7 +133,7 @@ def tile_kernelloglikelihood_k_kernel(
             if n % PAIR == 0 and b == 0:
                 r_grouped[n // PAIR] = r_stage.tile([P, PAIR * UNIT_COLS], BF16, align_bytes=64, name="r_grouped")
             words = r_grouped[n // PAIR][:].bitcast(F32).rearrange("p (b a j u) -> p b a j u", b=2 * PAIR, a=2, u=2)
-            copy = nc.scalar.copy if b == 1 and (n >= 30) else nc.vector.tensor_copy
+            copy = nc.scalar.copy if b == 1 and (n == 31) else nc.vector.tensor_copy
             copy(out=words[:, 2 * (n % PAIR) + b, :, :, :], in_=rt_ps[(n, b)][:].rearrange("p a u j -> p a j u"))
 
         def quantise_r(m, lo=0, hi=PAIR * BANK):
@@ -373,11 +373,9 @@ def tile_kernelloglikelihood_k_kernel(
             if n < n_units:
                 for b in range(2):
                     copy_r(n, b)
-            if 1 <= g <= PASSES:
-                transpose_z(g - 1)
             if 1 <= n <= n_units and n - 1 in GRAM_UNITS[UNITS[n - 1][0]]:
                 gram(n - 1)
-            limit = len(UNITS) if n >= n_units else 1 if n < FIRST[1] + 5 else 2 if n % 2 == 0 or n > 24 else 1
+            limit = len(UNITS) if n >= n_units else 1 if n < FIRST[1] + 7 or n % 2 else 2
             while product_todo and product_todo[0][0] <= n and limit > 0:
                 unit = product_todo[0][1]
                 products(unit)
@@ -390,6 +388,8 @@ def tile_kernelloglikelihood_k_kernel(
                             plan(max(n + 2, halved[q]) + 1, exponentials, q)
                         else:
                             plan(max(n + 1, halved[q]), distances, q)
+            if 1 <= g <= PASSES:
+                transpose_z(g - 1)
             if 0 <= g + 1 < PASSES:
                 project(g + 1)
             if n + 1 < n_units:

@@ -26,7 +26,7 @@ UNIT_COLS = 4 * BANK
 LOAD_AHEAD = 6
 PAIR = 2
 W_PLANES = 4
-R_BUFS = 6
+R_BUFS = 7
 W_BUFS = 6
 Q_BUFS = 6
 Z_LAG = 2
@@ -93,10 +93,15 @@ def tile_kernelloglikelihood_k_kernel(
         def load_reference(k):
             q, t0, nt, g0, np_ = UNITS[LOADS[k]]
             c0, width = load_cols(k)
-            r_sb[k] = r_rows.tile([P, nt, width], BF16, name="r_sb")
-            nc.sync.dma_start(
-                out=r_sb[k][:], in_=X_ref[t0 * P : (t0 + nt) * P, c0 : c0 + width].rearrange("(t p) c -> p t c", p=P)
-            )
+            halves = 2 if k == 0 else 1
+            for half in range(halves):
+                t1, count = t0 + half * nt // halves, nt // halves
+                rows = r_rows.tile([P, count, width], BF16, name="r_sb")
+                nc.sync.dma_start(
+                    out=rows[:], in_=X_ref[t1 * P : (t1 + count) * P, c0 : c0 + width].rearrange("(t p) c -> p t c", p=P)
+                )
+                for a in range(count):
+                    r_sb[(k, t1 - t0 + a)] = rows[:, a, :]
 
         def pieces(groups):
             result = []
@@ -114,7 +119,7 @@ def tile_kernelloglikelihood_k_kernel(
             entry = (g0 * K_PASS + lo) // K_PASS
             r_sq = unread.tile([P, SQUARE_COLS], BF16, name="r_sq")
             nc.scalar.activation(
-                out=r_sq[:, 0 : hi - lo], in_=r_sb[k][:, a, lo:hi], func=ACT.Square,
+                out=r_sq[:, 0 : hi - lo], in_=r_sb[(k, a)][:, lo:hi], func=ACT.Square,
                 accum_out=r2_parts[:, t0 + a, entry : entry + 1],
             )
 
@@ -124,7 +129,7 @@ def tile_kernelloglikelihood_k_kernel(
             rt_ps[(n, b)] = work.tile([P, 2, 2, P], F32, tag="work", name="rt_ps")
             for a in range(2):
                 g = g0 + (2 * b + a) // nt
-                words = r_sb[k][:, (2 * b + a) % nt, :].bitcast(F32)
+                words = r_sb[(k, (2 * b + a) % nt)].bitcast(F32)
                 for u in range(2):
                     w0 = (g * K_PASS - load_cols(k)[0]) // 2 + u * P
                     nc.tensor.transpose(rt_ps[(n, b)][:, a, u, :], words[:, w0 : w0 + P], ident[:])
@@ -375,7 +380,7 @@ def tile_kernelloglikelihood_k_kernel(
                     copy_r(n, b)
             if 1 <= n <= n_units and n - 1 in GRAM_UNITS[UNITS[n - 1][0]]:
                 gram(n - 1)
-            limit = len(UNITS) if n >= n_units else 1 if n < FIRST[1] + 7 or n % 2 else 2
+            limit = len(UNITS) if n >= n_units else 1 if n < FIRST[1] + 7 or n % 2 and n < 31 else 2
             while product_todo and product_todo[0][0] <= n and limit > 0:
                 unit = product_todo[0][1]
                 products(unit)
@@ -475,13 +480,17 @@ def tile_kernelloglikelihood_k_kernel(
             end = LAST[q] + 1 if q < len(GROUPS) - 1 else LAST[q]
             end = max(end, SQUARES_BEHIND - 1)
             if len(GRAM_UNITS[q]):
-                plan(GRAM_UNITS[q][-1] + 2, diagonal, q)
+                plan_early(GRAM_UNITS[q][-1] + 2, diagonal, q)
                 end = max(end, GRAM_UNITS[q][-1] + 2)
-            hurry = q == len(GROUPS) - 1
-            plan(end + 1 - hurry, sum_r2, q)
-            plan(end + 2 - hurry, spread_r2, q)
-            plan_early(end + 3 - hurry, halve_r2, q)
-            halved[q] = end + 3 - hurry
+            if q < len(GROUPS) - 1:
+                plan(end + 1, sum_r2, q)
+                plan(end + 2, spread_r2, q)
+                plan_early(end + 3, halve_r2, q)
+            else:
+                plan_early(end, sum_r2, q)
+                plan(end, spread_r2, q)
+                plan(end, halve_r2, q)
+            halved[q] = end + 3 if q < len(GROUPS) - 1 else end + 2
 
         with tc.manual_schedule():
             for b in range(2):

import math
from contextlib import ExitStack

import concourse.mybir as mybir
from concourse.masks import make_identity

F32 = mybir.dt.float32
BF16 = mybir.dt.bfloat16
I32 = mybir.dt.int32
U32 = mybir.dt.uint32
U8 = mybir.dt.uint8
FP8X4 = mybir.dt.float8_e4m3fn_x4
ALU = mybir.AluOpType
ACT = mybir.ActivationFunctionType
AX = mybir.AxisListType

P = 128
B, D, DC, NREF = 256, 512, 8192, 1024
K_PASS = 4 * P
BANK = 512
I_TILES = B // P
J_TILES = NREF // P
PASSES = DC // K_PASS
GROUPS = ((0, 4), (4, 6), (6, 7), (7, 8))
UNIT_COLS = 4 * BANK
LOAD_AHEAD = 6
PAIR = 2
W_PLANES = 4
R_BUFS = 7
W_BUFS = 6
Q_BUFS = 6
Z_LAG = 2
Z_PAIR = 2
EARLY_UNITS = 3
SQUARES_BEHIND = 19
SQUARE_COLS = 2048
GRAM_UNITS = (range(0, 16), range(18, 24), range(0), range(28, 30))
STEPS_BEHIND = 4

FLOPS = 2 * B * D * DC + 2 * B * DC * NREF

UNITS = [
    (q, t0, t1 - t0, g, 4 // (t1 - t0))
    for q, (t0, t1) in enumerate(GROUPS)
    for g in range(0, PASSES, 4 // (t1 - t0))
]
LOADS = [0, 1, 2, 3] + list(range(4, len(UNITS), 2))
LAST = [max(n for n, unit in enumerate(UNITS) if unit[0] == q) for q in range(len(GROUPS))]
FIRST = [min(n for n, unit in enumerate(UNITS) if unit[0] == q) for q in range(len(GROUPS))]

SQRT_2PI_HI = 41069.0 / 16384.0
COEFF_REST = -math.log(NREF) - DC * math.log(math.sqrt(2.0 * math.pi) / SQRT_2PI_HI)


def tile_kernelloglikelihood_k_kernel(
    tc, x, pca_weight_words, pca_weight_scales, pca_bias, X_ref, bandwidth, out
):
    nc = tc.nc
    with ExitStack() as stack:
        const = stack.enter_context(tc.tile_pool(name="const", bufs=1))
        r_rows = stack.enter_context(tc.tile_pool(name="r_rows", bufs=R_BUFS))
        r_stage = stack.enter_context(tc.tile_pool(name="r_stage", bufs=3))
        r_quant = stack.enter_context(tc.tile_pool(name="r_quant", bufs=Q_BUFS))
        w_pool = stack.enter_context(tc.tile_pool(name="w_pool", bufs=W_BUFS))
        b_pool = stack.enter_context(tc.tile_pool(name="b_pool", bufs=4))
        z_stage = stack.enter_context(tc.tile_pool(name="z_stage", bufs=8))
        z_group = stack.enter_context(tc.tile_pool(name="z_group", bufs=2))
        unread = stack.enter_context(tc.tile_pool(name="unread", bufs=4))
        work = stack.enter_context(tc.psum_pool(name="work", bufs=3))
        acc = stack.enter_context(tc.psum_pool(name="acc", bufs=1))

        ident = const.tile([P, P], F32)
        z_codes = const.tile([P, PASSES, B], U32, align_bytes=64)
        z_scales = const.tile([P, PASSES, B], U8, align_bytes=64)
        z2_parts = const.tile([P, I_TILES, PASSES], F32)
        r2_parts = const.tile([P, J_TILES, 1 + PASSES], F32)

        r_sb = {}
        rt_ps = {}
        r_grouped = {}
        r_codes = {}
        r_scales = {}
        cross = {}
        gram_ps = {}

        def load_of(n):
            return max(k for k in range(len(LOADS)) if LOADS[k] <= n)

        def load_cols(k):
            units = (LOADS + [len(UNITS)])[k + 1] - LOADS[k]
            return UNITS[LOADS[k]][3] * K_PASS, units * UNITS[LOADS[k]][4] * K_PASS

        def load_reference(k):
            q, t0, nt, g0, np_ = UNITS[LOADS[k]]
            c0, width = load_cols(k)
            halves = 2 if k == 0 else 1
            for half in range(halves):
                t1, count = t0 + half * nt // halves, nt // halves
                rows = r_rows.tile([P, count, width], BF16, name="r_sb")
                nc.sync.dma_start(
                    out=rows[:], in_=X_ref[t1 * P : (t1 + count) * P, c0 : c0 + width].rearrange("(t p) c -> p t c", p=P)
                )
                for a in range(count):
                    r_sb[(k, t1 - t0 + a)] = rows[:, a, :]

        def pieces(groups):
            result = []
            for k, n in enumerate(LOADS):
                q, t0, nt, g0, np_ = UNITS[n]
                width = min(SQUARE_COLS, load_cols(k)[1])
                for part in range(load_cols(k)[1] // width):
                    for a in range(nt):
                        if q in groups and (a > 0 or n + part * width // (np_ * K_PASS) not in GRAM_UNITS[q]):
                            result.append((k, a, part * width, (part + 1) * width))
            return result

        def square_r(k, a, lo, hi):
            q, t0, nt, g0, np_ = UNITS[LOADS[k]]
            entry = (g0 * K_PASS + lo) // K_PASS
            r_sq = unread.tile([P, SQUARE_COLS], BF16, name="r_sq")
            nc.scalar.activation(
                out=r_sq[:, 0 : hi - lo], in_=r_sb[(k, a)][:, lo:hi], func=ACT.Square,
                accum_out=r2_parts[:, t0 + a, entry : entry + 1],
            )

        def transpose_r(n, b):
            q, t0, nt, g0, np_ = UNITS[n]
            k = load_of(n)
            rt_ps[(n, b)] = work.tile([P, 2, 2, P], F32, tag="work", name="rt_ps")
            for a in range(2):
                g = g0 + (2 * b + a) // nt
                words = r_sb[(k, (2 * b + a) % nt)].bitcast(F32)
                for u in range(2):
                    w0 = (g * K_PASS - load_cols(k)[0]) // 2 + u * P
                    nc.tensor.transpose(rt_ps[(n, b)][:, a, u, :], words[:, w0 : w0 + P], ident[:])

        def copy_r(n, b):
            if n % PAIR == 0 and b == 0:
                r_grouped[n // PAIR] = r_stage.tile([P, PAIR * UNIT_COLS], BF16, align_bytes=64, name="r_grouped")
            words = r_grouped[n // PAIR][:].bitcast(F32).rearrange("p (b a j u) -> p b a j u", b=2 * PAIR, a=2, u=2)
            copy = nc.scalar.copy if b == 1 and (n == 31) else nc.vector.tensor_copy
            copy(out=words[:, 2 * (n % PAIR) + b, :, :, :], in_=rt_ps[(n, b)][:].rearrange("p a u j -> p a j u"))

        def quantise_r(m, lo=0, hi=PAIR * BANK):
            if lo == 0:
                r_codes[m] = r_quant.tile([P, PAIR * BANK], U32, align_bytes=64, name="r_codes")
                r_scales[m] = r_quant.tile([P, PAIR * BANK], U8, align_bytes=64, name="r_scales")
            nc.vector.quantize_mx(
                out=r_codes[m][:, lo:hi].bitcast(FP8X4), scales=r_scales[m][:, lo:hi], in_=r_grouped[m][:, 4 * lo : 4 * hi]
            )

        def products(n):
            q, t0, nt, g0, np_ = UNITS[n]
            for b in range(np_):
                first = (n % PAIR) * BANK + b * nt * P
                cols = slice(first, first + nt * P)
                for it in range(I_TILES):
                    if (it, q) not in cross:
                        cross[(it, q)] = acc.tile([P, BANK], F32, tag="acc_%d" % (it + I_TILES * (q % 2)), name="cross")
                    nc.tensor.matmul_mx(
                        out=cross[(it, q)][:, 0 : nt * P],
                        lhsT=z_codes[:, g0 + b, it * P : (it + 1) * P].bitcast(FP8X4),
                        lhsT_scale=z_scales[:, g0 + b, it * P : (it + 1) * P],
                        rhs=r_codes[n // PAIR][:, cols].bitcast(FP8X4),
                        rhs_scale=r_scales[n // PAIR][:, cols],
                        start=(g0 + b == 0),
                        stop=(g0 + b == PASSES - 1),
                    )

        def gram(n):
            q, t0, nt, g0, np_ = UNITS[n]
            if q not in gram_ps:
                gram_ps[q] = acc.tile([P, P], F32, tag="gram", name="gram_ps")
            columns = r_grouped[n // PAIR][:].rearrange("p (j t) -> p j t", t=4)
            for b in range(np_):
                for t in range(4):
                    first = (n % PAIR) * BANK + b * nt * P
                    plane = columns[:, first : first + P, t]
                    nc.tensor.matmul(
                        out=gram_ps[q][:],
                        lhsT=plane,
                        rhs=plane,
                        start=(n == GRAM_UNITS[q][0] and b == 0 and t == 0),
                        stop=(n == GRAM_UNITS[q][-1] and b == np_ - 1 and t == 3),
                    )

        def diagonal(q):
            off_diagonal = unread.tile([P, P], F32, tag="by_vector")
            nc.vector.scalar_tensor_tensor(
                out=off_diagonal[:], in0=gram_ps[q][:], scalar=1.0, in1=ident[:], op0=ALU.mult, op1=ALU.mult,
                accum_out=r2_parts[:, GROUPS[q][0], PASSES:],
            )

        early = {}
        w_words = {}
        bias = {}
        y_ps = {}
        z_f32 = {}
        z_bf = {}
        zt_ps = {}
        z_grouped = {}

        def load_w(g):
            w_words[g] = w_pool.tile([P, K_PASS], U32, align_bytes=64, name="w_words")
            w_bytes = pca_weight_words[0].rearrange("p n t -> p (n t)")
            nc.sync.dma_start(out=w_words[g][:].bitcast(I32), in_=w_bytes[:, 4 * g * K_PASS : 4 * (g + 1) * K_PASS].bitcast(I32))
            if g % Z_PAIR == 0:
                bias[g // Z_PAIR] = b_pool.tile([P, Z_PAIR * K_PASS], BF16, name="bias")
                nc.sync.dma_start(
                    out=bias[g // Z_PAIR][:], in_=pca_bias[g * K_PASS : (g + Z_PAIR) * K_PASS].partition_broadcast(P)
                )

        def transpose_x():
            x_words = early["x_sb"][:].bitcast(F32)
            early["xt_ps"] = work.tile([P, I_TILES, 2, P], F32, tag="work", name="xt_ps")
            for it in range(I_TILES):
                for u in range(2):
                    nc.tensor.transpose(early["xt_ps"][:, it, u, :], x_words[:, it, u : D // 2 : 2], ident[:])

        def copy_x():
            nc.vector.tensor_copy(
                out=early["x_grouped"][:].bitcast(F32).rearrange("p (a i u) -> p a i u", a=I_TILES, u=2),
                in_=early["xt_ps"][:].rearrange("p a u i -> p a i u"),
            )

        def quantise_x():
            nc.vector.quantize_mx(out=early["x_codes"][:].bitcast(FP8X4), scales=early["x_scales"][:], in_=early["x_grouped"][:])

        def project(g):
            plane, col0 = (g * K_PASS) // (DC // W_PLANES), (g * K_PASS) % (DC // W_PLANES)
            for it in range(I_TILES):
                y_ps[(g, it)] = acc.tile([P, K_PASS], F32, tag="acc_%d" % (I_TILES + it), name="y_ps")
                nc.tensor.matmul_mx(
                    out=y_ps[(g, it)][:],
                    lhsT=early["x_codes"][:, it * P : (it + 1) * P].bitcast(FP8X4),
                    lhsT_scale=early["x_scales"][:, it * P : (it + 1) * P],
                    rhs=w_words[g][:].bitcast(FP8X4),
                    rhs_scale=early["w_planes"][4 * plane : P, col0 : col0 + K_PASS],
                    start=True,
                    stop=True,
                )

        def add_bias(g):
            bias_cols = bias[g // Z_PAIR][:, (g % Z_PAIR) * K_PASS : (g % Z_PAIR + 1) * K_PASS]
            for it in range(I_TILES):
                z_f32[(g, it)] = z_stage.tile([P, K_PASS], F32, name="z_f32")
                nc.vector.tensor_tensor(out=z_f32[(g, it)][:], in0=y_ps[(g, it)][:], in1=bias_cols, op=ALU.add)

        def round_z(g):
            for it in range(I_TILES):
                z_bf[(g, it)] = z_stage.tile([P, K_PASS], BF16, name="z_bf")
                nc.gpsimd.tensor_scalar(
                    out=z_bf[(g, it)][:], in0=z_f32[(g, it)][:], scalar1=1.0, scalar2=0.0, op0=ALU.mult, op1=ALU.add
                )

        def square_z(g):
            for it in range(I_TILES):
                z_sq = unread.tile([P, BANK], BF16, bufs=10, tag="z_sq")
                nc.scalar.activation(
                    out=z_sq[:], in_=z_f32[(g, it)][:], func=ACT.Square, accum_out=z2_parts[:, it, g : g + 1]
                )

        def transpose_z(g):
            zt_ps[g] = work.tile([P, I_TILES, 2, P], F32, tag="work", name="zt_ps")
            for it in range(I_TILES):
                z_words = z_bf[(g, it)][:].bitcast(F32)
                for u in range(2):
                    nc.tensor.transpose(zt_ps[g][:, it, u, :], z_words[:, u * P : (u + 1) * P], ident[:])

        def copy_z(g):
            if g % Z_PAIR == 0:
                z_grouped[g // Z_PAIR] = z_group.tile([P, Z_PAIR * B * 4], BF16, align_bytes=64, name="z_grouped")
            words = z_grouped[g // Z_PAIR][:].bitcast(F32).rearrange("p (g a i u) -> p g a i u", g=Z_PAIR, a=I_TILES, u=2)
            nc.scalar.copy(out=words[:, g % Z_PAIR, :, :, :], in_=zt_ps[g][:].rearrange("p a u i -> p a i u"))

        def quantise_z(pair):
            passes = slice(pair * Z_PAIR, (pair + 1) * Z_PAIR)
            nc.vector.quantize_mx(
                out=z_codes[:, passes, :].rearrange("p g i -> p (g i)").bitcast(FP8X4),
                scales=z_scales[:, passes, :].rearrange("p g i -> p (g i)"),
                in_=z_grouped[pair][:],
            )

        late = {}
        r2_ps = {}

        def sum_z2():
            nc.vector.tensor_reduce(out=late["z2"][:], in_=z2_parts[:], axis=AX.X, op=ALU.add)

        def halve_z2():
            nc.vector.tensor_scalar(out=late["z2_half"][:], in0=late["z2"][:], scalar1=-0.5, scalar2=None, op0=ALU.mult)

        def sum_r2(q):
            t0, t1 = GROUPS[q]
            nc.vector.tensor_reduce(out=late["r2"][:, t0:t1], in_=r2_parts[:, t0:t1, :], axis=AX.X, op=ALU.add)

        def spread_r2(q):
            t0, t1 = GROUPS[q]
            r2_ps[q] = work.tile([P, t1 - t0, P], F32, tag="work", name="r2_ps")
            for jt in range(t0, t1):
                nc.tensor.transpose(r2_ps[q][:, jt - t0, :], late["r2"][:, jt : jt + 1].to_broadcast([P, P]), ident[:])

        def halve_r2(q):
            nc.scalar.activation(
                out=late["r2_half"][:, GROUPS[q][0] * P : GROUPS[q][1] * P],
                in_=r2_ps[q][:].rearrange("p m j -> p (m j)"),
                func=ACT.Copy,
                scale=-0.5,
            )

        def distances(q):
            cols = slice(GROUPS[q][0] * P, GROUPS[q][1] * P)
            w = late["w"]
            for it in range(I_TILES):
                nc.vector.scalar_tensor_tensor(
                    out=w[it][:, cols],
                    in0=cross[(it, q)][:, 0 : (GROUPS[q][1] - GROUPS[q][0]) * P],
                    scalar=late["z2_half"][:, it : it + 1],
                    in1=late["r2_half"][:, cols],
                    op0=ALU.add,
                    op1=ALU.add,
                )
            for it in range(I_TILES):
                nc.vector.tensor_scalar(
                    out=w[it][:, cols], in0=w[it][:, cols], scalar1=0.0, scalar2=None, op0=ALU.min, op1=ALU.max,
                    accum_out=late["w_max"][:, it, q : q + 1],
                )
            if q < len(GROUPS) - 1:
                nc.vector.tensor_scalar(
                    out=late["neg_l_max"][:, :, q], in0=late["w_max"][:, :, q], scalar1=late["inv_h2"][:],
                    scalar2=-1.0, op0=ALU.mult, op1=ALU.mult,
                )

        def exponentials(q):
            cols = slice(GROUPS[q][0] * P, GROUPS[q][1] * P)
            w = late["w"]
            for it in range(I_TILES):
                e_w = unread.tile([P, BANK], BF16, bufs=10, tag="z_sq")
                nc.scalar.activation(
                    out=e_w[:, 0 : (GROUPS[q][1] - GROUPS[q][0]) * P],
                    in_=w[it][:, cols],
                    func=ACT.Exp,
                    scale=late["inv_h2"][:],
                    bias=late["neg_l_max"][:, it, q : q + 1],
                    accum_out=late["sums"][:, it, q : q + 1],
                )

        n_units = len(UNITS)
        product_todo = []
        early_agenda = {}
        agenda = {}
        halved = {}

        def plan(step_, function, *args):
            agenda.setdefault(step_, []).append((function, args))

        def plan_early(step_, function, *args):
            early_agenda.setdefault(step_, []).append((function, args))

        squares = {}
        first_pieces, other_pieces = pieces([0]), pieces(range(1, len(GROUPS)))
        early_count = EARLY_UNITS * (UNITS[0][2] - 1)
        for i, piece in enumerate(first_pieces[:early_count]):
            squares.setdefault(i // (UNITS[0][2] - 1), []).append(piece)
        for i, piece in enumerate(first_pieces[early_count:]):
            spread = (SQUARES_BEHIND - EARLY_UNITS) / len(first_pieces[early_count:])
            squares.setdefault(max(EARLY_UNITS + int(i * spread), LOADS[piece[0]]), []).append(piece)
        for i, piece in enumerate(other_pieces):
            squares.setdefault(SQUARES_BEHIND + i * (n_units - 2 - SQUARES_BEHIND) // len(other_pieces), []).append(piece)

        def step(n):
            g = n - Z_LAG
            if 0 <= g < PASSES:
                add_bias(g)
                round_z(g)
            for entry in early_agenda.get(n, []):
                entry[0](*entry[1])
            if n < n_units:
                for b in range(2):
                    copy_r(n, b)
            if 1 <= n <= n_units and n - 1 in GRAM_UNITS[UNITS[n - 1][0]]:
                gram(n - 1)
            limit = len(UNITS) if n >= n_units else 1 if n < FIRST[1] + 7 or n % 2 and n < 31 else 2
            while product_todo and product_todo[0][0] <= n and limit > 0:
                unit = product_todo[0][1]
                products(unit)
                product_todo.remove(product_todo[0])
                limit -= 1
                for q in range(len(GROUPS)):
                    if unit == LAST[q]:
                        if q < len(GROUPS) - 1:
                            plan(max(n + 2, halved[q]), distances, q)
                            plan(max(n + 2, halved[q]) + 1, exponentials, q)
                        else:
                            plan(max(n + 1, halved[q]), distances, q)
            if 1 <= g <= PASSES:
                transpose_z(g - 1)
            if 0 <= g + 1 < PASSES:
                project(g + 1)
            if n + 1 < n_units:
                for b in range(2):
                    transpose_r(n + 1, b)
            if 1 <= g <= PASSES:
                square_z(g - 1)
                copy_z(g - 1)
            for piece in squares.get(n, []):
                square_r(*piece)
            if n == 0:
                copy_x()
                quantise_x()
            if n % PAIR == 0 and PAIR <= n < n_units:
                quantise_r(n // PAIR - 1)
            if n == n_units - 1:
                for lo, hi in ((0, BANK), (BANK, BANK + BANK // 2), (BANK + BANK // 2, 2 * BANK)):
                    quantise_r(n // PAIR, lo, hi)
            if g >= Z_PAIR + 1 and (g - 1) % Z_PAIR == 0 and (g - 1) // Z_PAIR <= PASSES // Z_PAIR:
                quantise_z((g - 1) // Z_PAIR - 1)
            for entry in agenda.get(n, []):
                entry[0](*entry[1])
            if 0 <= g and g + W_BUFS < PASSES:
                load_w(g + W_BUFS)
            if g >= 0 and n + LOAD_AHEAD in LOADS:
                load_reference(load_of(n + LOAD_AHEAD))

        h_bf = const.tile([P, 1], BF16)
        nc.sync.dma_start(out=h_bf[:], in_=bandwidth.partition_broadcast(P))
        load_reference(0)
        early["x_sb"] = const.tile([P, I_TILES, D], BF16, name="x_sb")
        nc.sync.dma_start(out=early["x_sb"][:], in_=x.rearrange("(t p) k -> p t k", p=P))
        load_reference(1)
        early["w_planes"] = const.tile([P, DC // W_PLANES], U8, align_bytes=64, name="w_planes")
        nc.vector.memset(early["w_planes"][:].bitcast(I32), 0)
        for quad in range(4):
            nc.sync.dma_start(
                out=early["w_planes"][32 * quad : 32 * quad + 4 * W_PLANES, :].bitcast(I32),
                in_=pca_weight_scales[0][4 * quad : 4 * quad + 4, :].rearrange("r (n c) -> n r c", n=W_PLANES).bitcast(I32),
            )
        load_w(0)
        load_reference(2)
        load_w(1)
        load_reference(3)
        load_w(2)
        for k in range(4, 6):
            load_reference(k)
            for g in range(LOADS[k] - 1, min(LOADS[k] + 1, W_BUFS)):
                load_w(g)
        early["x_grouped"] = const.tile([P, B * 4], BF16, align_bytes=64, name="x_grouped")
        early["x_codes"] = const.tile([P, B], U32, align_bytes=64, name="x_codes")
        early["x_scales"] = const.tile([P, B], U8, align_bytes=64, name="x_scales")

        make_identity(nc, ident[:])
        pads = const.tile([P, 2, P], F32)
        nc.vector.memset(pads[:], 0.0)
        nc.vector.memset(r2_parts[:], 0.0)
        h32 = const.tile([P, 1], F32)
        nc.vector.tensor_copy(out=h32[:], in_=h_bf[:])
        h_sq = const.tile([P, 1], F32)
        nc.vector.tensor_tensor(out=h_sq[:], in0=h32[:], in1=h32[:], op=ALU.mult)
        inv_h2 = const.tile([P, 1], F32)
        nc.vector.reciprocal(out=inv_h2[:], in_=h_sq[:])
        late["inv_h2"] = inv_h2
        late["z2"] = const.tile([P, I_TILES], F32, name="z2")
        late["z2_half"] = const.tile([P, I_TILES], F32, name="z2_half")
        late["r2"] = const.tile([P, J_TILES], F32, name="r2")
        late["r2_half"] = const.tile([P, NREF], F32, name="r2_half")
        late["w"] = [const.tile([P, NREF], F32, name="w_%d" % it) for it in range(I_TILES)]
        late["w_max"] = const.tile([P, I_TILES, len(GROUPS)], F32, name="w_max")
        late["neg_l_max"] = const.tile([P, I_TILES, len(GROUPS)], F32, name="neg_l_max")
        late["sums"] = const.tile([P, I_TILES, len(GROUPS)], F32, name="sums")

        for n, unit in enumerate(UNITS):
            ready = (n // PAIR + 1) * PAIR + 1 if n < n_units - PAIR else n_units
            if unit[0] == 0:
                ready = max(ready, (unit[3] // Z_PAIR * Z_PAIR + Z_PAIR - 1) + Z_LAG + 3)
            product_todo.append((ready, n))
        z_end = Z_LAG + PASSES
        plan(z_end + 1, sum_z2)
        plan(z_end + 2, halve_z2)
        for q in range(len(GROUPS)):
            end = LAST[q] + 1 if q < len(GROUPS) - 1 else LAST[q]
            end = max(end, SQUARES_BEHIND - 1)
            if len(GRAM_UNITS[q]):
                plan_early(GRAM_UNITS[q][-1] + 2, diagonal, q)
                end = max(end, GRAM_UNITS[q][-1] + 2)
            if q < len(GROUPS) - 1:
                plan(end + 1, sum_r2, q)
                plan(end + 2, spread_r2, q)
                plan_early(end + 3, halve_r2, q)
            else:
                plan_early(end, sum_r2, q)
                plan(end, spread_r2, q)
                plan(end, halve_r2, q)
            halved[q] = end + 3 if q < len(GROUPS) - 1 else end + 2

        with tc.manual_schedule():
            for b in range(2):
                transpose_r(0, b)
            transpose_x()
            for n in range(n_units + STEPS_BEHIND):
                step(n)
            assert not product_todo and max(agenda) < n_units + STEPS_BEHIND

            last = len(GROUPS) - 1
            top = const.tile([P, I_TILES], F32)
            nc.vector.tensor_reduce(out=top[:], in_=late["w_max"][:], axis=AX.X, op=ALU.max)
            neg_l_top = pads[:, 1, 0:I_TILES]
            nc.vector.tensor_scalar(out=neg_l_top, in0=top[:], scalar1=inv_h2[:], scalar2=-1.0, op0=ALU.mult, op1=ALU.mult)
            factor = const.tile([P, I_TILES, last], F32)
            for it in range(I_TILES):
                nc.scalar.activation(
                    out=factor[:, it, :], in_=late["w_max"][:, it, 0:last], func=ACT.Exp, scale=inv_h2[:],
                    bias=pads[:, 1, it : it + 1],
                )
            weighted = const.tile([P, I_TILES, len(GROUPS)], F32)
            nc.vector.tensor_tensor(out=weighted[:, :, 0:last], in0=late["sums"][:, :, 0:last], in1=factor[:], op=ALU.mult)
            for it in range(I_TILES):
                e_w = unread.tile([P, BANK], BF16, bufs=10, tag="z_sq")
                nc.scalar.activation(
                    out=e_w[:, 0 : (GROUPS[last][1] - GROUPS[last][0]) * P],
                    in_=late["w"][it][:, GROUPS[last][0] * P : GROUPS[last][1] * P],
                    func=ACT.Exp,
                    scale=inv_h2[:],
                    bias=pads[:, 1, it : it + 1],
                    accum_out=weighted[:, it, last : last + 1],
                )
            ln_h = const.tile([P, 1], F32)
            nc.scalar.activation(out=ln_h[:], in_=h32[:], func=ACT.Ln, scale=SQRT_2PI_HI)
            coeff = const.tile([P, 1], F32)
            nc.vector.tensor_reduce(out=pads[:, 0, 0:I_TILES], in_=weighted[:], axis=AX.X, op=ALU.add)
            nc.vector.tensor_scalar(
                out=coeff[:], in0=ln_h[:], scalar1=-float(DC), scalar2=COEFF_REST, op0=ALU.mult, op1=ALU.add
            )
            rows_ps = work.tile([P, 2, P], F32, tag="work")
            for i in (1, 0):
                nc.tensor.transpose(rows_ps[:, i, :], pads[:, i, :], ident[:])
            ln_sum = const.tile([P, P], F32)
            nc.scalar.activation(out=ln_sum[0:I_TILES, :], in_=rows_ps[0:I_TILES, 0, :], func=ACT.Ln)
            res_rows = const.tile([P, P], F32)
            nc.vector.scalar_tensor_tensor(
                out=res_rows[0:I_TILES, :], in0=ln_sum[0:I_TILES, :], scalar=coeff[0:I_TILES, :],
                in1=rows_ps[0:I_TILES, 1, :], op0=ALU.add, op1=ALU.subtract,
            )
            nc.sync.dma_start(out=out.rearrange("(t p) -> t p", p=P), in_=res_rows[0:I_TILES, :])
